import numpy as np
import ml_dtypes


def mxq(x, axis, fmt="e4m3"):
    dtype, down = {"e4m3": (ml_dtypes.float8_e4m3fn, 7), "e5m2": (ml_dtypes.float8_e5m2, 14)}[fmt]
    v = np.moveaxis(np.asarray(x, np.float32).astype(ml_dtypes.bfloat16).astype(np.float64), axis, -1)
    blocks = v.reshape(v.shape[:-1] + (-1, 32))
    amax = np.abs(blocks).max(-1, keepdims=True)
    byte = np.maximum(np.where(amax > 0, np.frexp(amax)[1] - 1 + 127, 0) - down, 1)
    scale = np.exp2(byte - 127.0)
    codes = (blocks / scale).astype(np.float32).astype(dtype).astype(np.float64)
    return np.moveaxis((codes * scale).reshape(v.shape), -1, axis)


WIDE = False


def mx_kscale(k):
    if not WIDE:
        return np.ones(k)
    levels = np.array([10, -10, 5, -5, 0])
    a = np.random.permutation(np.resize(levels, k // 512 * 4)).reshape(k // 512, 4)
    idx = np.arange(k)
    return np.exp2(a[idx // 512, idx % 128 // 32])


BF16 = ml_dtypes.bfloat16


def bf(x):
    return np.asarray(x, np.float32).astype(BF16)


def f64(x):
    return np.asarray(x).astype(np.float64)


B, I, J, P, D = 32, 512, 512, 32, 4
EPS = 1e-5


def stdz(t):
    m = t.mean(axis=(-1, -2), keepdims=True)
    s = t.std(axis=(-1, -2), keepdims=True, ddof=1)
    return (t - m) / (s + EPS)


def flat_softmax(t):
    e = np.exp(t - t.max(axis=(-1, -2), keepdims=True))
    return e / e.sum(axis=(-1, -2), keepdims=True)


def setup_inputs():
    s = mx_kscale(I)
    return {"x": bf((np.random.standard_normal((B, I, J)) + 0.25) * s[:, None]),
            "o_xi": bf((np.random.standard_normal((D, I, P)) * 2.0 / np.sqrt(I + P) + 2.0 / I) / s[:, None]),
            "p_xi": bf(np.random.standard_normal((D, J, P)) * 2.0 / np.sqrt(J + P)),
            "rel_o_xi": bf(np.random.standard_normal((D, I, P)) * 2.0 / np.sqrt(I + P) / s[:, None])}


def reference(x, o_xi, p_xi, rel_o_xi):
    xq = mxq(f64(x), 1, "e4m3").transpose(0, 2, 1)[:, None]
    mass = flat_softmax(xq @ mxq(f64(rel_o_xi), 1, "e4m3")).sum(-2)
    t = stdz(np.tanh(xq @ mxq(f64(o_xi), 1, "e4m3")))
    u = mxq(f64(p_xi), 1, "e4m3").transpose(0, 2, 1) @ mxq(t, 2, "e4m3")
    return stdz(np.tanh(u)), mass

@@ -1,0 +1,450 @@
+from contextlib import ExitStack
+
+import concourse.mybir as mybir
+from concourse.masks import make_identity
+
+F32 = mybir.dt.float32
+BF16 = mybir.dt.bfloat16
+U32 = mybir.dt.uint32
+U8 = mybir.dt.uint8
+FP8X4 = mybir.dt.float8_e4m3fn_x4
+ACT = mybir.ActivationFunctionType
+ALU = mybir.AluOpType
+AX = mybir.AxisListType
+
+P = 128
+NB = 32
+NI = 512
+NJ = 512
+NW = 32
+ND = 4
+EPS = 1e-5
+N1 = NJ * NW
+N2 = NW * NW
+S_COLS = 128
+LATE = 8
+
+FLOPS = 2 * NB * ND * (2 * NI * NJ * NW + NW * NJ * NW)
+
+
+def tile_selfprojectiondev_pb_t_kernel(tc, x, o_xi, p_xi, rel_o_xi, out_0, out_1):
+    nc = tc.nc
+    with ExitStack() as ctx:
+        const = ctx.enter_context(tc.tile_pool(name="const", bufs=1))
+        rawp = ctx.enter_context(tc.tile_pool(name="rawp", bufs=14))
+        grp = ctx.enter_context(tc.tile_pool(name="grp", bufs=3))
+        xq = ctx.enter_context(tc.tile_pool(name="xq", bufs=3))
+        xl = ctx.enter_context(tc.tile_pool(name="xl", bufs=LATE))
+        tp = ctx.enter_context(tc.tile_pool(name="tp", bufs=8))
+        junk = ctx.enter_context(tc.tile_pool(name="junk", bufs=2))
+        small = ctx.enter_context(tc.tile_pool(name="small", bufs=4))
+        tq = ctx.enter_context(tc.tile_pool(name="tq", bufs=2))
+        fin = ctx.enter_context(tc.tile_pool(name="fin", bufs=2))
+        pz = ctx.enter_context(tc.psum_pool(name="pz", bufs=2))
+        pr = ctx.enter_context(tc.psum_pool(name="pr", bufs=2))
+        pm = ctx.enter_context(tc.psum_pool(name="pm", bufs=1))
+        pu = ctx.enter_context(tc.psum_pool(name="pu", bufs=1))
+        pm2 = ctx.enter_context(tc.psum_pool(name="pm2", bufs=1))
+        ptr = ctx.enter_context(tc.psum_pool(name="ptr", bufs=1))
+        ctx.enter_context(tc.manual_schedule())
+
+        raw_w = const.tile([P, 2, ND, 4, NW], BF16)
+        nc.scalar.dma_start(
+            out=raw_w[:, 0].rearrange("p d t c -> p d (t c)"),
+            in_=o_xi.rearrange("d (p t) c -> p d (t c)", t=4),
+        )
+        nc.scalar.dma_start(
+            out=raw_w[:, 1].rearrange("p d t c -> p d (t c)"),
+            in_=rel_o_xi.rearrange("d (p t) c -> p d (t c)", t=4),
+        )
+        raw_p = const.tile([P, ND, 4, NW], BF16)
+        for d in range(ND):
+            nc.scalar.dma_start(out=raw_p[:, d], in_=p_xi[d].rearrange("(t p) q -> p t q", p=P))
+
+        raws = []
+        for g in range(NB // 2):
+            raw = rawp.tile([P, 2, 4, NJ], BF16, name="raw")
+            if g == 0:
+                for bb in range(2):
+                    nc.sync.dma_start(
+                        out=raw[:, bb].rearrange("p t j -> p (t j)"),
+                        in_=x[bb].rearrange("(p t) j -> p (t j)", t=4),
+                    )
+            else:
+                nc.sync.dma_start(
+                    out=raw[:].rearrange("p b t j -> p b (t j)"),
+                    in_=x[2 * g : 2 * g + 2].rearrange("b (p t) j -> p b (t j)", t=4),
+                )
+            raws.append(raw)
+
+        ones1 = const.tile([P, P], F32)
+        nc.gpsimd.memset(ones1[:], 1.0 / N1)
+        blk2 = const.tile([P, P], F32)
+        nc.gpsimd.memset(blk2[:], 0.0)
+        for d in range(ND):
+            nc.gpsimd.memset(blk2[NW * d : NW * (d + 1), NW * d : NW * (d + 1)], 1.0 / N2)
+        half = const.tile([P, 8], F32)
+        nc.gpsimd.memset(half[:], 0.5)
+        ident = const.tile([P, P], F32)
+        make_identity(nc, ident[:])
+        nm = const.tile([P, P], F32)
+        nc.gpsimd.memset(nm[:], 0.0)
+        se = const.tile([P, P], F32)
+        nc.gpsimd.memset(se[:], 0.0)
+        u_all = const.tile([P, NB, NW], F32)
+
+        gw = const.tile([P, 2, ND * NW, 4], BF16, align_bytes=64)
+        for s in range(2):
+            nc.vector.tensor_copy(
+                out=gw[:, s].rearrange("p (d c) t -> p d c t", d=ND),
+                in_=raw_w[:, s].rearrange("p d t c -> p d c t"),
+            )
+        gp = const.tile([P, ND * NW, 4], BF16, align_bytes=64)
+        w_codes = const.tile([P, 2 * P], U32, align_bytes=64)
+        w_plane = const.tile([P, 2 * P], U8, align_bytes=64)
+        nc.vector.quantize_mx(
+            out=w_codes[:].bitcast(FP8X4),
+            scales=w_plane[:],
+            in_=gw[:].rearrange("p s w t -> p (s w t)"),
+        )
+        p_codes = const.tile([P, P], U32, align_bytes=64)
+        p_plane = const.tile([P, P], U8, align_bytes=64)
+
+        def prep_p_copy():
+            nc.vector.tensor_copy(
+                out=gp[:].rearrange("p (d c) t -> p d c t", d=ND),
+                in_=raw_p[:].rearrange("p d t c -> p d c t"),
+            )
+
+        def prep_p_quant():
+            nc.vector.quantize_mx(
+                out=p_codes[:].bitcast(FP8X4),
+                scales=p_plane[:],
+                in_=gp[:].rearrange("p w t -> p (w t)"),
+            )
+
+        state = {}
+
+        def regroup_s(b):
+            grouped = grp.tile([P, NJ, 4], BF16, align_bytes=64, name="grouped")
+            state[("grouped", b)] = grouped
+            src = raws[b // 2][:, b % 2]
+            jv = NJ - S_COLS
+            nc.scalar.copy(
+                out=grouped[:, jv:NJ, :].rearrange("p (c i) t -> p c t i", i=4),
+                in_=src[:, :, jv:NJ].rearrange("p t (c i) -> p c t i", i=4),
+            )
+
+        def regroup_v(b):
+            grouped = state[("grouped", b)]
+            src = raws[b // 2][:, b % 2]
+            jv = NJ - S_COLS
+            nc.vector.tensor_copy(
+                out=grouped[:, 0:jv, :].rearrange("p (c i) t -> p c t i", i=4),
+                in_=src[:, :, 0:jv].rearrange("p t (c i) -> p c t i", i=4),
+            )
+
+        def quant_x(b):
+            grouped = state[("grouped", b)]
+            pool = xl if b >= NB - LATE else xq
+            codes = pool.tile([P, NJ], U32, align_bytes=64, name="codes")
+            plane = pool.tile([P, NJ], U8, align_bytes=64, name="plane")
+            nc.vector.quantize_mx(
+                out=codes[:].bitcast(FP8X4),
+                scales=plane[:],
+                in_=grouped[:].rearrange("p j t -> p (j t)"),
+            )
+            state[("xq", b)] = (codes, plane)
+
+        def mm_z(b):
+            codes, plane = state[("xq", b)]
+            z_ps = pz.tile([P, 4, ND, NW], F32, name="z_ps")
+            for jt in range(4):
+                cols = slice(jt * P, (jt + 1) * P)
+                nc.tensor.matmul_mx(
+                    out=z_ps[:, jt].rearrange("p d c -> p (d c)"),
+                    lhsT=codes[:, cols].bitcast(FP8X4),
+                    lhsT_scale=plane[:, cols],
+                    rhs=w_codes[:, 0:P].bitcast(FP8X4),
+                    rhs_scale=w_plane[:, 0:P],
+                    start=True,
+                    stop=True,
+                )
+            state[("z_ps", b)] = z_ps
+
+        def mm_r(b):
+            codes, plane = state[("xq", b)]
+            r_ps = pr.tile([P, NJ], F32, name="r_ps")
+            nc.tensor.matmul_mx(
+                out=r_ps[:],
+                lhsT=w_codes[:, P : 2 * P].bitcast(FP8X4),
+                lhsT_scale=w_plane[:, P : 2 * P],
+                rhs=codes[:].bitcast(FP8X4),
+                rhs_scale=plane[:],
+                start=True,
+                stop=True,
+            )
+            state[("r_ps", b)] = r_ps
+
+        def row_max(b):
+            r_ps = state[("r_ps", b)]
+            nc.vector.tensor_reduce(
+                out=nm[:, b : b + 1], in_=r_ps[:], axis=AX.X, op=ALU.max, negate=True
+            )
+
+        def tanh1(b):
+            z_ps = state[("z_ps", b)]
+            if b % 2 == 0:
+                state[("acc", b // 2)] = small.tile([P, 2, 2 * ND], F32, name="acc")
+            acc = state[("acc", b // 2)]
+            t_raw = tp.tile([P, ND, NW, 4], F32, name="t_raw")
+            for d in range(ND):
+                k = (b % 2) * ND + d
+                nc.scalar.activation(
+                    out=t_raw[:, d],
+                    in_=z_ps[:, :, d, :].rearrange("p t c -> p c t"),
+                    func=ACT.Tanh,
+                    accum_out=acc[:, 0, k : k + 1],
+                )
+            state[("t_raw", b)] = t_raw
+
+        def square1(b):
+            acc = state[("acc", b // 2)]
+            t_raw = state[("t_raw", b)]
+            for d in range(ND):
+                k = (b % 2) * ND + d
+                sq = junk.tile([P, P], BF16, name="sq")
+                nc.scalar.activation(
+                    out=sq[:],
+                    in_=t_raw[:, d].rearrange("p c t -> p (c t)"),
+                    func=ACT.Square,
+                    accum_out=acc[:, 1, k : k + 1],
+                )
+
+        def exp1(b):
+            r_ps = state[("r_ps", b)]
+            ex = junk.tile([P, NJ], BF16, name="ex")
+            nc.scalar.activation(
+                out=ex[:],
+                in_=r_ps[:],
+                func=ACT.Exp,
+                bias=nm[:, b : b + 1],
+                scale=1.0,
+                accum_out=se[:, b : b + 1],
+            )
+
+        def moments(mom_ps, n, count, tag):
+            mom = small.tile([P, 2 * n], F32, name="mom" + tag)
+            nc.vector.tensor_copy(out=mom[:], in_=mom_ps)
+            msq = small.tile([P, n], F32, name="msq" + tag)
+            nc.gpsimd.tensor_tensor(out=msq[:], in0=mom[:, 0:n], in1=mom[:, 0:n], op=ALU.mult)
+            var = small.tile([P, n], F32, name="var" + tag)
+            nc.gpsimd.tensor_tensor(out=var[:], in0=mom[:, n : 2 * n], in1=msq[:], op=ALU.subtract)
+            varc = small.tile([P, n], F32, name="varc" + tag)
+            nc.gpsimd.tensor_scalar(
+                out=varc[:], in0=var[:], scalar1=0.0, scalar2=count / (count - 1.0),
+                op0=ALU.max, op1=ALU.mult,
+            )
+            sd = small.tile([P, n], F32, name="sd" + tag)
+            nc.gpsimd.tensor_tensor(out=sd[:], in0=varc[:], in1=half[:, 0:n], op=ALU.pow)
+            sde = small.tile([P, n], F32, name="sde" + tag)
+            nc.gpsimd.tensor_scalar(
+                out=sde[:], in0=sd[:], scalar1=1.0, scalar2=EPS, op0=ALU.mult, op1=ALU.add
+            )
+            return mom, sde
+
+        def recip(sde, n, tag):
+            rstd = small.tile([P, n], F32, name="rstd" + tag)
+            nc.vector.reciprocal(out=rstd[:], in_=sde[:])
+            return rstd
+
+        def stats1_mm(h):
+            acc = state[("acc", h)]
+            mom_ps = pm.tile([P, 4 * ND], F32, name="mom_ps")
+            nc.tensor.matmul(
+                out=mom_ps[:], lhsT=ones1[:], rhs=acc[:].rearrange("p s n -> p (s n)"),
+                start=True, stop=True,
+            )
+            state[("mom_ps", h)] = mom_ps
+
+        def stats1_chain(h):
+            state[("st", h)] = moments(state[("mom_ps", h)][:], 2 * ND, float(N1), "a")
+
+        def stats1_recip(h):
+            mom, sde = state[("st", h)]
+            state[("st", h)] = (mom, recip(sde, 2 * ND, "a"))
+
+        def affine(b):
+            h = b // 2
+            mom, rstd = state[("st", h)]
+            if b % 4 == 0:
+                state[("tg", b // 4)] = (
+                    tq.tile([P, 4, ND, P], BF16, align_bytes=64, name="tg"),
+                    tq.tile([P, 4 * P], U32, align_bytes=64, name="t_codes"),
+                    tq.tile([P, 4 * P], U8, align_bytes=64, name="t_plane"),
+                )
+            tg, t_codes, t_plane = state[("tg", b // 4)]
+            t_raw = state[("t_raw", b)]
+            for d in range(ND):
+                k = (b % 2) * ND + d
+                nc.vector.tensor_scalar(
+                    out=tg[:, b % 4, d, :],
+                    in0=t_raw[:, d].rearrange("p c t -> p (c t)"),
+                    scalar1=mom[:, k : k + 1],
+                    scalar2=rstd[:, k : k + 1],
+                    op0=ALU.subtract,
+                    op1=ALU.mult,
+                )
+
+        def quant_t(h):
+            tg, t_codes, t_plane = state[("tg", h // 2)]
+            lo = (h % 2) * 2
+            cols = slice(lo * P, (lo + 2) * P)
+            nc.vector.quantize_mx(
+                out=t_codes[:, cols].bitcast(FP8X4),
+                scales=t_plane[:, cols],
+                in_=tg[:, lo : lo + 2].rearrange("p b d e -> p (b d e)"),
+            )
+
+        def s2_mm(q):
+            tg, t_codes, t_plane = state[("tg", q)]
+            u_ps = pu.tile([P, 4, ND, NW], F32, name="u_ps")
+            nc.tensor.matmul_mx(
+                out=u_ps[:].rearrange("p b d c -> p (b d c)"),
+                lhsT=p_codes[:].bitcast(FP8X4),
+                lhsT_scale=p_plane[:],
+                rhs=t_codes[:].bitcast(FP8X4),
+                rhs_scale=t_plane[:],
+                start=True,
+                stop=True,
+            )
+            state[("u_ps", q)] = u_ps
+
+        def s2_tanh(q):
+            u_ps = state[("u_ps", q)]
+            bs = slice(4 * q, 4 * q + 4)
+            for d in range(ND):
+                rows = slice(NW * d, NW * (d + 1))
+                nc.scalar.activation(out=u_all[rows, bs, :], in_=u_ps[rows, :, d, :], func=ACT.Tanh)
+            usq = fin.tile([P, 4, NW], F32, name="usq")
+            nc.scalar.activation(out=usq[:], in_=u_all[:, bs, :], func=ACT.Square)
+            state[("usq", q)] = usq
+
+        def s2_sums(q):
+            bs = slice(4 * q, 4 * q + 4)
+            usq = state[("usq", q)]
+            st2 = small.tile([P, 2, 4], F32, name="st2")
+            nc.vector.tensor_reduce(out=st2[:, 0, :], in_=u_all[:, bs, :], axis=AX.X, op=ALU.add)
+            nc.vector.tensor_reduce(out=st2[:, 1, :], in_=usq[:], axis=AX.X, op=ALU.add)
+            mom2_ps = pm2.tile([P, 8], F32, name="mom2_ps")
+            nc.tensor.matmul(
+                out=mom2_ps[:], lhsT=blk2[:], rhs=st2[:].rearrange("p s n -> p (s n)"),
+                start=True, stop=True,
+            )
+            state[("mom2_ps", q)] = mom2_ps
+
+        def s2_chain(q):
+            state[("st2", q)] = moments(state[("mom2_ps", q)][:], 4, float(N2), "b")
+
+        def s2_out(q):
+            bs = slice(4 * q, 4 * q + 4)
+            mom2, sde2 = state[("st2", q)]
+            rstd2 = recip(sde2, 4, "b")
+            cen = fin.tile([P, 4, NW], F32, name="cen")
+            nc.vector.tensor_tensor(
+                out=cen[:], in0=u_all[:, bs, :],
+                in1=mom2[:, 0:4].unsqueeze(2).to_broadcast([P, 4, NW]), op=ALU.subtract,
+            )
+            res = fin.tile([P, 4, NW], F32, name="res")
+            nc.vector.tensor_tensor(
+                out=res[:], in0=cen[:],
+                in1=rstd2[:].unsqueeze(2).to_broadcast([P, 4, NW]), op=ALU.mult,
+            )
+            nc.sync.dma_start(out=out_0[bs].rearrange("b d q c -> (d q) b c"), in_=res[:])
+
+        def mass():
+            tr_ps = ptr.tile([P, 2, P], F32, name="tr_ps")
+            nc.tensor.transpose(out=tr_ps[:, 0, :], in_=nm[:], identity=ident[:])
+            nc.tensor.transpose(out=tr_ps[:, 1, :], in_=se[:], identity=ident[:])
+            nmt = tr_ps[0:NB, 0, :].rearrange("b (d c) -> b d c", d=ND)
+            set_ = tr_ps[0:NB, 1, :].rearrange("b (d c) -> b d c", d=ND)
+            ntop = fin.tile([NB, ND], F32, name="ntop")
+            nc.vector.tensor_reduce(out=ntop[:], in_=nmt, axis=AX.X, op=ALU.min)
+            diff = fin.tile([NB, ND, NW], F32, name="diff")
+            nc.vector.tensor_tensor(
+                out=diff[:], in0=ntop[:].unsqueeze(2).to_broadcast([NB, ND, NW]), in1=nmt,
+                op=ALU.subtract,
+            )
+            corr = fin.tile([NB, ND, NW], F32, name="corr")
+            nc.scalar.activation(out=corr[:], in_=diff[:], func=ACT.Exp)
+            part = fin.tile([NB, ND, NW], F32, name="part")
+            nc.vector.tensor_tensor(out=part[:], in0=corr[:], in1=set_, op=ALU.mult)
+            den = fin.tile([NB, ND], F32, name="den")
+            nc.vector.tensor_reduce(out=den[:], in_=part[:], axis=AX.X, op=ALU.add)
+            rden = fin.tile([NB, ND], F32, name="rden")
+            nc.vector.reciprocal(out=rden[:], in_=den[:])
+            mres = fin.tile([NB, ND, NW], F32, name="mres")
+            nc.vector.tensor_tensor(
+                out=mres[:], in0=part[:],
+                in1=rden[:].unsqueeze(2).to_broadcast([NB, ND, NW]), op=ALU.mult,
+            )
+            nc.sync.dma_start(out=out_1, in_=mres[:])
+
+        def on(v, step=1, rem=0):
+            return 0 <= v < NB and v % step == rem
+
+        late_at = {NB: 1, NB + 1: 3, NB + 3: 1, NB + 4: 2, NB + 5: 1}
+        late_next = [NB - LATE]
+
+        for i in range(-2, NB + 14):
+            early = on(i) and i < NB - LATE
+            if on(i + 2):
+                regroup_s(i + 2)
+            if on(i + 1):
+                quant_x(i + 1)
+                mm_z(i + 1)
+                if i + 1 < NB - LATE:
+                    mm_r(i + 1)
+            if early:
+                row_max(i)
+            if on(i):
+                tanh1(i)
+            if on(i - 2, 2, 0):
+                stats1_chain((i - 2) // 2)
+            if on(i - 10, 4, 0):
+                s2_chain((i - 10) // 4)
+            if i == NB + 6:
+                mass()
+            if on(i - 4, 2, 0):
+                stats1_recip((i - 4) // 2)
+            if on(i + 2):
+                regroup_v(i + 2)
+            if i == 1:
+                prep_p_copy()
+            if on(i):
+                square1(i)
+                if i % 2 == 1:
+                    stats1_mm(i // 2)
+            if early:
+                exp1(i)
+            if on(i - 6, 2, 0):
+                quant_t((i - 6) // 2)
+                if (i - 6) % 4 == 2:
+                    s2_mm((i - 8) // 4)
+            if i == 2:
+                prep_p_quant()
+            if on(i - 4):
+                affine(i - 4)
+            if on(i - 8, 4, 0):
+                s2_tanh((i - 8) // 4)
+            if on(i - 9, 4, 0):
+                s2_sums((i - 9) // 4)
+            if on(i - 13, 4, 0):
+                s2_out((i - 13) // 4)
+            for n in range(late_at.get(i, 0)):
+                b = late_next[0]
+                late_next[0] = b + 1
+                mm_r(b)
+                row_max(b)
+                exp1(b)
+        assert late_next[0] == NB

@@ -1,3 +1,4 @@
+import math
 from contextlib import ExitStack
 
 import concourse.mybir as mybir
@@ -5,6 +6,7 @@ from concourse.masks import make_identity
 
 F32 = mybir.dt.float32
 BF16 = mybir.dt.bfloat16
+I32 = mybir.dt.int32
 U32 = mybir.dt.uint32
 U8 = mybir.dt.uint8
 FP8X4 = mybir.dt.float8_e4m3fn_x4
@@ -21,8 +23,13 @@ ND = 4
 EPS = 1e-5
 N1 = NJ * NW
 N2 = NW * NW
+ROOT_C1 = math.sqrt(N1 / (N1 - 1.0))
+ROOT_C2 = math.sqrt(N2 / (N2 - 1.0))
+MAGIC = 0x5F3759DF >> 7
 S_COLS = 128
-LATE = 8
+LATE_EXP = 12
+LATE_MAX = 12
+SW = 28
 
 FLOPS = 2 * NB * ND * (2 * NI * NJ * NW + NW * NJ * NW)
 
@@ -31,20 +38,19 @@ def tile_selfprojectiondev_pb_t_kernel(tc, x, o_xi, p_xi, rel_o_xi, out_0, out_1
     nc = tc.nc
     with ExitStack() as ctx:
         const = ctx.enter_context(tc.tile_pool(name="const", bufs=1))
-        rawp = ctx.enter_context(tc.tile_pool(name="rawp", bufs=14))
+        rawp = ctx.enter_context(tc.tile_pool(name="rawp", bufs=8))
         grp = ctx.enter_context(tc.tile_pool(name="grp", bufs=3))
         xq = ctx.enter_context(tc.tile_pool(name="xq", bufs=3))
-        xl = ctx.enter_context(tc.tile_pool(name="xl", bufs=LATE))
-        tp = ctx.enter_context(tc.tile_pool(name="tp", bufs=8))
+        xl = ctx.enter_context(tc.tile_pool(name="xl", bufs=LATE_EXP))
+        tp = ctx.enter_context(tc.tile_pool(name="tp", bufs=11))
         junk = ctx.enter_context(tc.tile_pool(name="junk", bufs=2))
-        small = ctx.enter_context(tc.tile_pool(name="small", bufs=4))
+        small = ctx.enter_context(tc.tile_pool(name="small", bufs=3))
         tq = ctx.enter_context(tc.tile_pool(name="tq", bufs=2))
-        fin = ctx.enter_context(tc.tile_pool(name="fin", bufs=2))
+        fin = ctx.enter_context(tc.tile_pool(name="fin", bufs=3))
         pz = ctx.enter_context(tc.psum_pool(name="pz", bufs=2))
         pr = ctx.enter_context(tc.psum_pool(name="pr", bufs=2))
-        pm = ctx.enter_context(tc.psum_pool(name="pm", bufs=1))
+        pm = ctx.enter_context(tc.psum_pool(name="pm", bufs=2))
         pu = ctx.enter_context(tc.psum_pool(name="pu", bufs=1))
-        pm2 = ctx.enter_context(tc.psum_pool(name="pm2", bufs=1))
         ptr = ctx.enter_context(tc.psum_pool(name="ptr", bufs=1))
         ctx.enter_context(tc.manual_schedule())
 
@@ -79,12 +85,16 @@ def tile_selfprojectiondev_pb_t_kernel(tc, x, o_xi, p_xi, rel_o_xi, out_0, out_1
 
         ones1 = const.tile([P, P], F32)
         nc.gpsimd.memset(ones1[:], 1.0 / N1)
+        ones1s = const.tile([P, P], F32)
+        nc.gpsimd.memset(ones1s[:], ROOT_C1 / N1)
         blk2 = const.tile([P, P], F32)
         nc.gpsimd.memset(blk2[:], 0.0)
+        blk2s = const.tile([P, P], F32)
+        nc.gpsimd.memset(blk2s[:], 0.0)
         for d in range(ND):
-            nc.gpsimd.memset(blk2[NW * d : NW * (d + 1), NW * d : NW * (d + 1)], 1.0 / N2)
-        half = const.tile([P, 8], F32)
-        nc.gpsimd.memset(half[:], 0.5)
+            rows = slice(NW * d, NW * (d + 1))
+            nc.gpsimd.memset(blk2[rows, rows], 1.0 / N2)
+            nc.gpsimd.memset(blk2s[rows, rows], ROOT_C2 / N2)
         ident = const.tile([P, P], F32)
         make_identity(nc, ident[:])
         nm = const.tile([P, P], F32)
@@ -124,6 +134,19 @@ def tile_selfprojectiondev_pb_t_kernel(tc, x, o_xi, p_xi, rel_o_xi, out_0, out_1
             )
 
         state = {}
+        pending = []
+        done = [0]
+
+        def small_step():
+            if done[0] < len(pending):
+                pending[done[0]]()
+                done[0] = done[0] + 1
+
+        def flush(upto):
+            while_guard = range(len(pending))
+            for n in while_guard:
+                if done[0] < upto:
+                    small_step()
 
         def regroup_s(b):
             grouped = grp.tile([P, NJ, 4], BF16, align_bytes=64, name="grouped")
@@ -143,10 +166,11 @@ def tile_selfprojectiondev_pb_t_kernel(tc, x, o_xi, p_xi, rel_o_xi, out_0, out_1
                 out=grouped[:, 0:jv, :].rearrange("p (c i) t -> p c t i", i=4),
                 in_=src[:, :, 0:jv].rearrange("p t (c i) -> p c t i", i=4),
             )
+            small_step()
 
         def quant_x(b):
             grouped = state[("grouped", b)]
-            pool = xl if b >= NB - LATE else xq
+            pool = xl if b >= NB - LATE_EXP else xq
             codes = pool.tile([P, NJ], U32, align_bytes=64, name="codes")
             plane = pool.tile([P, NJ], U8, align_bytes=64, name="plane")
             nc.vector.quantize_mx(
@@ -155,6 +179,7 @@ def tile_selfprojectiondev_pb_t_kernel(tc, x, o_xi, p_xi, rel_o_xi, out_0, out_1
                 in_=grouped[:].rearrange("p j t -> p (j t)"),
             )
             state[("xq", b)] = (codes, plane)
+            small_step()
 
         def mm_z(b):
             codes, plane = state[("xq", b)]
@@ -191,15 +216,16 @@ def tile_selfprojectiondev_pb_t_kernel(tc, x, o_xi, p_xi, rel_o_xi, out_0, out_1
             nc.vector.tensor_reduce(
                 out=nm[:, b : b + 1], in_=r_ps[:], axis=AX.X, op=ALU.max, negate=True
             )
+            small_step()
 
         def tanh1(b):
             z_ps = state[("z_ps", b)]
-            if b % 2 == 0:
-                state[("acc", b // 2)] = small.tile([P, 2, 2 * ND], F32, name="acc")
-            acc = state[("acc", b // 2)]
+            if b % 4 == 0:
+                state[("acc", b // 4)] = small.tile([P, 2, 4 * ND], F32, name="acc")
+            acc = state[("acc", b // 4)]
             t_raw = tp.tile([P, ND, NW, 4], F32, name="t_raw")
             for d in range(ND):
-                k = (b % 2) * ND + d
+                k = (b % 4) * ND + d
                 nc.scalar.activation(
                     out=t_raw[:, d],
                     in_=z_ps[:, :, d, :].rearrange("p t c -> p c t"),
@@ -209,15 +235,16 @@ def tile_selfprojectiondev_pb_t_kernel(tc, x, o_xi, p_xi, rel_o_xi, out_0, out_1
             state[("t_raw", b)] = t_raw
 
         def square1(b):
-            acc = state[("acc", b // 2)]
+            acc = state[("acc", b // 4)]
             t_raw = state[("t_raw", b)]
             for d in range(ND):
-                k = (b % 2) * ND + d
+                k = (b % 4) * ND + d
                 sq = junk.tile([P, P], BF16, name="sq")
                 nc.scalar.activation(
                     out=sq[:],
                     in_=t_raw[:, d].rearrange("p c t -> p (c t)"),
                     func=ACT.Square,
+                    scale=ROOT_C1,
                     accum_out=acc[:, 1, k : k + 1],
                 )
 
@@ -233,50 +260,61 @@ def tile_selfprojectiondev_pb_t_kernel(tc, x, o_xi, p_xi, rel_o_xi, out_0, out_1
                 accum_out=se[:, b : b + 1],
             )
 
-        def moments(mom_ps, n, count, tag):
-            mom = small.tile([P, 2 * n], F32, name="mom" + tag)
-            nc.vector.tensor_copy(out=mom[:], in_=mom_ps)
-            msq = small.tile([P, n], F32, name="msq" + tag)
-            nc.gpsimd.tensor_tensor(out=msq[:], in0=mom[:, 0:n], in1=mom[:, 0:n], op=ALU.mult)
-            var = small.tile([P, n], F32, name="var" + tag)
-            nc.gpsimd.tensor_tensor(out=var[:], in0=mom[:, n : 2 * n], in1=msq[:], op=ALU.subtract)
-            varc = small.tile([P, n], F32, name="varc" + tag)
-            nc.gpsimd.tensor_scalar(
-                out=varc[:], in0=var[:], scalar1=0.0, scalar2=count / (count - 1.0),
-                op0=ALU.max, op1=ALU.mult,
-            )
-            sd = small.tile([P, n], F32, name="sd" + tag)
-            nc.gpsimd.tensor_tensor(out=sd[:], in0=varc[:], in1=half[:, 0:n], op=ALU.pow)
-            sde = small.tile([P, n], F32, name="sde" + tag)
-            nc.gpsimd.tensor_scalar(
-                out=sde[:], in0=sd[:], scalar1=1.0, scalar2=EPS, op0=ALU.mult, op1=ALU.add
-            )
-            return mom, sde
+        def mom_tile(c):
+            if ("mom_ps", c) not in state:
+                state[("mom_ps", c)] = pm.tile([P, 3, SW], F32, name="mom_ps")
+            return state[("mom_ps", c)]
 
-        def recip(sde, n, tag):
-            rstd = small.tile([P, n], F32, name="rstd" + tag)
-            nc.vector.reciprocal(out=rstd[:], in_=sde[:])
-            return rstd
+        def moments_mm(c, lo, hi, sums, squares, plain, scaled):
+            mom_ps = mom_tile(c)
+            nc.tensor.matmul(out=mom_ps[:, 0, lo:hi], lhsT=plain[:], rhs=sums, start=True, stop=True)
+            nc.tensor.matmul(out=mom_ps[:, 1, lo:hi], lhsT=plain[:], rhs=squares, start=True, stop=True)
+            nc.tensor.matmul(out=mom_ps[:, 2, lo:hi], lhsT=scaled[:], rhs=sums, start=True, stop=True)
 
-        def stats1_mm(h):
-            acc = state[("acc", h)]
-            mom_ps = pm.tile([P, 4 * ND], F32, name="mom_ps")
-            nc.tensor.matmul(
-                out=mom_ps[:], lhsT=ones1[:], rhs=acc[:].rearrange("p s n -> p (s n)"),
-                start=True, stop=True,
-            )
-            state[("mom_ps", h)] = mom_ps
-
-        def stats1_chain(h):
-            state[("st", h)] = moments(state[("mom_ps", h)][:], 2 * ND, float(N1), "a")
-
-        def stats1_recip(h):
-            mom, sde = state[("st", h)]
-            state[("st", h)] = (mom, recip(sde, 2 * ND, "a"))
+        def chain(c, lo, hi):
+            mom_ps = mom_tile(c)
+            mom = small.tile([P, 3, SW], F32, name="mom")
+            var = small.tile([P, SW], F32, name="var")
+            tmp = small.tile([P, SW], F32, name="tmp")
+            bits = small.tile([P, SW], I32, name="bits")
+            guess = small.tile([P, SW], I32, name="guess")
+            rstd = small.tile([P, SW], F32, name="rstd")
+            cs = slice(lo, hi)
+            y = guess[:, cs].bitcast(F32)
+            v = var[:, cs]
+            w = tmp[:, cs]
+            tt = nc.vector.tensor_tensor
+            ts = nc.vector.tensor_scalar
+            stt = nc.vector.scalar_tensor_tensor
+            ops = [
+                lambda: nc.vector.tensor_copy(out=mom[:, :, cs], in_=mom_ps[:, :, cs]),
+                lambda: tt(out=w, in0=mom[:, 2, cs], in1=mom[:, 2, cs], op=ALU.mult),
+                lambda: tt(out=v, in0=mom[:, 1, cs], in1=w, op=ALU.subtract),
+                lambda: ts(out=v, in0=v, scalar1=1e-30, scalar2=None, op0=ALU.max),
+                lambda: ts(out=bits[:, cs], in0=v.bitcast(I32), scalar1=8, scalar2=None,
+                           op0=ALU.logical_shift_right),
+                lambda: ts(out=bits[:, cs], in0=bits[:, cs], scalar1=-1.0, scalar2=float(MAGIC),
+                           op0=ALU.mult, op1=ALU.add),
+                lambda: ts(out=guess[:, cs], in0=bits[:, cs], scalar1=7, scalar2=None,
+                           op0=ALU.logical_shift_left),
+            ]
+            for n in range(3):
+                ops.extend([
+                    lambda: tt(out=w, in0=y, in1=y, op=ALU.mult),
+                    lambda: stt(out=w, in0=w, scalar=-0.5, in1=v, op0=ALU.mult, op1=ALU.mult),
+                    lambda: stt(out=y, in0=w, scalar=1.5, in1=y, op0=ALU.add, op1=ALU.mult),
+                ])
+            ops.extend([
+                lambda: tt(out=w, in0=v, in1=y, op=ALU.mult),
+                lambda: ts(out=w, in0=w, scalar1=EPS, scalar2=None, op0=ALU.add),
+                lambda: nc.vector.reciprocal(out=rstd[:, cs], in_=w),
+            ])
+            pending.extend(ops)
+            state[("st", c)] = (mom, rstd, len(pending))
 
         def affine(b):
-            h = b // 2
-            mom, rstd = state[("st", h)]
+            mom, rstd, end = state[("st", b // 4)]
+            flush(end)
             if b % 4 == 0:
                 state[("tg", b // 4)] = (
                     tq.tile([P, 4, ND, P], BF16, align_bytes=64, name="tg"),
@@ -286,15 +324,16 @@ def tile_selfprojectiondev_pb_t_kernel(tc, x, o_xi, p_xi, rel_o_xi, out_0, out_1
             tg, t_codes, t_plane = state[("tg", b // 4)]
             t_raw = state[("t_raw", b)]
             for d in range(ND):
-                k = (b % 2) * ND + d
+                k = (b % 4) * ND + d
                 nc.vector.tensor_scalar(
                     out=tg[:, b % 4, d, :],
                     in0=t_raw[:, d].rearrange("p c t -> p (c t)"),
-                    scalar1=mom[:, k : k + 1],
+                    scalar1=mom[:, 0, k : k + 1],
                     scalar2=rstd[:, k : k + 1],
                     op0=ALU.subtract,
                     op1=ALU.mult,
                 )
+                small_step()
 
         def quant_t(h):
             tg, t_codes, t_plane = state[("tg", h // 2)]
@@ -305,6 +344,7 @@ def tile_selfprojectiondev_pb_t_kernel(tc, x, o_xi, p_xi, rel_o_xi, out_0, out_1
                 scales=t_plane[:, cols],
                 in_=tg[:, lo : lo + 2].rearrange("p b d e -> p (b d e)"),
             )
+            small_step()
 
         def s2_mm(q):
             tg, t_codes, t_plane = state[("tg", q)]
@@ -327,39 +367,42 @@ def tile_selfprojectiondev_pb_t_kernel(tc, x, o_xi, p_xi, rel_o_xi, out_0, out_1
                 rows = slice(NW * d, NW * (d + 1))
                 nc.scalar.activation(out=u_all[rows, bs, :], in_=u_ps[rows, :, d, :], func=ACT.Tanh)
             usq = fin.tile([P, 4, NW], F32, name="usq")
-            nc.scalar.activation(out=usq[:], in_=u_all[:, bs, :], func=ACT.Square)
+            nc.scalar.activation(out=usq[:], in_=u_all[:, bs, :], func=ACT.Square, scale=ROOT_C2)
             state[("usq", q)] = usq
+
+        def s2_place(q):
+            if q <= 4:
+                return q + 3, 16
+            return 8, 16 + 4 * (q - 5)
 
         def s2_sums(q):
             bs = slice(4 * q, 4 * q + 4)
             usq = state[("usq", q)]
             st2 = small.tile([P, 2, 4], F32, name="st2")
             nc.vector.tensor_reduce(out=st2[:, 0, :], in_=u_all[:, bs, :], axis=AX.X, op=ALU.add)
+            small_step()
             nc.vector.tensor_reduce(out=st2[:, 1, :], in_=usq[:], axis=AX.X, op=ALU.add)
-            mom2_ps = pm2.tile([P, 8], F32, name="mom2_ps")
-            nc.tensor.matmul(
-                out=mom2_ps[:], lhsT=blk2[:], rhs=st2[:].rearrange("p s n -> p (s n)"),
-                start=True, stop=True,
-            )
-            state[("mom2_ps", q)] = mom2_ps
-
-        def s2_chain(q):
-            state[("st2", q)] = moments(state[("mom2_ps", q)][:], 4, float(N2), "b")
+            small_step()
+            c, lo = s2_place(q)
+            moments_mm(c, lo, lo + 4, st2[:, 0, :], st2[:, 1, :], blk2, blk2s)
 
         def s2_out(q):
             bs = slice(4 * q, 4 * q + 4)
-            mom2, sde2 = state[("st2", q)]
-            rstd2 = recip(sde2, 4, "b")
+            c, lo = s2_place(q)
+            mom, rstd, end = state[("st", c)]
+            flush(end)
             cen = fin.tile([P, 4, NW], F32, name="cen")
             nc.vector.tensor_tensor(
                 out=cen[:], in0=u_all[:, bs, :],
-                in1=mom2[:, 0:4].unsqueeze(2).to_broadcast([P, 4, NW]), op=ALU.subtract,
+                in1=mom[:, 0, lo : lo + 4].unsqueeze(2).to_broadcast([P, 4, NW]), op=ALU.subtract,
             )
+            small_step()
             res = fin.tile([P, 4, NW], F32, name="res")
             nc.vector.tensor_tensor(
                 out=res[:], in0=cen[:],
-                in1=rstd2[:].unsqueeze(2).to_broadcast([P, 4, NW]), op=ALU.mult,
+                in1=rstd[:, lo : lo + 4].unsqueeze(2).to_broadcast([P, 4, NW]), op=ALU.mult,
             )
+            small_step()
             nc.sync.dma_start(out=out_0[bs].rearrange("b d q c -> (d q) b c"), in_=res[:])
 
         def mass():
@@ -370,81 +413,92 @@ def tile_selfprojectiondev_pb_t_kernel(tc, x, o_xi, p_xi, rel_o_xi, out_0, out_1
             set_ = tr_ps[0:NB, 1, :].rearrange("b (d c) -> b d c", d=ND)
             ntop = fin.tile([NB, ND], F32, name="ntop")
             nc.vector.tensor_reduce(out=ntop[:], in_=nmt, axis=AX.X, op=ALU.min)
+            small_step()
             diff = fin.tile([NB, ND, NW], F32, name="diff")
             nc.vector.tensor_tensor(
                 out=diff[:], in0=ntop[:].unsqueeze(2).to_broadcast([NB, ND, NW]), in1=nmt,
                 op=ALU.subtract,
             )
+            small_step()
             corr = fin.tile([NB, ND, NW], F32, name="corr")
             nc.scalar.activation(out=corr[:], in_=diff[:], func=ACT.Exp)
+            small_step()
+            small_step()
             part = fin.tile([NB, ND, NW], F32, name="part")
             nc.vector.tensor_tensor(out=part[:], in0=corr[:], in1=set_, op=ALU.mult)
+            small_step()
             den = fin.tile([NB, ND], F32, name="den")
             nc.vector.tensor_reduce(out=den[:], in_=part[:], axis=AX.X, op=ALU.add)
+            small_step()
             rden = fin.tile([NB, ND], F32, name="rden")
             nc.vector.reciprocal(out=rden[:], in_=den[:])
+            small_step()
             mres = fin.tile([NB, ND, NW], F32, name="mres")
             nc.vector.tensor_tensor(
                 out=mres[:], in0=part[:],
                 in1=rden[:].unsqueeze(2).to_broadcast([NB, ND, NW]), op=ALU.mult,
             )
+            small_step()
             nc.sync.dma_start(out=out_1, in_=mres[:])
 
         def on(v, step=1, rem=0):
             return 0 <= v < NB and v % step == rem
 
-        late_at = {NB: 1, NB + 1: 3, NB + 3: 1, NB + 4: 2, NB + 5: 1}
-        late_next = [NB - LATE]
+        late_at = {NB: 2, NB + 1: 2, NB + 2: 2, NB + 6: 1, NB + 7: 3, NB + 8: 2}
+        late_next = [NB - LATE_EXP]
 
-        for i in range(-2, NB + 14):
-            early = on(i) and i < NB - LATE
+        for i in range(-2, NB + 10):
             if on(i + 2):
                 regroup_s(i + 2)
+            if on(i - 4, 4, 0):
+                c = i // 4 - 1
+                chain(c, 0, 20 if c >= 3 else 16)
             if on(i + 1):
                 quant_x(i + 1)
                 mm_z(i + 1)
-                if i + 1 < NB - LATE:
+                if i + 1 < NB - LATE_MAX:
                     mm_r(i + 1)
-            if early:
+            if on(i) and i < NB - LATE_MAX:
                 row_max(i)
             if on(i):
                 tanh1(i)
-            if on(i - 2, 2, 0):
-                stats1_chain((i - 2) // 2)
-            if on(i - 10, 4, 0):
-                s2_chain((i - 10) // 4)
-            if i == NB + 6:
-                mass()
-            if on(i - 4, 2, 0):
-                stats1_recip((i - 4) // 2)
             if on(i + 2):
                 regroup_v(i + 2)
             if i == 1:
                 prep_p_copy()
             if on(i):
                 square1(i)
-                if i % 2 == 1:
-                    stats1_mm(i // 2)
-            if early:
+                if i % 4 == 3:
+                    acc = state[("acc", i // 4)]
+                    moments_mm(i // 4, 0, 16, acc[:, 0, :], acc[:, 1, :], ones1, ones1s)
+            if on(i) and i < NB - LATE_EXP:
                 exp1(i)
-            if on(i - 6, 2, 0):
-                quant_t((i - 6) // 2)
-                if (i - 6) % 4 == 2:
-                    s2_mm((i - 8) // 4)
+            if on(i - 9, 2, 0):
+                quant_t((i - 9) // 2)
+                if (i - 9) % 4 == 2:
+                    s2_mm((i - 11) // 4)
             if i == 2:
                 prep_p_quant()
-            if on(i - 4):
-                affine(i - 4)
-            if on(i - 8, 4, 0):
-                s2_tanh((i - 8) // 4)
-            if on(i - 9, 4, 0):
-                s2_sums((i - 9) // 4)
-            if on(i - 13, 4, 0):
-                s2_out((i - 13) // 4)
+            if on(i - 7):
+                affine(i - 7)
+            if on(i - 11, 4, 0):
+                s2_tanh((i - 11) // 4)
+            if on(i - 12, 4, 0):
+                s2_sums((i - 12) // 4)
+            if on(i - 19, 4, 0) and (i - 19) // 4 <= 4:
+                s2_out((i - 19) // 4)
             for n in range(late_at.get(i, 0)):
                 b = late_next[0]
                 late_next[0] = b + 1
                 mm_r(b)
-                row_max(b)
+                if b >= NB - LATE_MAX:
+                    row_max(b)
                 exp1(b)
+            if i == NB + 9:
+                chain(8, 16, 28)
+                flush(done[0] + 8)
+                mass()
+                for q in range(5, 8):
+                    s2_out(q)
         assert late_next[0] == NB
+        assert done[0] == len(pending)

@@ -26,9 +26,16 @@ N2 = NW * NW
 ROOT_C1 = math.sqrt(N1 / (N1 - 1.0))
 ROOT_C2 = math.sqrt(N2 / (N2 - 1.0))
 MAGIC = 0x5F3759DF >> 7
-S_COLS = 128
-LATE_EXP = 12
-LATE_MAX = 12
+LATE_EXP = 20
+LATE_MAX = 8
+
+
+def s_cols(b):
+    if b < NB - LATE_EXP:
+        return 128
+    if b < NB - LATE_MAX:
+        return 232
+    return 152
 SW = 28
 
 FLOPS = 2 * NB * ND * (2 * NI * NJ * NW + NW * NJ * NW)
@@ -42,16 +49,15 @@ def tile_selfprojectiondev_pb_t_kernel(tc, x, o_xi, p_xi, rel_o_xi, out_0, out_1
         grp = ctx.enter_context(tc.tile_pool(name="grp", bufs=3))
         xq = ctx.enter_context(tc.tile_pool(name="xq", bufs=3))
         xl = ctx.enter_context(tc.tile_pool(name="xl", bufs=LATE_EXP))
-        tp = ctx.enter_context(tc.tile_pool(name="tp", bufs=11))
+        tp = ctx.enter_context(tc.tile_pool(name="tp", bufs=12))
         junk = ctx.enter_context(tc.tile_pool(name="junk", bufs=2))
         small = ctx.enter_context(tc.tile_pool(name="small", bufs=3))
         tq = ctx.enter_context(tc.tile_pool(name="tq", bufs=2))
         fin = ctx.enter_context(tc.tile_pool(name="fin", bufs=3))
         pz = ctx.enter_context(tc.psum_pool(name="pz", bufs=2))
-        pr = ctx.enter_context(tc.psum_pool(name="pr", bufs=2))
+        pr = ctx.enter_context(tc.psum_pool(name="pr", bufs=3))
         pm = ctx.enter_context(tc.psum_pool(name="pm", bufs=2))
         pu = ctx.enter_context(tc.psum_pool(name="pu", bufs=1))
-        ptr = ctx.enter_context(tc.psum_pool(name="ptr", bufs=1))
         ctx.enter_context(tc.manual_schedule())
 
         raw_w = const.tile([P, 2, ND, 4, NW], BF16)
@@ -152,7 +158,7 @@ def tile_selfprojectiondev_pb_t_kernel(tc, x, o_xi, p_xi, rel_o_xi, out_0, out_1
             grouped = grp.tile([P, NJ, 4], BF16, align_bytes=64, name="grouped")
             state[("grouped", b)] = grouped
             src = raws[b // 2][:, b % 2]
-            jv = NJ - S_COLS
+            jv = NJ - s_cols(b)
             nc.scalar.copy(
                 out=grouped[:, jv:NJ, :].rearrange("p (c i) t -> p c t i", i=4),
                 in_=src[:, :, jv:NJ].rearrange("p t (c i) -> p c t i", i=4),
@@ -161,7 +167,7 @@ def tile_selfprojectiondev_pb_t_kernel(tc, x, o_xi, p_xi, rel_o_xi, out_0, out_1
         def regroup_v(b):
             grouped = state[("grouped", b)]
             src = raws[b // 2][:, b % 2]
-            jv = NJ - S_COLS
+            jv = NJ - s_cols(b)
             nc.vector.tensor_copy(
                 out=grouped[:, 0:jv, :].rearrange("p (c i) t -> p c t i", i=4),
                 in_=src[:, :, 0:jv].rearrange("p t (c i) -> p c t i", i=4),
@@ -348,7 +354,7 @@ def tile_selfprojectiondev_pb_t_kernel(tc, x, o_xi, p_xi, rel_o_xi, out_0, out_1
 
         def s2_mm(q):
             tg, t_codes, t_plane = state[("tg", q)]
-            u_ps = pu.tile([P, 4, ND, NW], F32, name="u_ps")
+            u_ps = pu.tile([P, 4, ND, NW], F32, name="u_ps", tag="u_ps")
             nc.tensor.matmul_mx(
                 out=u_ps[:].rearrange("p b d c -> p (b d c)"),
                 lhsT=p_codes[:].bitcast(FP8X4),
@@ -406,7 +412,7 @@ def tile_selfprojectiondev_pb_t_kernel(tc, x, o_xi, p_xi, rel_o_xi, out_0, out_1
             nc.sync.dma_start(out=out_0[bs].rearrange("b d q c -> (d q) b c"), in_=res[:])
 
         def mass():
-            tr_ps = ptr.tile([P, 2, P], F32, name="tr_ps")
+            tr_ps = pu.tile([P, 2, P], F32, name="tr_ps", tag="u_ps")
             nc.tensor.transpose(out=tr_ps[:, 0, :], in_=nm[:], identity=ident[:])
             nc.tensor.transpose(out=tr_ps[:, 1, :], in_=se[:], identity=ident[:])
             nmt = tr_ps[0:NB, 0, :].rearrange("b (d c) -> b d c", d=ND)
@@ -444,14 +450,18 @@ def tile_selfprojectiondev_pb_t_kernel(tc, x, o_xi, p_xi, rel_o_xi, out_0, out_1
         def on(v, step=1, rem=0):
             return 0 <= v < NB and v % step == rem
 
-        late_at = {NB: 2, NB + 1: 2, NB + 2: 2, NB + 6: 1, NB + 7: 3, NB + 8: 2}
+        late_at = {NB + 1: 3, NB + 2: 3, NB + 3: 3, NB + 4: 2, NB + 5: 2, NB + 6: 2, NB + 7: 1, NB + 8: 2, NB + 9: 2}
         late_next = [NB - LATE_EXP]
 
-        for i in range(-2, NB + 10):
+        for i in range(-2, NB + 12):
+            if on(i - 1) and i - 1 < NB - LATE_EXP:
+                exp1(i - 1)
+            if on(i - 13, 4, 0):
+                s2_tanh((i - 13) // 4)
             if on(i + 2):
                 regroup_s(i + 2)
-            if on(i - 4, 4, 0):
-                c = i // 4 - 1
+            if on(i - 5, 4, 0):
+                c = (i - 5) // 4
                 chain(c, 0, 20 if c >= 3 else 16)
             if on(i + 1):
                 quant_x(i + 1)
@@ -471,22 +481,18 @@ def tile_selfprojectiondev_pb_t_kernel(tc, x, o_xi, p_xi, rel_o_xi, out_0, out_1
                 if i % 4 == 3:
                     acc = state[("acc", i // 4)]
                     moments_mm(i // 4, 0, 16, acc[:, 0, :], acc[:, 1, :], ones1, ones1s)
-            if on(i) and i < NB - LATE_EXP:
-                exp1(i)
-            if on(i - 9, 2, 0):
-                quant_t((i - 9) // 2)
-                if (i - 9) % 4 == 2:
-                    s2_mm((i - 11) // 4)
+            if on(i - 10, 2, 0):
+                quant_t((i - 10) // 2)
+                if (i - 10) % 4 == 2:
+                    s2_mm((i - 12) // 4)
             if i == 2:
                 prep_p_quant()
-            if on(i - 7):
-                affine(i - 7)
-            if on(i - 11, 4, 0):
-                s2_tanh((i - 11) // 4)
-            if on(i - 12, 4, 0):
-                s2_sums((i - 12) // 4)
-            if on(i - 19, 4, 0) and (i - 19) // 4 <= 4:
-                s2_out((i - 19) // 4)
+            if on(i - 8):
+                affine(i - 8)
+            if on(i - 14, 4, 0):
+                s2_sums((i - 14) // 4)
+            if on(i - 20, 4, 0) and (i - 20) // 4 <= 4:
+                s2_out((i - 20) // 4)
             for n in range(late_at.get(i, 0)):
                 b = late_next[0]
                 late_next[0] = b + 1
@@ -494,7 +500,7 @@ def tile_selfprojectiondev_pb_t_kernel(tc, x, o_xi, p_xi, rel_o_xi, out_0, out_1
                 if b >= NB - LATE_MAX:
                     row_max(b)
                 exp1(b)
-            if i == NB + 9:
+            if i == NB + 11:
                 chain(8, 16, 28)
                 flush(done[0] + 8)
                 mass()

@@ -26,17 +26,21 @@ N2 = NW * NW
 ROOT_C1 = math.sqrt(N1 / (N1 - 1.0))
 ROOT_C2 = math.sqrt(N2 / (N2 - 1.0))
 MAGIC = 0x5F3759DF >> 7
-LATE_EXP = 20
-LATE_MAX = 8
+LATE_EXP = 12
+GROUPS = ((0, 8), (8, 16), (16, 24), (24, 28), (28, 32))
+SW = 40
 
 
 def s_cols(b):
-    if b < NB - LATE_EXP:
-        return 128
-    if b < NB - LATE_MAX:
-        return 232
-    return 152
-SW = 28
+    return 128 if b < NB - LATE_EXP else 288
+
+
+def group_of(b):
+    return b // 8 if b < 24 else 3 + (b - 24) // 4
+
+
+def s2_place(q):
+    return ((2, 32), (2, 36), (3, 16), (4, 16), (5, 0), (5, 4), (5, 8), (5, 12))[q]
 
 FLOPS = 2 * NB * ND * (2 * NI * NJ * NW + NW * NJ * NW)
 
@@ -48,8 +52,8 @@ def tile_selfprojectiondev_pb_t_kernel(tc, x, o_xi, p_xi, rel_o_xi, out_0, out_1
         rawp = ctx.enter_context(tc.tile_pool(name="rawp", bufs=8))
         grp = ctx.enter_context(tc.tile_pool(name="grp", bufs=3))
         xq = ctx.enter_context(tc.tile_pool(name="xq", bufs=3))
-        xl = ctx.enter_context(tc.tile_pool(name="xl", bufs=LATE_EXP))
-        tp = ctx.enter_context(tc.tile_pool(name="tp", bufs=12))
+        xl = ctx.enter_context(tc.tile_pool(name="xl", bufs=LATE_EXP // 2))
+        tp = ctx.enter_context(tc.tile_pool(name="tp", bufs=15))
         junk = ctx.enter_context(tc.tile_pool(name="junk", bufs=2))
         small = ctx.enter_context(tc.tile_pool(name="small", bufs=3))
         tq = ctx.enter_context(tc.tile_pool(name="tq", bufs=2))
@@ -154,44 +158,55 @@ def tile_selfprojectiondev_pb_t_kernel(tc, x, o_xi, p_xi, rel_o_xi, out_0, out_1
                 if done[0] < upto:
                     small_step()
 
+        def grouped_of(g):
+            if ("grouped", g) not in state:
+                state[("grouped", g)] = grp.tile([P, 2, NJ, 4], BF16, align_bytes=64, name="grouped")
+            return state[("grouped", g)]
+
         def regroup_s(b):
-            grouped = grp.tile([P, NJ, 4], BF16, align_bytes=64, name="grouped")
-            state[("grouped", b)] = grouped
-            src = raws[b // 2][:, b % 2]
+            grouped = grouped_of(b // 2)
             jv = NJ - s_cols(b)
             nc.scalar.copy(
-                out=grouped[:, jv:NJ, :].rearrange("p (c i) t -> p c t i", i=4),
-                in_=src[:, :, jv:NJ].rearrange("p t (c i) -> p c t i", i=4),
+                out=grouped[:, b % 2, jv:NJ, :].rearrange("p (c i) t -> p c t i", i=4),
+                in_=raws[b // 2][:, b % 2, :, jv:NJ].rearrange("p t (c i) -> p c t i", i=4),
             )
 
-        def regroup_v(b):
-            grouped = state[("grouped", b)]
-            src = raws[b // 2][:, b % 2]
-            jv = NJ - s_cols(b)
-            nc.vector.tensor_copy(
-                out=grouped[:, 0:jv, :].rearrange("p (c i) t -> p c t i", i=4),
-                in_=src[:, :, 0:jv].rearrange("p t (c i) -> p c t i", i=4),
-            )
-            small_step()
+        def regroup_v(g, split):
+            grouped = grouped_of(g)
+            jv = NJ - s_cols(2 * g)
+            if split:
+                for bb in range(2):
+                    nc.vector.tensor_copy(
+                        out=grouped[:, bb, 0:jv, :].rearrange("p (c i) t -> p c t i", i=4),
+                        in_=raws[g][:, bb, :, 0:jv].rearrange("p t (c i) -> p c t i", i=4),
+                    )
+                    small_step()
+            else:
+                nc.vector.tensor_copy(
+                    out=grouped[:, :, 0:jv, :].rearrange("p b (c i) t -> p b c t i", i=4),
+                    in_=raws[g][:, :, :, 0:jv].rearrange("p b t (c i) -> p b c t i", i=4),
+                )
+                small_step()
 
-        def quant_x(b):
-            grouped = state[("grouped", b)]
-            pool = xl if b >= NB - LATE_EXP else xq
-            codes = pool.tile([P, NJ], U32, align_bytes=64, name="codes")
-            plane = pool.tile([P, NJ], U8, align_bytes=64, name="plane")
+        def quant_x(g):
+            grouped = grouped_of(g)
+            pool = xl if 2 * g >= NB - LATE_EXP else xq
+            codes = pool.tile([P, 2 * NJ], U32, align_bytes=64, name="codes")
+            plane = pool.tile([P, 2 * NJ], U8, align_bytes=64, name="plane")
             nc.vector.quantize_mx(
                 out=codes[:].bitcast(FP8X4),
                 scales=plane[:],
-                in_=grouped[:].rearrange("p j t -> p (j t)"),
+                in_=grouped[:].rearrange("p b j t -> p (b j t)"),
             )
-            state[("xq", b)] = (codes, plane)
+            state[("xq", g)] = (codes, plane)
             small_step()
 
         def mm_z(b):
-            codes, plane = state[("xq", b)]
+            codes, plane = state[("xq", b // 2)]
+            off = (b % 2) * NJ
             z_ps = pz.tile([P, 4, ND, NW], F32, name="z_ps")
             for jt in range(4):
-                cols = slice(jt * P, (jt + 1) * P)
+                cols = slice(off + jt * P, off + (jt + 1) * P)
                 nc.tensor.matmul_mx(
                     out=z_ps[:, jt].rearrange("p d c -> p (d c)"),
                     lhsT=codes[:, cols].bitcast(FP8X4),
@@ -204,14 +219,15 @@ def tile_selfprojectiondev_pb_t_kernel(tc, x, o_xi, p_xi, rel_o_xi, out_0, out_1
             state[("z_ps", b)] = z_ps
 
         def mm_r(b):
-            codes, plane = state[("xq", b)]
+            codes, plane = state[("xq", b // 2)]
+            cols = slice((b % 2) * NJ, (b % 2 + 1) * NJ)
             r_ps = pr.tile([P, NJ], F32, name="r_ps")
             nc.tensor.matmul_mx(
                 out=r_ps[:],
                 lhsT=w_codes[:, P : 2 * P].bitcast(FP8X4),
                 lhsT_scale=w_plane[:, P : 2 * P],
-                rhs=codes[:].bitcast(FP8X4),
-                rhs_scale=plane[:],
+                rhs=codes[:, cols].bitcast(FP8X4),
+                rhs_scale=plane[:, cols],
                 start=True,
                 stop=True,
             )
@@ -226,12 +242,13 @@ def tile_selfprojectiondev_pb_t_kernel(tc, x, o_xi, p_xi, rel_o_xi, out_0, out_1
 
         def tanh1(b):
             z_ps = state[("z_ps", b)]
-            if b % 4 == 0:
-                state[("acc", b // 4)] = small.tile([P, 2, 4 * ND], F32, name="acc")
-            acc = state[("acc", b // 4)]
+            grp_k = group_of(b)
+            if b == GROUPS[grp_k][0]:
+                state[("acc", grp_k)] = small.tile([P, 2, 8 * ND], F32, name="acc")
+            acc = state[("acc", grp_k)]
             t_raw = tp.tile([P, ND, NW, 4], F32, name="t_raw")
             for d in range(ND):
-                k = (b % 4) * ND + d
+                k = (b - GROUPS[grp_k][0]) * ND + d
                 nc.scalar.activation(
                     out=t_raw[:, d],
                     in_=z_ps[:, :, d, :].rearrange("p t c -> p c t"),
@@ -241,10 +258,11 @@ def tile_selfprojectiondev_pb_t_kernel(tc, x, o_xi, p_xi, rel_o_xi, out_0, out_1
             state[("t_raw", b)] = t_raw
 
         def square1(b):
-            acc = state[("acc", b // 4)]
+            grp_k = group_of(b)
+            acc = state[("acc", grp_k)]
             t_raw = state[("t_raw", b)]
             for d in range(ND):
-                k = (b % 4) * ND + d
+                k = (b - GROUPS[grp_k][0]) * ND + d
                 sq = junk.tile([P, P], BF16, name="sq")
                 nc.scalar.activation(
                     out=sq[:],
@@ -319,7 +337,8 @@ def tile_selfprojectiondev_pb_t_kernel(tc, x, o_xi, p_xi, rel_o_xi, out_0, out_1
             state[("st", c)] = (mom, rstd, len(pending))
 
         def affine(b):
-            mom, rstd, end = state[("st", b // 4)]
+            grp_k = group_of(b)
+            mom, rstd, end = state[("st", grp_k)]
             flush(end)
             if b % 4 == 0:
                 state[("tg", b // 4)] = (
@@ -330,7 +349,7 @@ def tile_selfprojectiondev_pb_t_kernel(tc, x, o_xi, p_xi, rel_o_xi, out_0, out_1
             tg, t_codes, t_plane = state[("tg", b // 4)]
             t_raw = state[("t_raw", b)]
             for d in range(ND):
-                k = (b % 4) * ND + d
+                k = (b - GROUPS[grp_k][0]) * ND + d
                 nc.vector.tensor_scalar(
                     out=tg[:, b % 4, d, :],
                     in0=t_raw[:, d].rearrange("p c t -> p (c t)"),
@@ -341,14 +360,12 @@ def tile_selfprojectiondev_pb_t_kernel(tc, x, o_xi, p_xi, rel_o_xi, out_0, out_1
                 )
                 small_step()
 
-        def quant_t(h):
-            tg, t_codes, t_plane = state[("tg", h // 2)]
-            lo = (h % 2) * 2
-            cols = slice(lo * P, (lo + 2) * P)
+        def quant_t(q):
+            tg, t_codes, t_plane = state[("tg", q)]
             nc.vector.quantize_mx(
-                out=t_codes[:, cols].bitcast(FP8X4),
-                scales=t_plane[:, cols],
-                in_=tg[:, lo : lo + 2].rearrange("p b d e -> p (b d e)"),
+                out=t_codes[:].bitcast(FP8X4),
+                scales=t_plane[:],
+                in_=tg[:].rearrange("p b d e -> p (b d e)"),
             )
             small_step()
 
@@ -376,11 +393,6 @@ def tile_selfprojectiondev_pb_t_kernel(tc, x, o_xi, p_xi, rel_o_xi, out_0, out_1
             nc.scalar.activation(out=usq[:], in_=u_all[:, bs, :], func=ACT.Square, scale=ROOT_C2)
             state[("usq", q)] = usq
 
-        def s2_place(q):
-            if q <= 4:
-                return q + 3, 16
-            return 8, 16 + 4 * (q - 5)
-
         def s2_sums(q):
             bs = slice(4 * q, 4 * q + 4)
             usq = state[("usq", q)]
@@ -392,21 +404,22 @@ def tile_selfprojectiondev_pb_t_kernel(tc, x, o_xi, p_xi, rel_o_xi, out_0, out_1
             c, lo = s2_place(q)
             moments_mm(c, lo, lo + 4, st2[:, 0, :], st2[:, 1, :], blk2, blk2s)
 
-        def s2_out(q):
-            bs = slice(4 * q, 4 * q + 4)
-            c, lo = s2_place(q)
+        def s2_out(q0, q1):
+            n = 4 * (q1 - q0)
+            bs = slice(4 * q0, 4 * q1)
+            c, lo = s2_place(q0)
             mom, rstd, end = state[("st", c)]
             flush(end)
-            cen = fin.tile([P, 4, NW], F32, name="cen")
+            cen = fin.tile([P, n, NW], F32, name="cen")
             nc.vector.tensor_tensor(
                 out=cen[:], in0=u_all[:, bs, :],
-                in1=mom[:, 0, lo : lo + 4].unsqueeze(2).to_broadcast([P, 4, NW]), op=ALU.subtract,
+                in1=mom[:, 0, lo : lo + n].unsqueeze(2).to_broadcast([P, n, NW]), op=ALU.subtract,
             )
             small_step()
-            res = fin.tile([P, 4, NW], F32, name="res")
+            res = fin.tile([P, n, NW], F32, name="res")
             nc.vector.tensor_tensor(
                 out=res[:], in0=cen[:],
-                in1=rstd[:, lo : lo + 4].unsqueeze(2).to_broadcast([P, 4, NW]), op=ALU.mult,
+                in1=rstd[:, lo : lo + n].unsqueeze(2).to_broadcast([P, n, NW]), op=ALU.mult,
             )
             small_step()
             nc.sync.dma_start(out=out_0[bs].rearrange("b d q c -> (d q) b c"), in_=res[:])
@@ -450,61 +463,89 @@ def tile_selfprojectiondev_pb_t_kernel(tc, x, o_xi, p_xi, rel_o_xi, out_0, out_1
         def on(v, step=1, rem=0):
             return 0 <= v < NB and v % step == rem
 
-        late_at = {NB + 1: 3, NB + 2: 3, NB + 3: 3, NB + 4: 2, NB + 5: 2, NB + 6: 2, NB + 7: 1, NB + 8: 2, NB + 9: 2}
+        group_end = {}
+        for k in range(len(GROUPS)):
+            group_end[GROUPS[k][1]] = k
+        chain_cols = (32, 32, 40, 20, 20, 16)
         late_next = [NB - LATE_EXP]
 
-        for i in range(-2, NB + 12):
+        def late(count):
+            for n in range(count):
+                b = late_next[0]
+                late_next[0] = b + 1
+                mm_r(b)
+                exp1(b)
+
+        def unit(q, count):
+            quant_t(q)
+            s2_mm(q)
+            s2_tanh(q)
+            late(count)
+
+        regroup_s(0)
+        regroup_s(1)
+        regroup_v(0, True)
+        regroup_s(2)
+        regroup_s(3)
+        for i in range(-2, NB):
             if on(i - 1) and i - 1 < NB - LATE_EXP:
                 exp1(i - 1)
-            if on(i - 13, 4, 0):
-                s2_tanh((i - 13) // 4)
-            if on(i + 2):
-                regroup_s(i + 2)
-            if on(i - 5, 4, 0):
-                c = (i - 5) // 4
-                chain(c, 0, 20 if c >= 3 else 16)
+            if on(i - 17, 4, 0):
+                s2_tanh((i - 17) // 4)
+            if on(i + 4) and i >= 0:
+                regroup_s(i + 4)
+            if i - 1 in group_end and i - 1 < NB:
+                chain(group_end[i - 1], 0, chain_cols[group_end[i - 1]])
+            if i % 2 == 0 and on(i + 2):
+                quant_x((i + 2) // 2)
             if on(i + 1):
-                quant_x(i + 1)
                 mm_z(i + 1)
-                if i + 1 < NB - LATE_MAX:
-                    mm_r(i + 1)
-            if on(i) and i < NB - LATE_MAX:
-                row_max(i)
+                mm_r(i + 1)
             if on(i):
+                row_max(i)
                 tanh1(i)
-            if on(i + 2):
-                regroup_v(i + 2)
+            if i % 2 == 1 and on(i + 3):
+                regroup_v((i + 3) // 2, False)
             if i == 1:
                 prep_p_copy()
             if on(i):
                 square1(i)
-                if i % 4 == 3:
-                    acc = state[("acc", i // 4)]
-                    moments_mm(i // 4, 0, 16, acc[:, 0, :], acc[:, 1, :], ones1, ones1s)
-            if on(i - 10, 2, 0):
-                quant_t((i - 10) // 2)
-                if (i - 10) % 4 == 2:
-                    s2_mm((i - 12) // 4)
+                if i + 1 in group_end:
+                    k = group_end[i + 1]
+                    n1 = ND * (GROUPS[k][1] - GROUPS[k][0])
+                    acc = state[("acc", k)]
+                    moments_mm(k, 0, n1, acc[:, 0, 0:n1], acc[:, 1, 0:n1], ones1, ones1s)
+            if on(i - 16, 4, 0):
+                quant_t((i - 16) // 4)
+                s2_mm((i - 16) // 4)
             if i == 2:
                 prep_p_quant()
-            if on(i - 8):
-                affine(i - 8)
-            if on(i - 14, 4, 0):
-                s2_sums((i - 14) // 4)
-            if on(i - 20, 4, 0) and (i - 20) // 4 <= 4:
-                s2_out((i - 20) // 4)
-            for n in range(late_at.get(i, 0)):
-                b = late_next[0]
-                late_next[0] = b + 1
-                mm_r(b)
-                if b >= NB - LATE_MAX:
-                    row_max(b)
-                exp1(b)
-            if i == NB + 11:
-                chain(8, 16, 28)
-                flush(done[0] + 8)
-                mass()
-                for q in range(5, 8):
-                    s2_out(q)
+            if on(i - 12):
+                affine(i - 12)
+            if on(i - 18, 4, 0):
+                s2_sums((i - 18) // 4)
+            if i == 28:
+                s2_out(0, 2)
+
+        chain(4, 0, chain_cols[4])
+        unit(4, 5)
+        for b in range(20, 24):
+            affine(b)
+        s2_out(2, 3)
+        unit(5, 4)
+        for b in range(24, 28):
+            affine(b)
+        s2_sums(4)
+        unit(6, 3)
+        for b in range(28, 32):
+            affine(b)
+        s2_sums(5)
+        unit(7, 0)
+        s2_out(3, 4)
+        s2_sums(6)
+        mass()
+        s2_sums(7)
+        chain(5, 0, chain_cols[5])
+        s2_out(4, 8)
         assert late_next[0] == NB
         assert done[0] == len(pending)

@@ -26,21 +26,12 @@ N2 = NW * NW
 ROOT_C1 = math.sqrt(N1 / (N1 - 1.0))
 ROOT_C2 = math.sqrt(N2 / (N2 - 1.0))
 MAGIC = 0x5F3759DF >> 7
-LATE_EXP = 12
-GROUPS = ((0, 8), (8, 16), (16, 24), (24, 28), (28, 32))
-SW = 40
+LATE_EXP = 16
 
 
 def s_cols(b):
-    return 128 if b < NB - LATE_EXP else 288
-
-
-def group_of(b):
-    return b // 8 if b < 24 else 3 + (b - 24) // 4
-
-
-def s2_place(q):
-    return ((2, 32), (2, 36), (3, 16), (4, 16), (5, 0), (5, 4), (5, 8), (5, 12))[q]
+    return 128 if b < NB - LATE_EXP else 232
+SW = 28
 
 FLOPS = 2 * NB * ND * (2 * NI * NJ * NW + NW * NJ * NW)
 
@@ -52,8 +43,8 @@ def tile_selfprojectiondev_pb_t_kernel(tc, x, o_xi, p_xi, rel_o_xi, out_0, out_1
         rawp = ctx.enter_context(tc.tile_pool(name="rawp", bufs=8))
         grp = ctx.enter_context(tc.tile_pool(name="grp", bufs=3))
         xq = ctx.enter_context(tc.tile_pool(name="xq", bufs=3))
-        xl = ctx.enter_context(tc.tile_pool(name="xl", bufs=LATE_EXP // 2))
-        tp = ctx.enter_context(tc.tile_pool(name="tp", bufs=15))
+        xl = ctx.enter_context(tc.tile_pool(name="xl", bufs=LATE_EXP))
+        tp = ctx.enter_context(tc.tile_pool(name="tp", bufs=12))
         junk = ctx.enter_context(tc.tile_pool(name="junk", bufs=2))
         small = ctx.enter_context(tc.tile_pool(name="small", bufs=3))
         tq = ctx.enter_context(tc.tile_pool(name="tq", bufs=2))
@@ -158,55 +149,44 @@ def tile_selfprojectiondev_pb_t_kernel(tc, x, o_xi, p_xi, rel_o_xi, out_0, out_1
                 if done[0] < upto:
                     small_step()
 
-        def grouped_of(g):
-            if ("grouped", g) not in state:
-                state[("grouped", g)] = grp.tile([P, 2, NJ, 4], BF16, align_bytes=64, name="grouped")
-            return state[("grouped", g)]
-
         def regroup_s(b):
-            grouped = grouped_of(b // 2)
+            grouped = grp.tile([P, NJ, 4], BF16, align_bytes=64, name="grouped")
+            state[("grouped", b)] = grouped
+            src = raws[b // 2][:, b % 2]
             jv = NJ - s_cols(b)
             nc.scalar.copy(
-                out=grouped[:, b % 2, jv:NJ, :].rearrange("p (c i) t -> p c t i", i=4),
-                in_=raws[b // 2][:, b % 2, :, jv:NJ].rearrange("p t (c i) -> p c t i", i=4),
+                out=grouped[:, jv:NJ, :].rearrange("p (c i) t -> p c t i", i=4),
+                in_=src[:, :, jv:NJ].rearrange("p t (c i) -> p c t i", i=4),
             )
 
-        def regroup_v(g, split):
-            grouped = grouped_of(g)
-            jv = NJ - s_cols(2 * g)
-            if split:
-                for bb in range(2):
-                    nc.vector.tensor_copy(
-                        out=grouped[:, bb, 0:jv, :].rearrange("p (c i) t -> p c t i", i=4),
-                        in_=raws[g][:, bb, :, 0:jv].rearrange("p t (c i) -> p c t i", i=4),
-                    )
-                    small_step()
-            else:
-                nc.vector.tensor_copy(
-                    out=grouped[:, :, 0:jv, :].rearrange("p b (c i) t -> p b c t i", i=4),
-                    in_=raws[g][:, :, :, 0:jv].rearrange("p b t (c i) -> p b c t i", i=4),
-                )
-                small_step()
+        def regroup_v(b):
+            grouped = state[("grouped", b)]
+            src = raws[b // 2][:, b % 2]
+            jv = NJ - s_cols(b)
+            nc.vector.tensor_copy(
+                out=grouped[:, 0:jv, :].rearrange("p (c i) t -> p c t i", i=4),
+                in_=src[:, :, 0:jv].rearrange("p t (c i) -> p c t i", i=4),
+            )
+            small_step()
 
-        def quant_x(g):
-            grouped = grouped_of(g)
-            pool = xl if 2 * g >= NB - LATE_EXP else xq
-            codes = pool.tile([P, 2 * NJ], U32, align_bytes=64, name="codes")
-            plane = pool.tile([P, 2 * NJ], U8, align_bytes=64, name="plane")
+        def quant_x(b):
+            grouped = state[("grouped", b)]
+            pool = xl if b >= NB - LATE_EXP else xq
+            codes = pool.tile([P, NJ], U32, align_bytes=64, name="codes")
+            plane = pool.tile([P, NJ], U8, align_bytes=64, name="plane")
             nc.vector.quantize_mx(
                 out=codes[:].bitcast(FP8X4),
                 scales=plane[:],
-                in_=grouped[:].rearrange("p b j t -> p (b j t)"),
+                in_=grouped[:].rearrange("p j t -> p (j t)"),
             )
-            state[("xq", g)] = (codes, plane)
+            state[("xq", b)] = (codes, plane)
             small_step()
 
         def mm_z(b):
-            codes, plane = state[("xq", b // 2)]
-            off = (b % 2) * NJ
+            codes, plane = state[("xq", b)]
             z_ps = pz.tile([P, 4, ND, NW], F32, name="z_ps")
             for jt in range(4):
-                cols = slice(off + jt * P, off + (jt + 1) * P)
+                cols = slice(jt * P, (jt + 1) * P)
                 nc.tensor.matmul_mx(
                     out=z_ps[:, jt].rearrange("p d c -> p (d c)"),
                     lhsT=codes[:, cols].bitcast(FP8X4),
@@ -219,15 +199,14 @@ def tile_selfprojectiondev_pb_t_kernel(tc, x, o_xi, p_xi, rel_o_xi, out_0, out_1
             state[("z_ps", b)] = z_ps
 
         def mm_r(b):
-            codes, plane = state[("xq", b // 2)]
-            cols = slice((b % 2) * NJ, (b % 2 + 1) * NJ)
-            r_ps = pr.tile([P, NJ], F32, name="r_ps")
+            codes, plane = state[("xq", b)]
+            r_ps = pr.tile([P, NJ], F32, name="r_ps", tag="r_ps")
             nc.tensor.matmul_mx(
                 out=r_ps[:],
                 lhsT=w_codes[:, P : 2 * P].bitcast(FP8X4),
                 lhsT_scale=w_plane[:, P : 2 * P],
-                rhs=codes[:, cols].bitcast(FP8X4),
-                rhs_scale=plane[:, cols],
+                rhs=codes[:].bitcast(FP8X4),
+                rhs_scale=plane[:],
                 start=True,
                 stop=True,
             )
@@ -242,13 +221,12 @@ def tile_selfprojectiondev_pb_t_kernel(tc, x, o_xi, p_xi, rel_o_xi, out_0, out_1
 
         def tanh1(b):
             z_ps = state[("z_ps", b)]
-            grp_k = group_of(b)
-            if b == GROUPS[grp_k][0]:
-                state[("acc", grp_k)] = small.tile([P, 2, 8 * ND], F32, name="acc")
-            acc = state[("acc", grp_k)]
+            if b % 4 == 0:
+                state[("acc", b // 4)] = small.tile([P, 2, 4 * ND], F32, name="acc")
+            acc = state[("acc", b // 4)]
             t_raw = tp.tile([P, ND, NW, 4], F32, name="t_raw")
             for d in range(ND):
-                k = (b - GROUPS[grp_k][0]) * ND + d
+                k = (b % 4) * ND + d
                 nc.scalar.activation(
                     out=t_raw[:, d],
                     in_=z_ps[:, :, d, :].rearrange("p t c -> p c t"),
@@ -258,11 +236,10 @@ def tile_selfprojectiondev_pb_t_kernel(tc, x, o_xi, p_xi, rel_o_xi, out_0, out_1
             state[("t_raw", b)] = t_raw
 
         def square1(b):
-            grp_k = group_of(b)
-            acc = state[("acc", grp_k)]
+            acc = state[("acc", b // 4)]
             t_raw = state[("t_raw", b)]
             for d in range(ND):
-                k = (b - GROUPS[grp_k][0]) * ND + d
+                k = (b % 4) * ND + d
                 sq = junk.tile([P, P], BF16, name="sq")
                 nc.scalar.activation(
                     out=sq[:],
@@ -336,9 +313,28 @@ def tile_selfprojectiondev_pb_t_kernel(tc, x, o_xi, p_xi, rel_o_xi, out_0, out_1
             pending.extend(ops)
             state[("st", c)] = (mom, rstd, len(pending))
 
+        def last_stats_a(c, lo, hi):
+            mom_ps = mom_tile(c)
+            cs = slice(lo, hi)
+            mom = small.tile([P, 3, SW], F32, name="mom")
+            var = small.tile([P, SW], F32, name="var")
+            tmp = small.tile([P, SW], F32, name="tmp")
+            rstd = small.tile([P, SW], F32, name="rstd")
+            nc.vector.tensor_copy(out=mom[:, :, cs], in_=mom_ps[:, :, cs])
+            nc.vector.tensor_tensor(out=tmp[:, cs], in0=mom[:, 2, cs], in1=mom[:, 2, cs], op=ALU.mult)
+            nc.vector.tensor_tensor(out=var[:, cs], in0=mom[:, 1, cs], in1=tmp[:, cs], op=ALU.subtract)
+            nc.vector.tensor_scalar(out=var[:, cs], in0=var[:, cs], scalar1=1e-30, scalar2=None, op0=ALU.max)
+            nc.scalar.activation(out=tmp[:, cs], in_=var[:, cs], func=ACT.Sqrt)
+            state[("st", c)] = (mom, rstd, len(pending))
+            state["last"] = (tmp, rstd, cs)
+
+        def last_stats_b():
+            tmp, rstd, cs = state["last"]
+            nc.vector.tensor_scalar(out=tmp[:, cs], in0=tmp[:, cs], scalar1=EPS, scalar2=None, op0=ALU.add)
+            nc.vector.reciprocal(out=rstd[:, cs], in_=tmp[:, cs])
+
         def affine(b):
-            grp_k = group_of(b)
-            mom, rstd, end = state[("st", grp_k)]
+            mom, rstd, end = state[("st", b // 4)]
             flush(end)
             if b % 4 == 0:
                 state[("tg", b // 4)] = (
@@ -349,7 +345,7 @@ def tile_selfprojectiondev_pb_t_kernel(tc, x, o_xi, p_xi, rel_o_xi, out_0, out_1
             tg, t_codes, t_plane = state[("tg", b // 4)]
             t_raw = state[("t_raw", b)]
             for d in range(ND):
-                k = (b - GROUPS[grp_k][0]) * ND + d
+                k = (b % 4) * ND + d
                 nc.vector.tensor_scalar(
                     out=tg[:, b % 4, d, :],
                     in0=t_raw[:, d].rearrange("p c t -> p (c t)"),
@@ -393,6 +389,11 @@ def tile_selfprojectiondev_pb_t_kernel(tc, x, o_xi, p_xi, rel_o_xi, out_0, out_1
             nc.scalar.activation(out=usq[:], in_=u_all[:, bs, :], func=ACT.Square, scale=ROOT_C2)
             state[("usq", q)] = usq
 
+        def s2_place(q):
+            if q <= 4:
+                return q + 3, 16
+            return 8, 16 + 4 * (q - 5)
+
         def s2_sums(q):
             bs = slice(4 * q, 4 * q + 4)
             usq = state[("usq", q)]
@@ -404,32 +405,29 @@ def tile_selfprojectiondev_pb_t_kernel(tc, x, o_xi, p_xi, rel_o_xi, out_0, out_1
             c, lo = s2_place(q)
             moments_mm(c, lo, lo + 4, st2[:, 0, :], st2[:, 1, :], blk2, blk2s)
 
-        def s2_out(q0, q1):
-            n = 4 * (q1 - q0)
-            bs = slice(4 * q0, 4 * q1)
-            c, lo = s2_place(q0)
+        def s2_out(q):
+            bs = slice(4 * q, 4 * q + 4)
+            c, lo = s2_place(q)
             mom, rstd, end = state[("st", c)]
             flush(end)
-            cen = fin.tile([P, n, NW], F32, name="cen")
+            cen = fin.tile([P, 4, NW], F32, name="cen")
             nc.vector.tensor_tensor(
                 out=cen[:], in0=u_all[:, bs, :],
-                in1=mom[:, 0, lo : lo + n].unsqueeze(2).to_broadcast([P, n, NW]), op=ALU.subtract,
+                in1=mom[:, 0, lo : lo + 4].unsqueeze(2).to_broadcast([P, 4, NW]), op=ALU.subtract,
             )
             small_step()
-            res = fin.tile([P, n, NW], F32, name="res")
+            res = fin.tile([P, 4, NW], F32, name="res")
             nc.vector.tensor_tensor(
                 out=res[:], in0=cen[:],
-                in1=rstd[:, lo : lo + n].unsqueeze(2).to_broadcast([P, n, NW]), op=ALU.mult,
+                in1=rstd[:, lo : lo + 4].unsqueeze(2).to_broadcast([P, 4, NW]), op=ALU.mult,
             )
             small_step()
             nc.sync.dma_start(out=out_0[bs].rearrange("b d q c -> (d q) b c"), in_=res[:])
 
-        def mass():
-            tr_ps = pu.tile([P, 2, P], F32, name="tr_ps", tag="u_ps")
-            nc.tensor.transpose(out=tr_ps[:, 0, :], in_=nm[:], identity=ident[:])
-            nc.tensor.transpose(out=tr_ps[:, 1, :], in_=se[:], identity=ident[:])
-            nmt = tr_ps[0:NB, 0, :].rearrange("b (d c) -> b d c", d=ND)
-            set_ = tr_ps[0:NB, 1, :].rearrange("b (d c) -> b d c", d=ND)
+        def mass_a():
+            nm_ps = pr.tile([P, P], F32, name="nm_ps", tag="r_ps")
+            nc.tensor.transpose(out=nm_ps[:], in_=nm[:], identity=ident[:])
+            nmt = nm_ps[0:NB, :].rearrange("b (d c) -> b d c", d=ND)
             ntop = fin.tile([NB, ND], F32, name="ntop")
             nc.vector.tensor_reduce(out=ntop[:], in_=nmt, axis=AX.X, op=ALU.min)
             small_step()
@@ -441,32 +439,33 @@ def tile_selfprojectiondev_pb_t_kernel(tc, x, o_xi, p_xi, rel_o_xi, out_0, out_1
             small_step()
             corr = fin.tile([NB, ND, NW], F32, name="corr")
             nc.scalar.activation(out=corr[:], in_=diff[:], func=ACT.Exp)
-            small_step()
-            small_step()
+            state["mass"] = corr
+
+        def warm_sqrt():
+            warm = fin.tile([P, 1], F32, name="warm")
+            nc.scalar.activation(out=warm[:], in_=ones1[:, 0:1], func=ACT.Sqrt)
+
+        def mass_b():
+            corr = state["mass"]
+            se_ps = pr.tile([P, P], F32, name="se_ps", tag="r_ps")
+            nc.tensor.transpose(out=se_ps[:], in_=se[:], identity=ident[:])
+            set_ = se_ps[0:NB, :].rearrange("b (d c) -> b d c", d=ND)
             part = fin.tile([NB, ND, NW], F32, name="part")
             nc.vector.tensor_tensor(out=part[:], in0=corr[:], in1=set_, op=ALU.mult)
-            small_step()
             den = fin.tile([NB, ND], F32, name="den")
             nc.vector.tensor_reduce(out=den[:], in_=part[:], axis=AX.X, op=ALU.add)
-            small_step()
             rden = fin.tile([NB, ND], F32, name="rden")
             nc.vector.reciprocal(out=rden[:], in_=den[:])
-            small_step()
             mres = fin.tile([NB, ND, NW], F32, name="mres")
             nc.vector.tensor_tensor(
                 out=mres[:], in0=part[:],
                 in1=rden[:].unsqueeze(2).to_broadcast([NB, ND, NW]), op=ALU.mult,
             )
-            small_step()
             nc.sync.dma_start(out=out_1, in_=mres[:])
 
         def on(v, step=1, rem=0):
             return 0 <= v < NB and v % step == rem
 
-        group_end = {}
-        for k in range(len(GROUPS)):
-            group_end[GROUPS[k][1]] = k
-        chain_cols = (32, 32, 40, 20, 20, 16)
         late_next = [NB - LATE_EXP]
 
         def late(count):
@@ -476,76 +475,72 @@ def tile_selfprojectiondev_pb_t_kernel(tc, x, o_xi, p_xi, rel_o_xi, out_0, out_1
                 mm_r(b)
                 exp1(b)
 
-        def unit(q, count):
-            quant_t(q)
-            s2_mm(q)
-            s2_tanh(q)
-            late(count)
-
-        regroup_s(0)
-        regroup_s(1)
-        regroup_v(0, True)
-        regroup_s(2)
-        regroup_s(3)
         for i in range(-2, NB):
             if on(i - 1) and i - 1 < NB - LATE_EXP:
                 exp1(i - 1)
-            if on(i - 17, 4, 0):
-                s2_tanh((i - 17) // 4)
-            if on(i + 4) and i >= 0:
-                regroup_s(i + 4)
-            if i - 1 in group_end and i - 1 < NB:
-                chain(group_end[i - 1], 0, chain_cols[group_end[i - 1]])
-            if i % 2 == 0 and on(i + 2):
-                quant_x((i + 2) // 2)
+            if on(i - 13, 4, 0):
+                s2_tanh((i - 13) // 4)
+            if on(i + 2):
+                regroup_s(i + 2)
+            if on(i - 5, 4, 0):
+                c = (i - 5) // 4
+                chain(c, 0, 20 if c >= 3 else 16)
             if on(i + 1):
+                quant_x(i + 1)
                 mm_z(i + 1)
                 mm_r(i + 1)
             if on(i):
                 row_max(i)
                 tanh1(i)
-            if i % 2 == 1 and on(i + 3):
-                regroup_v((i + 3) // 2, False)
+            if on(i + 2):
+                regroup_v(i + 2)
             if i == 1:
                 prep_p_copy()
             if on(i):
                 square1(i)
-                if i + 1 in group_end:
-                    k = group_end[i + 1]
-                    n1 = ND * (GROUPS[k][1] - GROUPS[k][0])
-                    acc = state[("acc", k)]
-                    moments_mm(k, 0, n1, acc[:, 0, 0:n1], acc[:, 1, 0:n1], ones1, ones1s)
-            if on(i - 16, 4, 0):
-                quant_t((i - 16) // 4)
-                s2_mm((i - 16) // 4)
+                if i % 4 == 3:
+                    acc = state[("acc", i // 4)]
+                    moments_mm(i // 4, 0, 16, acc[:, 0, :], acc[:, 1, :], ones1, ones1s)
+            if on(i - 12, 4, 0):
+                quant_t((i - 12) // 4)
+                s2_mm((i - 12) // 4)
             if i == 2:
                 prep_p_quant()
-            if on(i - 12):
-                affine(i - 12)
-            if on(i - 18, 4, 0):
-                s2_sums((i - 18) // 4)
-            if i == 28:
-                s2_out(0, 2)
+            if on(i - 8):
+                affine(i - 8)
+            if on(i - 14, 4, 0):
+                s2_sums((i - 14) // 4)
+            if on(i - 20, 4, 0):
+                s2_out((i - 20) // 4)
 
-        chain(4, 0, chain_cols[4])
-        unit(4, 5)
-        for b in range(20, 24):
-            affine(b)
-        s2_out(2, 3)
-        unit(5, 4)
+        quant_t(5)
+        s2_mm(5)
+        chain(7, 0, 20)
+        mass_a()
+        s2_tanh(5)
+        late(8)
         for b in range(24, 28):
             affine(b)
-        s2_sums(4)
-        unit(6, 3)
+        s2_out(3)
+        quant_t(6)
+        s2_mm(6)
+        s2_tanh(6)
+        late(8)
         for b in range(28, 32):
             affine(b)
         s2_sums(5)
-        unit(7, 0)
-        s2_out(3, 4)
+        quant_t(7)
+        s2_mm(7)
+        s2_tanh(7)
+        warm_sqrt()
+        s2_out(4)
         s2_sums(6)
-        mass()
         s2_sums(7)
-        chain(5, 0, chain_cols[5])
-        s2_out(4, 8)
+        last_stats_a(8, 16, 28)
+        mass_b()
+        last_stats_b()
+        s2_out(7)
+        s2_out(5)
+        s2_out(6)
         assert late_next[0] == NB
         assert done[0] == len(pending)

@@ -41,8 +41,8 @@ def tile_selfprojectiondev_pb_t_kernel(tc, x, o_xi, p_xi, rel_o_xi, out_0, out_1
     with ExitStack() as ctx:
         const = ctx.enter_context(tc.tile_pool(name="const", bufs=1))
         rawp = ctx.enter_context(tc.tile_pool(name="rawp", bufs=8))
-        grp = ctx.enter_context(tc.tile_pool(name="grp", bufs=3))
-        xq = ctx.enter_context(tc.tile_pool(name="xq", bufs=3))
+        grp = ctx.enter_context(tc.tile_pool(name="grp", bufs=4))
+        xq = ctx.enter_context(tc.tile_pool(name="xq", bufs=4))
         xl = ctx.enter_context(tc.tile_pool(name="xl", bufs=LATE_EXP))
         tp = ctx.enter_context(tc.tile_pool(name="tp", bufs=12))
         junk = ctx.enter_context(tc.tile_pool(name="junk", bufs=2))
@@ -475,25 +475,26 @@ def tile_selfprojectiondev_pb_t_kernel(tc, x, o_xi, p_xi, rel_o_xi, out_0, out_1
                 mm_r(b)
                 exp1(b)
 
-        for i in range(-2, NB):
+        for i in range(-4, NB):
             if on(i - 1) and i - 1 < NB - LATE_EXP:
                 exp1(i - 1)
             if on(i - 13, 4, 0):
                 s2_tanh((i - 13) // 4)
-            if on(i + 2):
-                regroup_s(i + 2)
+            if on(i + 4):
+                regroup_s(i + 4)
             if on(i - 5, 4, 0):
                 c = (i - 5) // 4
                 chain(c, 0, 20 if c >= 3 else 16)
+            if on(i + 2):
+                quant_x(i + 2)
             if on(i + 1):
-                quant_x(i + 1)
                 mm_z(i + 1)
                 mm_r(i + 1)
             if on(i):
                 row_max(i)
                 tanh1(i)
-            if on(i + 2):
-                regroup_v(i + 2)
+            if on(i + 3):
+                regroup_v(i + 3)
             if i == 1:
                 prep_p_copy()
             if on(i):

@@ -30,7 +30,7 @@ LATE_EXP = 16
 
 
 def s_cols(b):
-    return 128 if b < NB - LATE_EXP else 232
+    return 96 if b < NB - LATE_EXP else 200
 SW = 28
 
 FLOPS = 2 * NB * ND * (2 * NI * NJ * NW + NW * NJ * NW)
@@ -41,8 +41,8 @@ def tile_selfprojectiondev_pb_t_kernel(tc, x, o_xi, p_xi, rel_o_xi, out_0, out_1
     with ExitStack() as ctx:
         const = ctx.enter_context(tc.tile_pool(name="const", bufs=1))
         rawp = ctx.enter_context(tc.tile_pool(name="rawp", bufs=8))
-        grp = ctx.enter_context(tc.tile_pool(name="grp", bufs=4))
-        xq = ctx.enter_context(tc.tile_pool(name="xq", bufs=4))
+        grp = ctx.enter_context(tc.tile_pool(name="grp", bufs=3))
+        xq = ctx.enter_context(tc.tile_pool(name="xq", bufs=3))
         xl = ctx.enter_context(tc.tile_pool(name="xl", bufs=LATE_EXP))
         tp = ctx.enter_context(tc.tile_pool(name="tp", bufs=12))
         junk = ctx.enter_context(tc.tile_pool(name="junk", bufs=2))
@@ -475,26 +475,25 @@ def tile_selfprojectiondev_pb_t_kernel(tc, x, o_xi, p_xi, rel_o_xi, out_0, out_1
                 mm_r(b)
                 exp1(b)
 
-        for i in range(-4, NB):
+        for i in range(-2, NB):
             if on(i - 1) and i - 1 < NB - LATE_EXP:
                 exp1(i - 1)
             if on(i - 13, 4, 0):
                 s2_tanh((i - 13) // 4)
-            if on(i + 4):
-                regroup_s(i + 4)
+            if on(i + 2):
+                regroup_s(i + 2)
             if on(i - 5, 4, 0):
                 c = (i - 5) // 4
                 chain(c, 0, 20 if c >= 3 else 16)
-            if on(i + 2):
-                quant_x(i + 2)
             if on(i + 1):
+                quant_x(i + 1)
                 mm_z(i + 1)
                 mm_r(i + 1)
             if on(i):
                 row_max(i)
                 tanh1(i)
-            if on(i + 3):
-                regroup_v(i + 3)
+            if on(i + 2):
+                regroup_v(i + 2)
             if i == 1:
                 prep_p_copy()
             if on(i):

@@ -23,15 +23,20 @@ ND = 4
 EPS = 1e-5
 N1 = NJ * NW
 N2 = NW * NW
-ROOT_C1 = math.sqrt(N1 / (N1 - 1.0))
-ROOT_C2 = math.sqrt(N2 / (N2 - 1.0))
-MAGIC = 0x5F3759DF >> 7
-LATE_EXP = 16
+ROOT1 = math.sqrt(N1 / (N1 - 1.0))
+ROOT2 = math.sqrt(N2 / (N2 - 1.0))
+MAGIC = float(0x5F3759DF)
+EARLY = 24
+EARLY_MAX = 29
+GROUPS = [range(0, 8), range(8, 16), range(16, 24), range(24, 28), range(28, 32)]
+UNITS = [(0, 1), (2, 3), (4, 5), (6,), (7,)]
+W = 24
 
 
 def s_cols(b):
-    return 96 if b < NB - LATE_EXP else 200
-SW = 28
+    if b < 15:
+        return 72
+    return 120 if b < EARLY + 2 else 248
 
 FLOPS = 2 * NB * ND * (2 * NI * NJ * NW + NW * NJ * NW)
 
@@ -43,18 +48,21 @@ def tile_selfprojectiondev_pb_t_kernel(tc, x, o_xi, p_xi, rel_o_xi, out_0, out_1
         rawp = ctx.enter_context(tc.tile_pool(name="rawp", bufs=8))
         grp = ctx.enter_context(tc.tile_pool(name="grp", bufs=3))
         xq = ctx.enter_context(tc.tile_pool(name="xq", bufs=3))
-        xl = ctx.enter_context(tc.tile_pool(name="xl", bufs=LATE_EXP))
-        tp = ctx.enter_context(tc.tile_pool(name="tp", bufs=12))
+        xl = ctx.enter_context(tc.tile_pool(name="xl", bufs=NB - EARLY))
+        tp = ctx.enter_context(tc.tile_pool(name="tp", bufs=18))
+        tbp = ctx.enter_context(tc.tile_pool(name="tbp", bufs=4))
         junk = ctx.enter_context(tc.tile_pool(name="junk", bufs=2))
         small = ctx.enter_context(tc.tile_pool(name="small", bufs=3))
         tq = ctx.enter_context(tc.tile_pool(name="tq", bufs=2))
         fin = ctx.enter_context(tc.tile_pool(name="fin", bufs=3))
-        pz = ctx.enter_context(tc.psum_pool(name="pz", bufs=2))
+        pz = ctx.enter_context(tc.psum_pool(name="pz", bufs=3))
         pr = ctx.enter_context(tc.psum_pool(name="pr", bufs=3))
-        pm = ctx.enter_context(tc.psum_pool(name="pm", bufs=2))
+        pm = ctx.enter_context(tc.psum_pool(name="pm", bufs=1))
         pu = ctx.enter_context(tc.psum_pool(name="pu", bufs=1))
         ctx.enter_context(tc.manual_schedule())
 
+        nm = const.tile([P, P], F32)
+        nc.gpsimd.memset(nm[:], 0.0)
         raw_w = const.tile([P, 2, ND, 4, NW], BF16)
         nc.scalar.dma_start(
             out=raw_w[:, 0].rearrange("p d t c -> p d (t c)"),
@@ -65,8 +73,13 @@ def tile_selfprojectiondev_pb_t_kernel(tc, x, o_xi, p_xi, rel_o_xi, out_0, out_1
             in_=rel_o_xi.rearrange("d (p t) c -> p d (t c)", t=4),
         )
         raw_p = const.tile([P, ND, 4, NW], BF16)
-        for d in range(ND):
-            nc.scalar.dma_start(out=raw_p[:, d], in_=p_xi[d].rearrange("(t p) q -> p t q", p=P))
+        nc.scalar.dma_start(
+            out=raw_p[:].rearrange("p d t c -> p d (t c)"),
+            in_=p_xi.rearrange("d (p t) c -> p d (t c)", t=4),
+        )
+
+        warm = const.tile([P, 1], F32)
+        nc.scalar.activation(out=warm[:], in_=nm[:, 0:1], func=ACT.Exp)
 
         raws = []
         for g in range(NB // 2):
@@ -84,68 +97,70 @@ def tile_selfprojectiondev_pb_t_kernel(tc, x, o_xi, p_xi, rel_o_xi, out_0, out_1
                 )
             raws.append(raw)
 
-        ones1 = const.tile([P, P], F32)
-        nc.gpsimd.memset(ones1[:], 1.0 / N1)
-        ones1s = const.tile([P, P], F32)
-        nc.gpsimd.memset(ones1s[:], ROOT_C1 / N1)
+        blk1 = const.tile([P, P], F32)
+        nc.gpsimd.memset(blk1[:], 0.0)
         blk2 = const.tile([P, P], F32)
         nc.gpsimd.memset(blk2[:], 0.0)
-        blk2s = const.tile([P, P], F32)
-        nc.gpsimd.memset(blk2s[:], 0.0)
         for d in range(ND):
             rows = slice(NW * d, NW * (d + 1))
+            nc.gpsimd.memset(blk1[rows, rows], 1.0 / N1)
             nc.gpsimd.memset(blk2[rows, rows], 1.0 / N2)
-            nc.gpsimd.memset(blk2s[rows, rows], ROOT_C2 / N2)
         ident = const.tile([P, P], F32)
         make_identity(nc, ident[:])
-        nm = const.tile([P, P], F32)
-        nc.gpsimd.memset(nm[:], 0.0)
         se = const.tile([P, P], F32)
         nc.gpsimd.memset(se[:], 0.0)
         u_all = const.tile([P, NB, NW], F32)
 
         gw = const.tile([P, 2, ND * NW, 4], BF16, align_bytes=64)
-        for s in range(2):
-            nc.vector.tensor_copy(
-                out=gw[:, s].rearrange("p (d c) t -> p d c t", d=ND),
-                in_=raw_w[:, s].rearrange("p d t c -> p d c t"),
-            )
-        gp = const.tile([P, ND * NW, 4], BF16, align_bytes=64)
         w_codes = const.tile([P, 2 * P], U32, align_bytes=64)
         w_plane = const.tile([P, 2 * P], U8, align_bytes=64)
-        nc.vector.quantize_mx(
-            out=w_codes[:].bitcast(FP8X4),
-            scales=w_plane[:],
-            in_=gw[:].rearrange("p s w t -> p (s w t)"),
-        )
-        p_codes = const.tile([P, P], U32, align_bytes=64)
-        p_plane = const.tile([P, P], U8, align_bytes=64)
+
+        def prep_w():
+            nc.scalar.copy(
+                out=gw[:, 0].rearrange("p (d c) t -> p d c t", d=ND),
+                in_=raw_w[:, 0].rearrange("p d t c -> p d c t"),
+            )
+            nc.vector.tensor_copy(
+                out=gw[:, 1].rearrange("p (d c) t -> p d c t", d=ND),
+                in_=raw_w[:, 1].rearrange("p d t c -> p d c t"),
+            )
+            nc.vector.quantize_mx(
+                out=w_codes[:].bitcast(FP8X4),
+                scales=w_plane[:],
+                in_=gw[:].rearrange("p s w t -> p (s w t)"),
+            )
+
+        gp = const.tile([P, ND, ND * NW, 4], BF16, align_bytes=64)
+        nc.gpsimd.memset(gp[:], 0.0)
+        p_codes = const.tile([P, ND, P], U32, align_bytes=64)
+        p_plane = const.tile([P, ND, P], U8, align_bytes=64)
 
         def prep_p_copy():
-            nc.vector.tensor_copy(
-                out=gp[:].rearrange("p (d c) t -> p d c t", d=ND),
-                in_=raw_p[:].rearrange("p d t c -> p d c t"),
-            )
+            for d in range(ND):
+                nc.vector.tensor_copy(
+                    out=gp[:, d, NW * d : NW * (d + 1), :],
+                    in_=raw_p[:, d].rearrange("p t q -> p q t"),
+                )
 
         def prep_p_quant():
             nc.vector.quantize_mx(
-                out=p_codes[:].bitcast(FP8X4),
-                scales=p_plane[:],
-                in_=gp[:].rearrange("p w t -> p (w t)"),
+                out=p_codes[:].rearrange("p d w -> p (d w)").bitcast(FP8X4),
+                scales=p_plane[:].rearrange("p d w -> p (d w)"),
+                in_=gp[:].rearrange("p d w t -> p (d w t)"),
             )
 
         state = {}
         pending = []
         done = [0]
 
-        def small_step():
-            if done[0] < len(pending):
-                pending[done[0]]()
-                done[0] = done[0] + 1
+        def small_step(count=1):
+            for n in range(count):
+                if done[0] < len(pending):
+                    pending[done[0]]()
+                    done[0] = done[0] + 1
 
         def flush(upto):
-            while_guard = range(len(pending))
-            for n in while_guard:
+            for n in range(len(pending)):
                 if done[0] < upto:
                     small_step()
 
@@ -171,7 +186,7 @@ def tile_selfprojectiondev_pb_t_kernel(tc, x, o_xi, p_xi, rel_o_xi, out_0, out_1
 
         def quant_x(b):
             grouped = state[("grouped", b)]
-            pool = xl if b >= NB - LATE_EXP else xq
+            pool = xl if b >= EARLY else xq
             codes = pool.tile([P, NJ], U32, align_bytes=64, name="codes")
             plane = pool.tile([P, NJ], U8, align_bytes=64, name="plane")
             nc.vector.quantize_mx(
@@ -182,34 +197,27 @@ def tile_selfprojectiondev_pb_t_kernel(tc, x, o_xi, p_xi, rel_o_xi, out_0, out_1
             state[("xq", b)] = (codes, plane)
             small_step()
 
-        def mm_z(b):
+        def mm_x(b, which, out):
             codes, plane = state[("xq", b)]
-            z_ps = pz.tile([P, 4, ND, NW], F32, name="z_ps")
-            for jt in range(4):
-                cols = slice(jt * P, (jt + 1) * P)
-                nc.tensor.matmul_mx(
-                    out=z_ps[:, jt].rearrange("p d c -> p (d c)"),
-                    lhsT=codes[:, cols].bitcast(FP8X4),
-                    lhsT_scale=plane[:, cols],
-                    rhs=w_codes[:, 0:P].bitcast(FP8X4),
-                    rhs_scale=w_plane[:, 0:P],
-                    start=True,
-                    stop=True,
-                )
-            state[("z_ps", b)] = z_ps
-
-        def mm_r(b):
-            codes, plane = state[("xq", b)]
-            r_ps = pr.tile([P, NJ], F32, name="r_ps", tag="r_ps")
+            cols = slice(which * P, (which + 1) * P)
             nc.tensor.matmul_mx(
-                out=r_ps[:],
-                lhsT=w_codes[:, P : 2 * P].bitcast(FP8X4),
-                lhsT_scale=w_plane[:, P : 2 * P],
+                out=out,
+                lhsT=w_codes[:, cols].bitcast(FP8X4),
+                lhsT_scale=w_plane[:, cols],
                 rhs=codes[:].bitcast(FP8X4),
                 rhs_scale=plane[:],
                 start=True,
                 stop=True,
             )
+
+        def mm_z(b):
+            z_ps = pz.tile([P, NJ], F32, name="z_ps", tag="z_ps")
+            mm_x(b, 0, z_ps[:])
+            state[("z_ps", b)] = z_ps
+
+        def mm_r(b):
+            r_ps = pr.tile([P, NJ], F32, name="r_ps", tag="r_ps")
+            mm_x(b, 1, r_ps[:])
             state[("r_ps", b)] = r_ps
 
         def row_max(b):
@@ -219,68 +227,63 @@ def tile_selfprojectiondev_pb_t_kernel(tc, x, o_xi, p_xi, rel_o_xi, out_0, out_1
             )
             small_step()
 
+        group_of = {}
+        for g, members in enumerate(GROUPS):
+            for b in members:
+                group_of[b] = (g, b - members[0])
+
         def tanh1(b):
             z_ps = state[("z_ps", b)]
-            if b % 4 == 0:
-                state[("acc", b // 4)] = small.tile([P, 2, 4 * ND], F32, name="acc")
-            acc = state[("acc", b // 4)]
-            t_raw = tp.tile([P, ND, NW, 4], F32, name="t_raw")
-            for d in range(ND):
-                k = (b % 4) * ND + d
-                nc.scalar.activation(
-                    out=t_raw[:, d],
-                    in_=z_ps[:, :, d, :].rearrange("p t c -> p c t"),
-                    func=ACT.Tanh,
-                    accum_out=acc[:, 0, k : k + 1],
-                )
+            g, k = group_of[b]
+            if k == 0:
+                state[("acc", g)] = small.tile([P, 2, 8], F32, name="acc")
+            acc = state[("acc", g)]
+            t_raw = tp.tile([P, NJ], F32, name="t_raw")
+            nc.scalar.activation(out=t_raw[:], in_=z_ps[:], func=ACT.Tanh, accum_out=acc[:, 0, k : k + 1])
             state[("t_raw", b)] = t_raw
 
         def square1(b):
-            acc = state[("acc", b // 4)]
-            t_raw = state[("t_raw", b)]
-            for d in range(ND):
-                k = (b % 4) * ND + d
-                sq = junk.tile([P, P], BF16, name="sq")
-                nc.scalar.activation(
-                    out=sq[:],
-                    in_=t_raw[:, d].rearrange("p c t -> p (c t)"),
-                    func=ACT.Square,
-                    scale=ROOT_C1,
-                    accum_out=acc[:, 1, k : k + 1],
-                )
+            g, k = group_of[b]
+            sq = junk.tile([P, NJ], BF16, name="sq")
+            nc.scalar.activation(
+                out=sq[:], in_=state[("t_raw", b)][:], func=ACT.Square,
+                accum_out=state[("acc", g)][:, 1, k : k + 1],
+            )
 
         def exp1(b):
             r_ps = state[("r_ps", b)]
             ex = junk.tile([P, NJ], BF16, name="ex")
             nc.scalar.activation(
-                out=ex[:],
-                in_=r_ps[:],
-                func=ACT.Exp,
-                bias=nm[:, b : b + 1],
-                scale=1.0,
+                out=ex[:], in_=r_ps[:], func=ACT.Exp, bias=nm[:, b : b + 1], scale=1.0,
                 accum_out=se[:, b : b + 1],
             )
 
         def mom_tile(c):
             if ("mom_ps", c) not in state:
-                state[("mom_ps", c)] = pm.tile([P, 3, SW], F32, name="mom_ps")
+                state[("mom_ps", c)] = pm.tile([P, 2, W], F32, name="mom_ps")
             return state[("mom_ps", c)]
 
-        def moments_mm(c, lo, hi, sums, squares, plain, scaled):
-            mom_ps = mom_tile(c)
-            nc.tensor.matmul(out=mom_ps[:, 0, lo:hi], lhsT=plain[:], rhs=sums, start=True, stop=True)
-            nc.tensor.matmul(out=mom_ps[:, 1, lo:hi], lhsT=plain[:], rhs=squares, start=True, stop=True)
-            nc.tensor.matmul(out=mom_ps[:, 2, lo:hi], lhsT=scaled[:], rhs=sums, start=True, stop=True)
+        def moments(c, lo, sums, blk):
+            width = sums.shape[2]
+            nc.tensor.matmul(
+                out=mom_tile(c)[:, :, lo : lo + width], lhsT=blk[:], rhs=sums, start=True, stop=True
+            )
 
-        def chain(c, lo, hi):
+        def t_moments(g):
+            moments(g, 0, state[("acc", g)][:, :, 0 : len(GROUPS[g])], blk1)
+
+        def chain_tiles(c):
+            mom = small.tile([P, 2, W], F32, name="mom")
+            var = small.tile([P, W], F32, name="var")
+            tmp = small.tile([P, W], F32, name="tmp")
+            rstd = small.tile([P, W], F32, name="rstd")
+            return mom, var, tmp, rstd
+
+        def chain(c, n1, n2):
             mom_ps = mom_tile(c)
-            mom = small.tile([P, 3, SW], F32, name="mom")
-            var = small.tile([P, SW], F32, name="var")
-            tmp = small.tile([P, SW], F32, name="tmp")
-            bits = small.tile([P, SW], I32, name="bits")
-            guess = small.tile([P, SW], I32, name="guess")
-            rstd = small.tile([P, SW], F32, name="rstd")
-            cs = slice(lo, hi)
+            mom, var, tmp, rstd = chain_tiles(c)
+            guess = small.tile([P, W], I32, name="guess")
+            cs = slice(0, n1 + n2)
             y = guess[:, cs].bitcast(F32)
             v = var[:, cs]
             w = tmp[:, cs]
@@ -289,15 +292,11 @@ def tile_selfprojectiondev_pb_t_kernel(tc, x, o_xi, p_xi, rel_o_xi, out_0, out_1
             stt = nc.vector.scalar_tensor_tensor
             ops = [
                 lambda: nc.vector.tensor_copy(out=mom[:, :, cs], in_=mom_ps[:, :, cs]),
-                lambda: tt(out=w, in0=mom[:, 2, cs], in1=mom[:, 2, cs], op=ALU.mult),
+                lambda: tt(out=w, in0=mom[:, 0, cs], in1=mom[:, 0, cs], op=ALU.mult),
                 lambda: tt(out=v, in0=mom[:, 1, cs], in1=w, op=ALU.subtract),
                 lambda: ts(out=v, in0=v, scalar1=1e-30, scalar2=None, op0=ALU.max),
-                lambda: ts(out=bits[:, cs], in0=v.bitcast(I32), scalar1=8, scalar2=None,
-                           op0=ALU.logical_shift_right),
-                lambda: ts(out=bits[:, cs], in0=bits[:, cs], scalar1=-1.0, scalar2=float(MAGIC),
+                lambda: ts(out=guess[:, cs], in0=v.bitcast(I32), scalar1=-0.5, scalar2=MAGIC,
                            op0=ALU.mult, op1=ALU.add),
-                lambda: ts(out=guess[:, cs], in0=bits[:, cs], scalar1=7, scalar2=None,
-                           op0=ALU.logical_shift_left),
             ]
             for n in range(3):
                 ops.extend([
@@ -305,23 +304,23 @@ def tile_selfprojectiondev_pb_t_kernel(tc, x, o_xi, p_xi, rel_o_xi, out_0, out_1
                     lambda: stt(out=w, in0=w, scalar=-0.5, in1=v, op0=ALU.mult, op1=ALU.mult),
                     lambda: stt(out=y, in0=w, scalar=1.5, in1=y, op0=ALU.add, op1=ALU.mult),
                 ])
-            ops.extend([
-                lambda: tt(out=w, in0=v, in1=y, op=ALU.mult),
-                lambda: ts(out=w, in0=w, scalar1=EPS, scalar2=None, op0=ALU.add),
-                lambda: nc.vector.reciprocal(out=rstd[:, cs], in_=w),
-            ])
+            ops.append(lambda: tt(out=w, in0=v, in1=y, op=ALU.mult))
+            if n1:
+                ops.append(lambda: ts(out=tmp[:, 0:n1], in0=tmp[:, 0:n1], scalar1=ROOT1, scalar2=EPS,
+                                      op0=ALU.mult, op1=ALU.add))
+            if n2:
+                ops.append(lambda: ts(out=tmp[:, n1 : n1 + n2], in0=tmp[:, n1 : n1 + n2], scalar1=ROOT2,
+                                      scalar2=EPS, op0=ALU.mult, op1=ALU.add))
+            ops.append(lambda: nc.vector.reciprocal(out=rstd[:, cs], in_=w))
             pending.extend(ops)
             state[("st", c)] = (mom, rstd, len(pending))
 
-        def last_stats_a(c, lo, hi):
+        def last_stats_a(c, n2):
             mom_ps = mom_tile(c)
-            cs = slice(lo, hi)
-            mom = small.tile([P, 3, SW], F32, name="mom")
-            var = small.tile([P, SW], F32, name="var")
-            tmp = small.tile([P, SW], F32, name="tmp")
-            rstd = small.tile([P, SW], F32, name="rstd")
+            mom, var, tmp, rstd = chain_tiles(c)
+            cs = slice(0, n2)
             nc.vector.tensor_copy(out=mom[:, :, cs], in_=mom_ps[:, :, cs])
-            nc.vector.tensor_tensor(out=tmp[:, cs], in0=mom[:, 2, cs], in1=mom[:, 2, cs], op=ALU.mult)
+            nc.vector.tensor_tensor(out=tmp[:, cs], in0=mom[:, 0, cs], in1=mom[:, 0, cs], op=ALU.mult)
             nc.vector.tensor_tensor(out=var[:, cs], in0=mom[:, 1, cs], in1=tmp[:, cs], op=ALU.subtract)
             nc.vector.tensor_scalar(out=var[:, cs], in0=var[:, cs], scalar1=1e-30, scalar2=None, op0=ALU.max)
             nc.scalar.activation(out=tmp[:, cs], in_=var[:, cs], func=ACT.Sqrt)
@@ -330,99 +329,128 @@ def tile_selfprojectiondev_pb_t_kernel(tc, x, o_xi, p_xi, rel_o_xi, out_0, out_1
 
         def last_stats_b():
             tmp, rstd, cs = state["last"]
-            nc.vector.tensor_scalar(out=tmp[:, cs], in0=tmp[:, cs], scalar1=EPS, scalar2=None, op0=ALU.add)
+            nc.vector.tensor_scalar(
+                out=tmp[:, cs], in0=tmp[:, cs], scalar1=ROOT2, scalar2=EPS, op0=ALU.mult, op1=ALU.add
+            )
             nc.vector.reciprocal(out=rstd[:, cs], in_=tmp[:, cs])
 
         def affine(b):
-            mom, rstd, end = state[("st", b // 4)]
+            g, k = group_of[b]
+            mom, rstd, end = state[("st", g)]
             flush(end)
-            if b % 4 == 0:
-                state[("tg", b // 4)] = (
-                    tq.tile([P, 4, ND, P], BF16, align_bytes=64, name="tg"),
-                    tq.tile([P, 4 * P], U32, align_bytes=64, name="t_codes"),
-                    tq.tile([P, 4 * P], U8, align_bytes=64, name="t_plane"),
+            tb = tbp.tile([P, NJ], BF16, align_bytes=64, name="tb")
+            nc.vector.tensor_scalar(
+                out=tb[:], in0=state[("t_raw", b)][:], scalar1=mom[:, 0, k : k + 1],
+                scalar2=rstd[:, k : k + 1], op0=ALU.subtract, op1=ALU.mult,
+            )
+            state[("tb", b)] = tb
+            small_step()
+
+        def flip(b):
+            if b % 2 == 0:
+                state[("tp", b // 2)] = pz.tile([P, 2, 2, P], F32, name="tp_ps", tag="z_ps")
+            tp_ps = state[("tp", b // 2)]
+            words = state[("tb", b)][:].bitcast(F32)
+            for u in range(2):
+                nc.tensor.transpose(out=tp_ps[:, b % 2, u, :], in_=words[:, u : NJ // 2 : 2], identity=ident[:])
+
+        def gather(pair):
+            q = pair // 2
+            h = 2 * (pair % 2)
+            if h == 0:
+                state[("tg", q)] = (
+                    tq.tile([P, ND, 4, NW, 4], BF16, align_bytes=64, name="tg"),
+                    tq.tile([P, ND, P], U32, align_bytes=64, name="t_codes"),
+                    tq.tile([P, ND, P], U8, align_bytes=64, name="t_plane"),
                 )
-            tg, t_codes, t_plane = state[("tg", b // 4)]
-            t_raw = state[("t_raw", b)]
-            for d in range(ND):
-                k = (b % 4) * ND + d
-                nc.vector.tensor_scalar(
-                    out=tg[:, b % 4, d, :],
-                    in0=t_raw[:, d].rearrange("p c t -> p (c t)"),
-                    scalar1=mom[:, 0, k : k + 1],
-                    scalar2=rstd[:, k : k + 1],
-                    op0=ALU.subtract,
-                    op1=ALU.mult,
-                )
-                small_step()
+            tg = state[("tg", q)][0]
+            dst = tg[:, :, h : h + 2].rearrange("p d b c t -> p d b (c t)").bitcast(F32)
+            src = state[("tp", pair)]
+            nc.scalar.copy(
+                out=dst.rearrange("p d b (c u) -> p b d c u", u=2),
+                in_=src[:].rearrange("p b u (d c) -> p b d c u", d=ND),
+            )
 
         def quant_t(q):
             tg, t_codes, t_plane = state[("tg", q)]
             nc.vector.quantize_mx(
-                out=t_codes[:].bitcast(FP8X4),
-                scales=t_plane[:],
-                in_=tg[:].rearrange("p b d e -> p (b d e)"),
+                out=t_codes[:].rearrange("p d w -> p (d w)").bitcast(FP8X4),
+                scales=t_plane[:].rearrange("p d w -> p (d w)"),
+                in_=tg[:].rearrange("p d b c t -> p (d b c t)"),
             )
             small_step()
+
+        unit_of = {}
+        for n, quads in enumerate(UNITS):
+            for k, q in enumerate(quads):
+                unit_of[q] = (n, k)
 
         def s2_mm(q):
             tg, t_codes, t_plane = state[("tg", q)]
-            u_ps = pu.tile([P, 4, ND, NW], F32, name="u_ps", tag="u_ps")
-            nc.tensor.matmul_mx(
-                out=u_ps[:].rearrange("p b d c -> p (b d c)"),
-                lhsT=p_codes[:].bitcast(FP8X4),
-                lhsT_scale=p_plane[:],
-                rhs=t_codes[:].bitcast(FP8X4),
-                rhs_scale=t_plane[:],
-                start=True,
-                stop=True,
-            )
-            state[("u_ps", q)] = u_ps
-
-        def s2_tanh(q):
-            u_ps = state[("u_ps", q)]
-            bs = slice(4 * q, 4 * q + 4)
+            n, k = unit_of[q]
+            if k == 0:
+                state[("u_ps", n)] = pu.tile([P, 2, P], F32, name="u_ps")
+            u_ps = state[("u_ps", n)]
             for d in range(ND):
-                rows = slice(NW * d, NW * (d + 1))
-                nc.scalar.activation(out=u_all[rows, bs, :], in_=u_ps[rows, :, d, :], func=ACT.Tanh)
-            usq = fin.tile([P, 4, NW], F32, name="usq")
-            nc.scalar.activation(out=usq[:], in_=u_all[:, bs, :], func=ACT.Square, scale=ROOT_C2)
-            state[("usq", q)] = usq
+                nc.tensor.matmul_mx(
+                    out=u_ps[:, k, :],
+                    lhsT=p_codes[:, d].bitcast(FP8X4),
+                    lhsT_scale=p_plane[:, d],
+                    rhs=t_codes[:, d].bitcast(FP8X4),
+                    rhs_scale=t_plane[:, d],
+                    start=(d == 0),
+                    stop=(d == ND - 1),
+                )
 
-        def s2_place(q):
-            if q <= 4:
-                return q + 3, 16
-            return 8, 16 + 4 * (q - 5)
+        def unit_batches(n):
+            return slice(4 * UNITS[n][0], 4 * UNITS[n][-1] + 4)
 
-        def s2_sums(q):
-            bs = slice(4 * q, 4 * q + 4)
-            usq = state[("usq", q)]
-            st2 = small.tile([P, 2, 4], F32, name="st2")
-            nc.vector.tensor_reduce(out=st2[:, 0, :], in_=u_all[:, bs, :], axis=AX.X, op=ALU.add)
+        def s2_tanh(n):
+            nq = len(UNITS[n])
+            bs = unit_batches(n)
+            flat = u_all[:, bs, :].rearrange("p b c -> p (b c)")
+            nc.scalar.activation(
+                out=flat, in_=state[("u_ps", n)][:, 0:nq, :].rearrange("p k c -> p (k c)"), func=ACT.Tanh
+            )
+            usq = fin.tile([P, 8, NW], F32, name="usq")
+            nc.scalar.activation(
+                out=usq[:, 0 : 4 * nq].rearrange("p b c -> p (b c)"), in_=flat, func=ACT.Square
+            )
+            state[("usq", n)] = usq
+
+        def s2_sums(n, c, lo):
+            nb = 4 * len(UNITS[n])
+            st2 = small.tile([P, 2, 8], F32, name="st2")
+            nc.vector.tensor_reduce(
+                out=st2[:, 0, 0:nb], in_=u_all[:, unit_batches(n), :], axis=AX.X, op=ALU.add
+            )
             small_step()
-            nc.vector.tensor_reduce(out=st2[:, 1, :], in_=usq[:], axis=AX.X, op=ALU.add)
+            nc.vector.tensor_reduce(
+                out=st2[:, 1, 0:nb], in_=state[("usq", n)][:, 0:nb], axis=AX.X, op=ALU.add
+            )
             small_step()
-            c, lo = s2_place(q)
-            moments_mm(c, lo, lo + 4, st2[:, 0, :], st2[:, 1, :], blk2, blk2s)
+            moments(c, lo, st2[:, :, 0:nb], blk2)
+            state[("place", n)] = (c, lo)
 
-        def s2_out(q):
-            bs = slice(4 * q, 4 * q + 4)
-            c, lo = s2_place(q)
+        def s2_out(n):
+            bs = unit_batches(n)
+            nb = 4 * len(UNITS[n])
+            c, lo = state[("place", n)]
             mom, rstd, end = state[("st", c)]
             flush(end)
-            cen = fin.tile([P, 4, NW], F32, name="cen")
+            cen = fin.tile([P, 8, NW], F32, name="cen")
             nc.vector.tensor_tensor(
-                out=cen[:], in0=u_all[:, bs, :],
-                in1=mom[:, 0, lo : lo + 4].unsqueeze(2).to_broadcast([P, 4, NW]), op=ALU.subtract,
+                out=cen[:, 0:nb], in0=u_all[:, bs, :],
+                in1=mom[:, 0, lo : lo + nb].unsqueeze(2).to_broadcast([P, nb, NW]), op=ALU.subtract,
             )
             small_step()
-            res = fin.tile([P, 4, NW], F32, name="res")
+            res = fin.tile([P, 8, NW], F32, name="res")
             nc.vector.tensor_tensor(
-                out=res[:], in0=cen[:],
-                in1=rstd[:, lo : lo + 4].unsqueeze(2).to_broadcast([P, 4, NW]), op=ALU.mult,
+                out=res[:, 0:nb], in0=cen[:, 0:nb],
+                in1=rstd[:, lo : lo + nb].unsqueeze(2).to_broadcast([P, nb, NW]), op=ALU.mult,
             )
             small_step()
-            nc.sync.dma_start(out=out_0[bs].rearrange("b d q c -> (d q) b c"), in_=res[:])
+            nc.sync.dma_start(out=out_0[bs].rearrange("b d q c -> (d q) b c"), in_=res[:, 0:nb])
 
         def mass_a():
             nm_ps = pr.tile([P, P], F32, name="nm_ps", tag="r_ps")
@@ -430,20 +458,16 @@ def tile_selfprojectiondev_pb_t_kernel(tc, x, o_xi, p_xi, rel_o_xi, out_0, out_1
             nmt = nm_ps[0:NB, :].rearrange("b (d c) -> b d c", d=ND)
             ntop = fin.tile([NB, ND], F32, name="ntop")
             nc.vector.tensor_reduce(out=ntop[:], in_=nmt, axis=AX.X, op=ALU.min)
-            small_step()
             diff = fin.tile([NB, ND, NW], F32, name="diff")
             nc.vector.tensor_tensor(
-                out=diff[:], in0=ntop[:].unsqueeze(2).to_broadcast([NB, ND, NW]), in1=nmt,
-                op=ALU.subtract,
+                out=diff[:], in0=ntop[:].unsqueeze(2).to_broadcast([NB, ND, NW]), in1=nmt, op=ALU.subtract
             )
-            small_step()
             corr = fin.tile([NB, ND, NW], F32, name="corr")
             nc.scalar.activation(out=corr[:], in_=diff[:], func=ACT.Exp)
             state["mass"] = corr
 
         def warm_sqrt():
-            warm = fin.tile([P, 1], F32, name="warm")
-            nc.scalar.activation(out=warm[:], in_=ones1[:, 0:1], func=ACT.Sqrt)
+            nc.scalar.activation(out=warm[:], in_=blk1[:, 0:1], func=ACT.Sqrt)
 
         def mass_b():
             corr = state["mass"]
@@ -463,84 +487,124 @@ def tile_selfprojectiondev_pb_t_kernel(tc, x, o_xi, p_xi, rel_o_xi, out_0, out_1
             )
             nc.sync.dma_start(out=out_1, in_=mres[:])
 
-        def on(v, step=1, rem=0):
-            return 0 <= v < NB and v % step == rem
+        def on(v):
+            return 0 <= v < NB
 
-        late_next = [NB - LATE_EXP]
+        def affine_list(i):
+            if 13 <= i <= 27:
+                return [i - 13]
+            return {28: [15, 16], 29: [17, 18], 30: [19, 20], 31: [21, 22, 23]}.get(i, [])
 
-        def late(count):
-            for n in range(count):
-                b = late_next[0]
-                late_next[0] = b + 1
-                mm_r(b)
-                exp1(b)
+        def flips(batches):
+            for b in batches:
+                flip(b)
+
+        def gathers(batches):
+            for b in batches:
+                if b % 2 == 1:
+                    gather(b // 2)
 
         for i in range(-2, NB):
-            if on(i - 1) and i - 1 < NB - LATE_EXP:
+            if on(i - 1) and i - 1 < EARLY:
                 exp1(i - 1)
-            if on(i - 13, 4, 0):
-                s2_tanh((i - 13) // 4)
             if on(i + 2):
                 regroup_s(i + 2)
-            if on(i - 5, 4, 0):
-                c = (i - 5) // 4
-                chain(c, 0, 20 if c >= 3 else 16)
+            if i in (9, 17):
+                chain((i - 9) // 8, 8, 0)
+            if i == 25:
+                chain(2, 8, 8)
+            if i == 29:
+                chain(3, 4, 0)
+            flips(affine_list(i - 1))
             if on(i + 1):
                 quant_x(i + 1)
                 mm_z(i + 1)
-                mm_r(i + 1)
-            if on(i):
+                if i + 1 < EARLY_MAX:
+                    mm_r(i + 1)
+            if on(i) and i < EARLY_MAX:
                 row_max(i)
+            if on(i):
                 tanh1(i)
             if on(i + 2):
                 regroup_v(i + 2)
+            if i == -2:
+                prep_w()
             if i == 1:
                 prep_p_copy()
             if on(i):
                 square1(i)
-                if i % 4 == 3:
-                    acc = state[("acc", i // 4)]
-                    moments_mm(i // 4, 0, 16, acc[:, 0, :], acc[:, 1, :], ones1, ones1s)
-            if on(i - 12, 4, 0):
-                quant_t((i - 12) // 4)
-                s2_mm((i - 12) // 4)
+                g, k = group_of[i]
+                if i == GROUPS[g][-1] and i < NB - 1:
+                    t_moments(g)
+            gathers(affine_list(i - 1))
             if i == 2:
                 prep_p_quant()
-            if on(i - 8):
-                affine(i - 8)
-            if on(i - 14, 4, 0):
-                s2_sums((i - 14) // 4)
-            if on(i - 20, 4, 0):
-                s2_out((i - 20) // 4)
+            for b in affine_list(i):
+                affine(b)
+            if i in (18, 22, 26, 30):
+                quant_t((i - 18) // 4)
+                s2_mm((i - 18) // 4)
+            if i == 23:
+                s2_tanh(0)
+            if i == 24:
+                s2_sums(0, 2, 8)
+            if i == 31:
+                s2_tanh(1)
 
-        quant_t(5)
-        s2_mm(5)
-        chain(7, 0, 20)
-        mass_a()
-        s2_tanh(5)
-        late(8)
+        flips(affine_list(NB - 1))
+        gathers(affine_list(NB - 1))
+        mm_r(24)
+        mm_r(25)
+        exp1(24)
+        quant_t(4)
+        s2_mm(4)
         for b in range(24, 28):
             affine(b)
-        s2_out(3)
-        quant_t(6)
-        s2_mm(6)
-        s2_tanh(6)
-        late(8)
+        s2_sums(1, 4, 4)
+        t_moments(4)
+        exp1(25)
+        flips(range(24, 28))
+        gathers(range(24, 28))
+        mm_r(26)
+        mm_r(29)
+        quant_t(5)
+        s2_mm(5)
+        row_max(29)
+        exp1(26)
+        chain(4, 4, 8)
+        mm_r(30)
+        s2_tanh(2)
         for b in range(28, 32):
             affine(b)
-        s2_sums(5)
+        flips(range(28, 32))
+        exp1(29)
+        gathers(range(28, 32))
+        quant_t(6)
+        s2_mm(6)
+        mm_r(27)
+        row_max(30)
+        exp1(30)
+        s2_tanh(3)
+        mm_r(31)
+        s2_sums(2, 5, 0)
         quant_t(7)
         s2_mm(7)
-        s2_tanh(7)
+        exp1(27)
+        mm_r(28)
+        row_max(31)
+        exp1(31)
+        s2_tanh(4)
+        exp1(28)
+        s2_out(0)
+        s2_out(1)
+        mass_a()
+        s2_sums(3, 5, 8)
+        s2_sums(4, 5, 12)
         warm_sqrt()
-        s2_out(4)
-        s2_sums(6)
-        s2_sums(7)
-        last_stats_a(8, 16, 28)
+        last_stats_a(5, 16)
         mass_b()
         last_stats_b()
-        s2_out(7)
-        s2_out(5)
-        s2_out(6)
-        assert late_next[0] == NB
+        s2_out(4)
+        s2_out(3)
+        s2_out(2)
         assert done[0] == len(pending)

@@ -26,17 +26,14 @@ N2 = NW * NW
 ROOT1 = math.sqrt(N1 / (N1 - 1.0))
 ROOT2 = math.sqrt(N2 / (N2 - 1.0))
 MAGIC = float(0x5F3759DF)
-EARLY = 24
-EARLY_MAX = 29
+LAG = 8
 GROUPS = [range(0, 8), range(8, 16), range(16, 24), range(24, 28), range(28, 32)]
 UNITS = [(0, 1), (2, 3), (4, 5), (6,), (7,)]
 W = 24
 
 
 def s_cols(b):
-    if b < 15:
-        return 72
-    return 120 if b < EARLY + 2 else 248
+    return 112 if b < 15 else 136
 
 FLOPS = 2 * NB * ND * (2 * NI * NJ * NW + NW * NJ * NW)
 
@@ -46,9 +43,8 @@ def tile_selfprojectiondev_pb_t_kernel(tc, x, o_xi, p_xi, rel_o_xi, out_0, out_1
     with ExitStack() as ctx:
         const = ctx.enter_context(tc.tile_pool(name="const", bufs=1))
         rawp = ctx.enter_context(tc.tile_pool(name="rawp", bufs=8))
-        grp = ctx.enter_context(tc.tile_pool(name="grp", bufs=3))
-        xq = ctx.enter_context(tc.tile_pool(name="xq", bufs=3))
-        xl = ctx.enter_context(tc.tile_pool(name="xl", bufs=NB - EARLY))
+        grp = ctx.enter_context(tc.tile_pool(name="grp", bufs=4))
+        xl = ctx.enter_context(tc.tile_pool(name="xl", bufs=LAG + 4))
         tp = ctx.enter_context(tc.tile_pool(name="tp", bufs=18))
         tbp = ctx.enter_context(tc.tile_pool(name="tbp", bufs=4))
         junk = ctx.enter_context(tc.tile_pool(name="junk", bufs=2))
@@ -186,9 +182,8 @@ def tile_selfprojectiondev_pb_t_kernel(tc, x, o_xi, p_xi, rel_o_xi, out_0, out_1
 
         def quant_x(b):
             grouped = state[("grouped", b)]
-            pool = xl if b >= EARLY else xq
-            codes = pool.tile([P, NJ], U32, align_bytes=64, name="codes")
-            plane = pool.tile([P, NJ], U8, align_bytes=64, name="plane")
+            codes = xl.tile([P, NJ], U32, align_bytes=64, name="codes")
+            plane = xl.tile([P, NJ], U8, align_bytes=64, name="plane")
             nc.vector.quantize_mx(
                 out=codes[:].bitcast(FP8X4),
                 scales=plane[:],
@@ -315,23 +310,27 @@ def tile_selfprojectiondev_pb_t_kernel(tc, x, o_xi, p_xi, rel_o_xi, out_0, out_1
             pending.extend(ops)
             state[("st", c)] = (mom, rstd, len(pending))
 
-        def last_stats_a(c, n2):
+        def root_a(c, n1, n2):
             mom_ps = mom_tile(c)
             mom, var, tmp, rstd = chain_tiles(c)
-            cs = slice(0, n2)
+            cs = slice(0, n1 + n2)
             nc.vector.tensor_copy(out=mom[:, :, cs], in_=mom_ps[:, :, cs])
             nc.vector.tensor_tensor(out=tmp[:, cs], in0=mom[:, 0, cs], in1=mom[:, 0, cs], op=ALU.mult)
             nc.vector.tensor_tensor(out=var[:, cs], in0=mom[:, 1, cs], in1=tmp[:, cs], op=ALU.subtract)
             nc.vector.tensor_scalar(out=var[:, cs], in0=var[:, cs], scalar1=1e-30, scalar2=None, op0=ALU.max)
             nc.scalar.activation(out=tmp[:, cs], in_=var[:, cs], func=ACT.Sqrt)
             state[("st", c)] = (mom, rstd, len(pending))
-            state["last"] = (tmp, rstd, cs)
+            state[("root", c)] = (tmp, rstd, n1, n2)
 
-        def last_stats_b():
-            tmp, rstd, cs = state["last"]
-            nc.vector.tensor_scalar(
-                out=tmp[:, cs], in0=tmp[:, cs], scalar1=ROOT2, scalar2=EPS, op0=ALU.mult, op1=ALU.add
-            )
+        def root_b(c):
+            tmp, rstd, n1, n2 = state[("root", c)]
+            cs = slice(0, n1 + n2)
+            for root, lo, hi in ((ROOT1, 0, n1), (ROOT2, n1, n1 + n2)):
+                if lo < hi:
+                    nc.vector.tensor_scalar(
+                        out=tmp[:, lo:hi], in0=tmp[:, lo:hi], scalar1=root, scalar2=EPS,
+                        op0=ALU.mult, op1=ALU.add,
+                    )
             nc.vector.reciprocal(out=rstd[:, cs], in_=tmp[:, cs])
 
         def affine(b):
@@ -504,35 +503,39 @@ def tile_selfprojectiondev_pb_t_kernel(tc, x, o_xi, p_xi, rel_o_xi, out_0, out_1
                 if b % 2 == 1:
                     gather(b // 2)
 
-        for i in range(-2, NB):
-            if on(i - 1) and i - 1 < EARLY:
-                exp1(i - 1)
-            if on(i + 2):
-                regroup_s(i + 2)
+        def softmax_mm(i):
+            if on(i - LAG + 1):
+                mm_r(i - LAG + 1)
+
+        for i in range(-3, NB):
             if i in (9, 17):
                 chain((i - 9) // 8, 8, 0)
             if i == 25:
                 chain(2, 8, 8)
             if i == 29:
                 chain(3, 4, 0)
+            if on(i):
+                tanh1(i)
+            if on(i - LAG - 1):
+                exp1(i - LAG - 1)
             flips(affine_list(i - 1))
             if on(i + 1):
                 quant_x(i + 1)
                 mm_z(i + 1)
-                if i + 1 < EARLY_MAX:
-                    mm_r(i + 1)
-            if on(i) and i < EARLY_MAX:
-                row_max(i)
+            if on(i + 3):
+                regroup_s(i + 3)
             if on(i):
-                tanh1(i)
-            if on(i + 2):
-                regroup_v(i + 2)
-            if i == -2:
+                square1(i)
+            softmax_mm(i)
+            if on(i - LAG):
+                row_max(i - LAG)
+            if on(i + 3):
+                regroup_v(i + 3)
+            if i == -3:
                 prep_w()
             if i == 1:
                 prep_p_copy()
             if on(i):
-                square1(i)
                 g, k = group_of[i]
                 if i == GROUPS[g][-1] and i < NB - 1:
                     t_moments(g)
@@ -551,60 +554,65 @@ def tile_selfprojectiondev_pb_t_kernel(tc, x, o_xi, p_xi, rel_o_xi, out_0, out_1
             if i == 31:
                 s2_tanh(1)
 
+        step = [NB]
+
+        def softmax_step():
+            i = step[0]
+            step[0] = i + 1
+            exp1(i - LAG - 1)
+            softmax_mm(i)
+            if on(i - LAG):
+                row_max(i - LAG)
+
         flips(affine_list(NB - 1))
-        gathers(affine_list(NB - 1))
-        mm_r(24)
-        mm_r(25)
-        exp1(24)
-        quant_t(4)
-        s2_mm(4)
+        gathers([19, 21, 23])
         for b in range(24, 28):
             affine(b)
+        softmax_step()
         s2_sums(1, 4, 4)
         t_moments(4)
-        exp1(25)
         flips(range(24, 28))
-        gathers(range(24, 28))
-        mm_r(26)
-        mm_r(29)
+        gathers([25, 27])
+        quant_t(4)
+        s2_mm(4)
+        chain(4, 4, 8)
+        softmax_step()
+        small_step(1)
         quant_t(5)
         s2_mm(5)
-        row_max(29)
-        exp1(26)
-        chain(4, 4, 8)
-        mm_r(30)
+        small_step(1)
+        softmax_step()
+        small_step(1)
+        s2_out(0)
         s2_tanh(2)
+        softmax_step()
+        small_step(1)
+        quant_t(6)
+        s2_mm(6)
+        small_step(1)
         for b in range(28, 32):
             affine(b)
         flips(range(28, 32))
-        exp1(29)
-        gathers(range(28, 32))
-        quant_t(6)
-        s2_mm(6)
-        mm_r(27)
-        row_max(30)
-        exp1(30)
+        gathers([29, 31])
+        softmax_step()
         s2_tanh(3)
-        mm_r(31)
         s2_sums(2, 5, 0)
+        softmax_step()
         quant_t(7)
         s2_mm(7)
-        exp1(27)
-        mm_r(28)
-        row_max(31)
-        exp1(31)
+        softmax_step()
+        s2_sums(3, 5, 8)
         s2_tanh(4)
-        exp1(28)
-        s2_out(0)
+        softmax_step()
         s2_out(1)
         mass_a()
-        s2_sums(3, 5, 8)
         s2_sums(4, 5, 12)
-        warm_sqrt()
-        last_stats_a(5, 16)
+        softmax_step()
+        root_a(5, 0, 16)
         mass_b()
-        last_stats_b()
+        root_b(5)
         s2_out(4)
         s2_out(3)
         s2_out(2)
         assert done[0] == len(pending)
+        assert step[0] == NB + LAG + 1

@@ -26,14 +26,14 @@ N2 = NW * NW
 ROOT1 = math.sqrt(N1 / (N1 - 1.0))
 ROOT2 = math.sqrt(N2 / (N2 - 1.0))
 MAGIC = float(0x5F3759DF)
-LAG = 8
-GROUPS = [range(0, 8), range(8, 16), range(16, 24), range(24, 28), range(28, 32)]
-UNITS = [(0, 1), (2, 3), (4, 5), (6,), (7,)]
+LAG = 4
+GROUPS = [range(8 * g, 8 * g + 8) for g in range(4)]
+UNITS = [(0, 1), (2, 3), (4, 5, 6), (7,)]
 W = 24
 
 
 def s_cols(b):
-    return 112 if b < 15 else 136
+    return 104 if b < 15 else 120
 
 FLOPS = 2 * NB * ND * (2 * NI * NJ * NW + NW * NJ * NW)
 
@@ -46,13 +46,14 @@ def tile_selfprojectiondev_pb_t_kernel(tc, x, o_xi, p_xi, rel_o_xi, out_0, out_1
         grp = ctx.enter_context(tc.tile_pool(name="grp", bufs=4))
         xl = ctx.enter_context(tc.tile_pool(name="xl", bufs=LAG + 4))
         tp = ctx.enter_context(tc.tile_pool(name="tp", bufs=18))
-        tbp = ctx.enter_context(tc.tile_pool(name="tbp", bufs=4))
+        tbp = ctx.enter_context(tc.tile_pool(name="tbp", bufs=8))
         junk = ctx.enter_context(tc.tile_pool(name="junk", bufs=2))
         small = ctx.enter_context(tc.tile_pool(name="small", bufs=3))
-        tq = ctx.enter_context(tc.tile_pool(name="tq", bufs=2))
+        tq = ctx.enter_context(tc.tile_pool(name="tq", bufs=4))
         fin = ctx.enter_context(tc.tile_pool(name="fin", bufs=3))
-        pz = ctx.enter_context(tc.psum_pool(name="pz", bufs=3))
-        pr = ctx.enter_context(tc.psum_pool(name="pr", bufs=3))
+        pz = ctx.enter_context(tc.psum_pool(name="pz", bufs=2))
+        pt = ctx.enter_context(tc.psum_pool(name="pt", bufs=2))
+        pr = ctx.enter_context(tc.psum_pool(name="pr", bufs=2))
         pm = ctx.enter_context(tc.psum_pool(name="pm", bufs=1))
         pu = ctx.enter_context(tc.psum_pool(name="pu", bufs=1))
         ctx.enter_context(tc.manual_schedule())
@@ -210,8 +211,8 @@ def tile_selfprojectiondev_pb_t_kernel(tc, x, o_xi, p_xi, rel_o_xi, out_0, out_1
             mm_x(b, 0, z_ps[:])
             state[("z_ps", b)] = z_ps
 
-        def mm_r(b):
-            r_ps = pr.tile([P, NJ], F32, name="r_ps", tag="r_ps")
+        def mm_r(b, pool=pr, tag="r_ps"):
+            r_ps = pool.tile([P, NJ], F32, name="r_ps", tag=tag)
             mm_x(b, 1, r_ps[:])
             state[("r_ps", b)] = r_ps
 
@@ -345,15 +346,34 @@ def tile_selfprojectiondev_pb_t_kernel(tc, x, o_xi, p_xi, rel_o_xi, out_0, out_1
             state[("tb", b)] = tb
             small_step()
 
+        def offsets(c, n):
+            mom, rstd, end = state[("st", c)]
+            flush(end)
+            off = small.tile([P, W], F32, name="off")
+            nc.vector.scalar_tensor_tensor(
+                out=off[:, 0:n], in0=mom[:, 0, 0:n], scalar=-1.0, in1=rstd[:, 0:n],
+                op0=ALU.mult, op1=ALU.mult,
+            )
+            state[("off", c)] = off
+
+        def affine_s(b):
+            g, k = group_of[b]
+            tb = tbp.tile([P, NJ], BF16, align_bytes=64, name="tb")
+            nc.scalar.activation(
+                out=tb[:], in_=state[("t_raw", b)][:], func=ACT.Identity,
+                bias=state[("off", g)][:, k : k + 1], scale=state[("st", g)][1][:, k : k + 1],
+            )
+            state[("tb", b)] = tb
+
         def flip(b):
             if b % 2 == 0:
-                state[("tp", b // 2)] = pz.tile([P, 2, 2, P], F32, name="tp_ps", tag="z_ps")
+                state[("tp", b // 2)] = pt.tile([P, 2, 2, P], F32, name="tp_ps", tag="tp_ps")
             tp_ps = state[("tp", b // 2)]
             words = state[("tb", b)][:].bitcast(F32)
             for u in range(2):
                 nc.tensor.transpose(out=tp_ps[:, b % 2, u, :], in_=words[:, u : NJ // 2 : 2], identity=ident[:])
 
-        def gather(pair):
+        def gather(pair, engine_copy):
             q = pair // 2
             h = 2 * (pair % 2)
             if h == 0:
@@ -365,7 +385,7 @@ def tile_selfprojectiondev_pb_t_kernel(tc, x, o_xi, p_xi, rel_o_xi, out_0, out_1
             tg = state[("tg", q)][0]
             dst = tg[:, :, h : h + 2].rearrange("p d b c t -> p d b (c t)").bitcast(F32)
             src = state[("tp", pair)]
-            nc.scalar.copy(
+            engine_copy(
                 out=dst.rearrange("p d b (c u) -> p b d c u", u=2),
                 in_=src[:].rearrange("p b u (d c) -> p b d c u", d=ND),
             )
@@ -388,7 +408,8 @@ def tile_selfprojectiondev_pb_t_kernel(tc, x, o_xi, p_xi, rel_o_xi, out_0, out_1
             tg, t_codes, t_plane = state[("tg", q)]
             n, k = unit_of[q]
             if k == 0:
-                state[("u_ps", n)] = pu.tile([P, 2, P], F32, name="u_ps")
+                pool, tag = (pr, "r_ps") if n == len(UNITS) - 1 else (pu, "u_ps")
+                state[("u_ps", n)] = pool.tile([P, 3, P], F32, name="u_ps", tag=tag)
             u_ps = state[("u_ps", n)]
             for d in range(ND):
                 nc.tensor.matmul_mx(
@@ -411,7 +432,7 @@ def tile_selfprojectiondev_pb_t_kernel(tc, x, o_xi, p_xi, rel_o_xi, out_0, out_1
             nc.scalar.activation(
                 out=flat, in_=state[("u_ps", n)][:, 0:nq, :].rearrange("p k c -> p (k c)"), func=ACT.Tanh
             )
-            usq = fin.tile([P, 8, NW], F32, name="usq")
+            usq = fin.tile([P, 12, NW], F32, name="usq")
             nc.scalar.activation(
                 out=usq[:, 0 : 4 * nq].rearrange("p b c -> p (b c)"), in_=flat, func=ACT.Square
             )
@@ -419,7 +440,7 @@ def tile_selfprojectiondev_pb_t_kernel(tc, x, o_xi, p_xi, rel_o_xi, out_0, out_1
 
         def s2_sums(n, c, lo):
             nb = 4 * len(UNITS[n])
-            st2 = small.tile([P, 2, 8], F32, name="st2")
+            st2 = small.tile([P, 2, 12], F32, name="st2")
             nc.vector.tensor_reduce(
                 out=st2[:, 0, 0:nb], in_=u_all[:, unit_batches(n), :], axis=AX.X, op=ALU.add
             )
@@ -437,19 +458,33 @@ def tile_selfprojectiondev_pb_t_kernel(tc, x, o_xi, p_xi, rel_o_xi, out_0, out_1
             c, lo = state[("place", n)]
             mom, rstd, end = state[("st", c)]
             flush(end)
-            cen = fin.tile([P, 8, NW], F32, name="cen")
+            cen = fin.tile([P, 12, NW], F32, name="cen")
             nc.vector.tensor_tensor(
                 out=cen[:, 0:nb], in0=u_all[:, bs, :],
                 in1=mom[:, 0, lo : lo + nb].unsqueeze(2).to_broadcast([P, nb, NW]), op=ALU.subtract,
             )
             small_step()
-            res = fin.tile([P, 8, NW], F32, name="res")
+            res = fin.tile([P, 12, NW], F32, name="res")
             nc.vector.tensor_tensor(
                 out=res[:, 0:nb], in0=cen[:, 0:nb],
                 in1=rstd[:, lo : lo + nb].unsqueeze(2).to_broadcast([P, nb, NW]), op=ALU.mult,
             )
             small_step()
             nc.sync.dma_start(out=out_0[bs].rearrange("b d q c -> (d q) b c"), in_=res[:, 0:nb])
+
+        def s2_out_s(n):
+            bs = unit_batches(n)
+            c, lo = state[("place", n)]
+            res = fin.tile([P, 12, NW], F32, name="res")
+            for k in range(4 * len(UNITS[n])):
+                nc.scalar.activation(
+                    out=res[:, k], in_=u_all[:, bs.start + k, :], func=ACT.Identity,
+                    bias=state[("off", c)][:, lo + k : lo + k + 1],
+                    scale=state[("st", c)][1][:, lo + k : lo + k + 1],
+                )
+            nc.scalar.dma_start(
+                out=out_0[bs].rearrange("b d q c -> (d q) b c"), in_=res[:, 0 : 4 * len(UNITS[n])]
+            )
 
         def mass_a():
             nm_ps = pr.tile([P, P], F32, name="nm_ps", tag="r_ps")
@@ -501,22 +536,25 @@ def tile_selfprojectiondev_pb_t_kernel(tc, x, o_xi, p_xi, rel_o_xi, out_0, out_1
         def gathers(batches):
             for b in batches:
                 if b % 2 == 1:
-                    gather(b // 2)
+                    gather(b // 2, nc.scalar.copy)
 
         def softmax_mm(i):
             if on(i - LAG + 1):
-                mm_r(i - LAG + 1)
+                if i < NB - 1:
+                    mm_r(i - LAG + 1)
+                else:
+                    mm_r(i - LAG + 1, pz, "z_ps")
 
         for i in range(-3, NB):
             if i in (9, 17):
                 chain((i - 9) // 8, 8, 0)
             if i == 25:
                 chain(2, 8, 8)
-            if i == 29:
-                chain(3, 4, 0)
             if on(i):
                 tanh1(i)
-            if on(i - LAG - 1):
+            if i == NB - 1:
+                s2_tanh(1)
+            elif on(i - LAG - 1):
                 exp1(i - LAG - 1)
             flips(affine_list(i - 1))
             if on(i + 1):
@@ -551,68 +589,66 @@ def tile_selfprojectiondev_pb_t_kernel(tc, x, o_xi, p_xi, rel_o_xi, out_0, out_1
                 s2_tanh(0)
             if i == 24:
                 s2_sums(0, 2, 8)
-            if i == 31:
-                s2_tanh(1)
 
-        step = [NB]
+        next_max = [NB - LAG]
+        next_exp = [NB - LAG - 2]
 
-        def softmax_step():
-            i = step[0]
-            step[0] = i + 1
-            exp1(i - LAG - 1)
-            softmax_mm(i)
-            if on(i - LAG):
-                row_max(i - LAG)
+        def late_max():
+            b = next_max[0]
+            next_max[0] = b + 1
+            row_max(b)
 
+        def late_exp():
+            b = next_exp[0]
+            next_exp[0] = b + 1
+            exp1(b)
+
+        t_moments(3)
         flips(affine_list(NB - 1))
-        gathers([19, 21, 23])
-        for b in range(24, 28):
-            affine(b)
-        softmax_step()
-        s2_sums(1, 4, 4)
-        t_moments(4)
-        flips(range(24, 28))
-        gathers([25, 27])
+        warm_sqrt()
+        mm_r(29, pz, "z_ps")
+        root_a(3, 8, 0)
+        gathers([21, 23])
+        late_max()
         quant_t(4)
         s2_mm(4)
-        chain(4, 4, 8)
-        softmax_step()
-        small_step(1)
+        root_b(3)
+        for b in range(24, 32):
+            affine(b)
+            flip(b)
+        gathers([25, 27, 29, 31])
+        mm_r(30, pt, "tp_ps")
+        mm_r(31, pt, "tp_ps")
         quant_t(5)
         s2_mm(5)
-        small_step(1)
-        softmax_step()
-        small_step(1)
-        s2_out(0)
-        s2_tanh(2)
-        softmax_step()
-        small_step(1)
+        late_max()
         quant_t(6)
         s2_mm(6)
-        small_step(1)
-        for b in range(28, 32):
-            affine(b)
-        flips(range(28, 32))
-        gathers([29, 31])
-        softmax_step()
-        s2_tanh(3)
-        s2_sums(2, 5, 0)
-        softmax_step()
+        late_exp()
+        late_exp()
+        late_max()
         quant_t(7)
         s2_mm(7)
-        softmax_step()
-        s2_sums(3, 5, 8)
-        s2_tanh(4)
-        softmax_step()
-        s2_out(1)
+        late_exp()
+        late_max()
+        s2_tanh(2)
+        s2_sums(1, 5, 0)
         mass_a()
-        s2_sums(4, 5, 12)
-        softmax_step()
-        root_a(5, 0, 16)
+        s2_out(0)
+        s2_tanh(3)
+        s2_sums(2, 5, 8)
+        late_exp()
+        late_exp()
+        late_exp()
+        warm_sqrt()
+        s2_sums(3, 5, 20)
+        root_a(5, 0, 24)
         mass_b()
         root_b(5)
-        s2_out(4)
-        s2_out(3)
+        offsets(5, 24)
+        s2_out_s(3)
         s2_out(2)
+        s2_out_s(1)
         assert done[0] == len(pending)
-        assert step[0] == NB + LAG + 1
+        assert next_exp[0] == NB
+        assert next_max[0] == NB

@@ -33,7 +33,7 @@ W = 24
 
 
 def s_cols(b):
-    return 104 if b < 15 else 120
+    return 96 if b < 15 else 104
 
 FLOPS = 2 * NB * ND * (2 * NI * NJ * NW + NW * NJ * NW)
 
@@ -603,11 +603,13 @@ def tile_selfprojectiondev_pb_t_kernel(tc, x, o_xi, p_xi, rel_o_xi, out_0, out_1
             next_exp[0] = b + 1
             exp1(b)
 
+        s2_sums(1, 3, 8)
         t_moments(3)
+        s2_out(0)
         flips(affine_list(NB - 1))
         warm_sqrt()
         mm_r(29, pz, "z_ps")
-        root_a(3, 8, 0)
+        root_a(3, 8, 8)
         gathers([21, 23])
         late_max()
         quant_t(4)
@@ -632,23 +634,21 @@ def tile_selfprojectiondev_pb_t_kernel(tc, x, o_xi, p_xi, rel_o_xi, out_0, out_1
         late_exp()
         late_max()
         s2_tanh(2)
-        s2_sums(1, 5, 0)
+        s2_out(1)
         mass_a()
-        s2_out(0)
         s2_tanh(3)
-        s2_sums(2, 5, 8)
+        s2_sums(2, 5, 0)
         late_exp()
         late_exp()
         late_exp()
         warm_sqrt()
-        s2_sums(3, 5, 20)
-        root_a(5, 0, 24)
+        s2_sums(3, 5, 12)
+        root_a(5, 0, 16)
         mass_b()
         root_b(5)
-        offsets(5, 24)
+        offsets(5, 16)
         s2_out_s(3)
         s2_out(2)
-        s2_out_s(1)
         assert done[0] == len(pending)
         assert next_exp[0] == NB
         assert next_max[0] == NB

@@ -33,7 +33,7 @@ W = 24
 
 
 def s_cols(b):
-    return 96 if b < 15 else 104
+    return 104 if b < 15 else 112
 
 FLOPS = 2 * NB * ND * (2 * NI * NJ * NW + NW * NJ * NW)
 
@@ -50,6 +50,7 @@ def tile_selfprojectiondev_pb_t_kernel(tc, x, o_xi, p_xi, rel_o_xi, out_0, out_1
         junk = ctx.enter_context(tc.tile_pool(name="junk", bufs=2))
         small = ctx.enter_context(tc.tile_pool(name="small", bufs=3))
         tq = ctx.enter_context(tc.tile_pool(name="tq", bufs=4))
+        up = ctx.enter_context(tc.tile_pool(name="up", bufs=4))
         fin = ctx.enter_context(tc.tile_pool(name="fin", bufs=3))
         pz = ctx.enter_context(tc.psum_pool(name="pz", bufs=2))
         pt = ctx.enter_context(tc.psum_pool(name="pt", bufs=2))
@@ -82,10 +83,20 @@ def tile_selfprojectiondev_pb_t_kernel(tc, x, o_xi, p_xi, rel_o_xi, out_0, out_1
         for g in range(NB // 2):
             raw = rawp.tile([P, 2, 4, NJ], BF16, name="raw")
             if g == 0:
+                for cols in (slice(0, NJ // 2), slice(NJ // 2, NJ)):
+                    nc.sync.dma_start(
+                        out=raw[:, 0, :, cols],
+                        in_=x[0, :, cols].rearrange("(p t) j -> p t j", t=4),
+                    )
+                nc.sync.dma_start(
+                    out=raw[:, 1].rearrange("p t j -> p (t j)"),
+                    in_=x[1].rearrange("(p t) j -> p (t j)", t=4),
+                )
+            elif g < 2:
                 for bb in range(2):
                     nc.sync.dma_start(
                         out=raw[:, bb].rearrange("p t j -> p (t j)"),
-                        in_=x[bb].rearrange("(p t) j -> p (t j)", t=4),
+                        in_=x[2 * g + bb].rearrange("(p t) j -> p (t j)", t=4),
                     )
             else:
                 nc.sync.dma_start(
@@ -106,7 +117,6 @@ def tile_selfprojectiondev_pb_t_kernel(tc, x, o_xi, p_xi, rel_o_xi, out_0, out_1
         make_identity(nc, ident[:])
         se = const.tile([P, P], F32)
         nc.gpsimd.memset(se[:], 0.0)
-        u_all = const.tile([P, NB, NW], F32)
 
         gw = const.tile([P, 2, ND * NW, 4], BF16, align_bytes=64)
         w_codes = const.tile([P, 2 * P], U32, align_bytes=64)
@@ -127,23 +137,22 @@ def tile_selfprojectiondev_pb_t_kernel(tc, x, o_xi, p_xi, rel_o_xi, out_0, out_1
                 in_=gw[:].rearrange("p s w t -> p (s w t)"),
             )
 
-        gp = const.tile([P, ND, ND * NW, 4], BF16, align_bytes=64)
+        gp = const.tile([P, ND, ND * NW + NW, 4], BF16, align_bytes=64)
+        gp_words = gp[:].rearrange("p d w t -> p (d w t)")
         nc.gpsimd.memset(gp[:], 0.0)
         p_codes = const.tile([P, ND, P], U32, align_bytes=64)
         p_plane = const.tile([P, ND, P], U8, align_bytes=64)
 
         def prep_p_copy():
-            for d in range(ND):
-                nc.vector.tensor_copy(
-                    out=gp[:, d, NW * d : NW * (d + 1), :],
-                    in_=raw_p[:, d].rearrange("p t q -> p q t"),
-                )
+            nc.vector.tensor_copy(
+                out=gp[:, :, 0:NW, :], in_=raw_p[:].rearrange("p d t q -> p d q t")
+            )
 
         def prep_p_quant():
             nc.vector.quantize_mx(
                 out=p_codes[:].rearrange("p d w -> p (d w)").bitcast(FP8X4),
                 scales=p_plane[:].rearrange("p d w -> p (d w)"),
-                in_=gp[:].rearrange("p d w t -> p (d w t)"),
+                in_=gp_words[:, 0 : ND * ND * NW * 4],
             )
 
         state = {}
@@ -175,10 +184,11 @@ def tile_selfprojectiondev_pb_t_kernel(tc, x, o_xi, p_xi, rel_o_xi, out_0, out_1
             grouped = state[("grouped", b)]
             src = raws[b // 2][:, b % 2]
             jv = NJ - s_cols(b)
-            nc.vector.tensor_copy(
-                out=grouped[:, 0:jv, :].rearrange("p (c i) t -> p c t i", i=4),
-                in_=src[:, :, 0:jv].rearrange("p t (c i) -> p c t i", i=4),
-            )
+            for lo, hi in ((0, NJ // 2), (NJ // 2, jv)) if b == 0 else ((0, jv),):
+                nc.vector.tensor_copy(
+                    out=grouped[:, lo:hi, :].rearrange("p (c i) t -> p c t i", i=4),
+                    in_=src[:, :, lo:hi].rearrange("p t (c i) -> p c t i", i=4),
+                )
             small_step()
 
         def quant_x(b):
@@ -427,26 +437,21 @@ def tile_selfprojectiondev_pb_t_kernel(tc, x, o_xi, p_xi, rel_o_xi, out_0, out_1
 
         def s2_tanh(n):
             nq = len(UNITS[n])
-            bs = unit_batches(n)
-            flat = u_all[:, bs, :].rearrange("p b c -> p (b c)")
+            uu = up.tile([P, 2, 12, NW], F32, name="uu")
+            flat = uu[:, 0, 0 : 4 * nq].rearrange("p b c -> p (b c)")
             nc.scalar.activation(
                 out=flat, in_=state[("u_ps", n)][:, 0:nq, :].rearrange("p k c -> p (k c)"), func=ACT.Tanh
             )
-            usq = fin.tile([P, 12, NW], F32, name="usq")
             nc.scalar.activation(
-                out=usq[:, 0 : 4 * nq].rearrange("p b c -> p (b c)"), in_=flat, func=ACT.Square
+                out=uu[:, 1, 0 : 4 * nq].rearrange("p b c -> p (b c)"), in_=flat, func=ACT.Square
             )
-            state[("usq", n)] = usq
+            state[("uu", n)] = uu
 
         def s2_sums(n, c, lo):
             nb = 4 * len(UNITS[n])
             st2 = small.tile([P, 2, 12], F32, name="st2")
             nc.vector.tensor_reduce(
-                out=st2[:, 0, 0:nb], in_=u_all[:, unit_batches(n), :], axis=AX.X, op=ALU.add
-            )
-            small_step()
-            nc.vector.tensor_reduce(
-                out=st2[:, 1, 0:nb], in_=state[("usq", n)][:, 0:nb], axis=AX.X, op=ALU.add
+                out=st2[:, :, 0:nb], in_=state[("uu", n)][:, :, 0:nb], axis=AX.X, op=ALU.add
             )
             small_step()
             moments(c, lo, st2[:, :, 0:nb], blk2)
@@ -460,7 +465,7 @@ def tile_selfprojectiondev_pb_t_kernel(tc, x, o_xi, p_xi, rel_o_xi, out_0, out_1
             flush(end)
             cen = fin.tile([P, 12, NW], F32, name="cen")
             nc.vector.tensor_tensor(
-                out=cen[:, 0:nb], in0=u_all[:, bs, :],
+                out=cen[:, 0:nb], in0=state[("uu", n)][:, 0, 0:nb],
                 in1=mom[:, 0, lo : lo + nb].unsqueeze(2).to_broadcast([P, nb, NW]), op=ALU.subtract,
             )
             small_step()
@@ -478,7 +483,7 @@ def tile_selfprojectiondev_pb_t_kernel(tc, x, o_xi, p_xi, rel_o_xi, out_0, out_1
             res = fin.tile([P, 12, NW], F32, name="res")
             for k in range(4 * len(UNITS[n])):
                 nc.scalar.activation(
-                    out=res[:, k], in_=u_all[:, bs.start + k, :], func=ACT.Identity,
+                    out=res[:, k], in_=state[("uu", n)][:, 0, k], func=ACT.Identity,
                     bias=state[("off", c)][:, lo + k : lo + k + 1],
                     scale=state[("st", c)][1][:, lo + k : lo + k + 1],
                 )
@@ -546,10 +551,6 @@ def tile_selfprojectiondev_pb_t_kernel(tc, x, o_xi, p_xi, rel_o_xi, out_0, out_1
                     mm_r(i - LAG + 1, pz, "z_ps")
 
         for i in range(-3, NB):
-            if i in (9, 17):
-                chain((i - 9) // 8, 8, 0)
-            if i == 25:
-                chain(2, 8, 8)
             if on(i):
                 tanh1(i)
             if i == NB - 1:
@@ -565,12 +566,18 @@ def tile_selfprojectiondev_pb_t_kernel(tc, x, o_xi, p_xi, rel_o_xi, out_0, out_1
             if on(i):
                 square1(i)
             softmax_mm(i)
-            if on(i - LAG):
-                row_max(i - LAG)
+            if i == 24:
+                s2_sums(0, 2, 8)
             if on(i + 3):
                 regroup_v(i + 3)
             if i == -3:
                 prep_w()
+            if i in (8, 16):
+                chain(i // 8 - 1, 8, 0)
+            if i == 24:
+                chain(2, 8, 8)
+            if on(i - LAG):
+                row_max(i - LAG)
             if i == 1:
                 prep_p_copy()
             if on(i):
@@ -587,8 +594,6 @@ def tile_selfprojectiondev_pb_t_kernel(tc, x, o_xi, p_xi, rel_o_xi, out_0, out_1
                 s2_mm((i - 18) // 4)
             if i == 23:
                 s2_tanh(0)
-            if i == 24:
-                s2_sums(0, 2, 8)
 
         next_max = [NB - LAG]
         next_exp = [NB - LAG - 2]

@@ -33,7 +33,7 @@ W = 24
 
 
 def s_cols(b):
-    return 104 if b < 15 else 112
+    return 80 if b < 15 else 88
 
 FLOPS = 2 * NB * ND * (2 * NI * NJ * NW + NW * NJ * NW)
 
@@ -116,7 +116,7 @@ def tile_selfprojectiondev_pb_t_kernel(tc, x, o_xi, p_xi, rel_o_xi, out_0, out_1
         ident = const.tile([P, P], F32)
         make_identity(nc, ident[:])
         se = const.tile([P, P], F32)
-        nc.gpsimd.memset(se[:], 0.0)
+        nc.vector.memset(se[:], 0.0)
 
         gw = const.tile([P, 2, ND * NW, 4], BF16, align_bytes=64)
         w_codes = const.tile([P, 2 * P], U32, align_bytes=64)
@@ -139,7 +139,7 @@ def tile_selfprojectiondev_pb_t_kernel(tc, x, o_xi, p_xi, rel_o_xi, out_0, out_1
 
         gp = const.tile([P, ND, ND * NW + NW, 4], BF16, align_bytes=64)
         gp_words = gp[:].rearrange("p d w t -> p (d w t)")
-        nc.gpsimd.memset(gp[:], 0.0)
+        nc.vector.memset(gp[:], 0.0)
         p_codes = const.tile([P, ND, P], U32, align_bytes=64)
         p_plane = const.tile([P, ND, P], U8, align_bytes=64)
 

@@ -33,7 +33,7 @@ W = 24
 
 
 def s_cols(b):
-    return 80 if b < 15 else 88
+    return 104 if b < 15 else 104
 
 FLOPS = 2 * NB * ND * (2 * NI * NJ * NW + NW * NJ * NW)
 
@@ -71,10 +71,11 @@ def tile_selfprojectiondev_pb_t_kernel(tc, x, o_xi, p_xi, rel_o_xi, out_0, out_1
             in_=rel_o_xi.rearrange("d (p t) c -> p d (t c)", t=4),
         )
         raw_p = const.tile([P, ND, 4, NW], BF16)
-        nc.scalar.dma_start(
-            out=raw_p[:].rearrange("p d t c -> p d (t c)"),
-            in_=p_xi.rearrange("d (p t) c -> p d (t c)", t=4),
-        )
+        for u in range(2):
+            nc.scalar.dma_start(
+                out=raw_p[:, :, 2 * u : 2 * u + 2, :].rearrange("p d e q -> p d (e q)"),
+                in_=p_xi[:, 2 * P * u : 2 * P * (u + 1), :].rearrange("d (p e) q -> p d (e q)", e=2),
+            )
 
         warm = const.tile([P, 1], F32)
         nc.scalar.activation(out=warm[:], in_=nm[:, 0:1], func=ACT.Exp)
@@ -381,7 +382,7 @@ def tile_selfprojectiondev_pb_t_kernel(tc, x, o_xi, p_xi, rel_o_xi, out_0, out_1
             tp_ps = state[("tp", b // 2)]
             words = state[("tb", b)][:].bitcast(F32)
             for u in range(2):
-                nc.tensor.transpose(out=tp_ps[:, b % 2, u, :], in_=words[:, u : NJ // 2 : 2], identity=ident[:])
+                nc.tensor.transpose(out=tp_ps[:, b % 2, u, :], in_=words[:, P * u : P * (u + 1)], identity=ident[:])
 
         def gather(pair, engine_copy):
             q = pair // 2
@@ -457,9 +458,8 @@ def tile_selfprojectiondev_pb_t_kernel(tc, x, o_xi, p_xi, rel_o_xi, out_0, out_1
             moments(c, lo, st2[:, :, 0:nb], blk2)
             state[("place", n)] = (c, lo)
 
-        def s2_out(n):
-            bs = unit_batches(n)
-            nb = 4 * len(UNITS[n])
+        def s2_out(n, nb):
+            bs = slice(4 * UNITS[n][0], 4 * UNITS[n][0] + nb)
             c, lo = state[("place", n)]
             mom, rstd, end = state[("st", c)]
             flush(end)
@@ -477,18 +477,20 @@ def tile_selfprojectiondev_pb_t_kernel(tc, x, o_xi, p_xi, rel_o_xi, out_0, out_1
             small_step()
             nc.sync.dma_start(out=out_0[bs].rearrange("b d q c -> (d q) b c"), in_=res[:, 0:nb])
 
-        def s2_out_s(n):
-            bs = unit_batches(n)
-            c, lo = state[("place", n)]
+        def s2_out_s(batches):
             res = fin.tile([P, 12, NW], F32, name="res")
-            for k in range(4 * len(UNITS[n])):
+            for m, b in enumerate(batches):
+                n = unit_of[b // 4][0]
+                k = b - 4 * UNITS[n][0]
+                c, lo = state[("place", n)]
                 nc.scalar.activation(
-                    out=res[:, k], in_=state[("uu", n)][:, 0, k], func=ACT.Identity,
+                    out=res[:, m], in_=state[("uu", n)][:, 0, k], func=ACT.Identity,
                     bias=state[("off", c)][:, lo + k : lo + k + 1],
                     scale=state[("st", c)][1][:, lo + k : lo + k + 1],
                 )
             nc.scalar.dma_start(
-                out=out_0[bs].rearrange("b d q c -> (d q) b c"), in_=res[:, 0 : 4 * len(UNITS[n])]
+                out=out_0[batches[0] : batches[-1] + 1].rearrange("b d q c -> (d q) b c"),
+                in_=res[:, 0 : len(batches)],
             )
 
         def mass_a():
@@ -558,7 +560,7 @@ def tile_selfprojectiondev_pb_t_kernel(tc, x, o_xi, p_xi, rel_o_xi, out_0, out_1
             elif on(i - LAG - 1):
                 exp1(i - LAG - 1)
             flips(affine_list(i - 1))
-            if on(i + 1):
+            if on(i + 1) and i >= 0:
                 quant_x(i + 1)
                 mm_z(i + 1)
             if on(i + 3):
@@ -566,32 +568,34 @@ def tile_selfprojectiondev_pb_t_kernel(tc, x, o_xi, p_xi, rel_o_xi, out_0, out_1
             if on(i):
                 square1(i)
             softmax_mm(i)
+            if i in (18, 22, 26, 30):
+                quant_t((i - 18) // 4)
+                s2_mm((i - 18) // 4)
             if i == 24:
                 s2_sums(0, 2, 8)
             if on(i + 3):
                 regroup_v(i + 3)
             if i == -3:
                 prep_w()
+                quant_x(0)
+                mm_z(0)
             if i in (8, 16):
                 chain(i // 8 - 1, 8, 0)
             if i == 24:
                 chain(2, 8, 8)
             if on(i - LAG):
                 row_max(i - LAG)
-            if i == 1:
+            if i == 8:
                 prep_p_copy()
             if on(i):
                 g, k = group_of[i]
                 if i == GROUPS[g][-1] and i < NB - 1:
                     t_moments(g)
             gathers(affine_list(i - 1))
-            if i == 2:
+            if i == 9:
                 prep_p_quant()
             for b in affine_list(i):
                 affine(b)
-            if i in (18, 22, 26, 30):
-                quant_t((i - 18) // 4)
-                s2_mm((i - 18) // 4)
             if i == 23:
                 s2_tanh(0)
 
@@ -610,7 +614,7 @@ def tile_selfprojectiondev_pb_t_kernel(tc, x, o_xi, p_xi, rel_o_xi, out_0, out_1
 
         s2_sums(1, 3, 8)
         t_moments(3)
-        s2_out(0)
+        s2_out(0, 8)
         flips(affine_list(NB - 1))
         warm_sqrt()
         mm_r(29, pz, "z_ps")
@@ -639,7 +643,7 @@ def tile_selfprojectiondev_pb_t_kernel(tc, x, o_xi, p_xi, rel_o_xi, out_0, out_1
         late_exp()
         late_max()
         s2_tanh(2)
-        s2_out(1)
+        s2_out(1, 8)
         mass_a()
         s2_tanh(3)
         s2_sums(2, 5, 0)
@@ -652,8 +656,8 @@ def tile_selfprojectiondev_pb_t_kernel(tc, x, o_xi, p_xi, rel_o_xi, out_0, out_1
         mass_b()
         root_b(5)
         offsets(5, 16)
-        s2_out_s(3)
-        s2_out(2)
+        s2_out_s(range(24, 32))
+        s2_out(2, 8)
         assert done[0] == len(pending)
         assert next_exp[0] == NB
         assert next_max[0] == NB

@@ -20,20 +20,23 @@ NI = 512
 NJ = 512
 NW = 32
 ND = 4
+PACK = 4
 EPS = 1e-5
-N1 = NJ * NW
-N2 = NW * NW
-ROOT1 = math.sqrt(N1 / (N1 - 1.0))
-ROOT2 = math.sqrt(N2 / (N2 - 1.0))
-MAGIC = float(0x5F3759DF)
-LAG = 4
-GROUPS = [range(8 * g, 8 * g + 8) for g in range(4)]
+N_T = NJ * NW
+N_PROJ = NW * NW
+ROOT_T = math.sqrt(N_T / (N_T - 1.0))
+ROOT_PROJ = math.sqrt(N_PROJ / (N_PROJ - 1.0))
+VAR_FLOOR = 1e-30
+RSQRT_GUESS = float(0x5F3759DF)
+SCALAR_COLS = 96
+RUN = 4
+SOFTMAX_LAG = 4
+T_LAG = 13
+GROUP = 8
+QUAD = 4
 UNITS = [(0, 1), (2, 3), (4, 5, 6), (7,)]
-W = 24
-
-
-def s_cols(b):
-    return 104 if b < 15 else 104
+UNIT_MAX = 12
+STATS = 24
 
 FLOPS = 2 * NB * ND * (2 * NI * NJ * NW + NW * NJ * NW)
 
@@ -42,622 +45,557 @@ def tile_selfprojectiondev_pb_t_kernel(tc, x, o_xi, p_xi, rel_o_xi, out_0, out_1
     nc = tc.nc
     with ExitStack() as ctx:
         const = ctx.enter_context(tc.tile_pool(name="const", bufs=1))
-        rawp = ctx.enter_context(tc.tile_pool(name="rawp", bufs=8))
-        grp = ctx.enter_context(tc.tile_pool(name="grp", bufs=4))
-        xl = ctx.enter_context(tc.tile_pool(name="xl", bufs=LAG + 4))
-        tp = ctx.enter_context(tc.tile_pool(name="tp", bufs=18))
-        tbp = ctx.enter_context(tc.tile_pool(name="tbp", bufs=8))
-        junk = ctx.enter_context(tc.tile_pool(name="junk", bufs=2))
+        load = ctx.enter_context(tc.tile_pool(name="load", bufs=8))
+        regroup = ctx.enter_context(tc.tile_pool(name="regroup", bufs=4))
+        packed_x = ctx.enter_context(tc.tile_pool(name="packed_x", bufs=SOFTMAX_LAG + 4))
+        tanh = ctx.enter_context(tc.tile_pool(name="tanh", bufs=T_LAG + 5))
+        standard = ctx.enter_context(tc.tile_pool(name="standard", bufs=GROUP))
+        unread = ctx.enter_context(tc.tile_pool(name="unread", bufs=2))
         small = ctx.enter_context(tc.tile_pool(name="small", bufs=3))
-        tq = ctx.enter_context(tc.tile_pool(name="tq", bufs=4))
-        up = ctx.enter_context(tc.tile_pool(name="up", bufs=4))
+        packed_t = ctx.enter_context(tc.tile_pool(name="packed_t", bufs=4))
+        proj = ctx.enter_context(tc.tile_pool(name="proj", bufs=len(UNITS)))
         fin = ctx.enter_context(tc.tile_pool(name="fin", bufs=3))
-        pz = ctx.enter_context(tc.psum_pool(name="pz", bufs=2))
-        pt = ctx.enter_context(tc.psum_pool(name="pt", bufs=2))
-        pr = ctx.enter_context(tc.psum_pool(name="pr", bufs=2))
-        pm = ctx.enter_context(tc.psum_pool(name="pm", bufs=1))
-        pu = ctx.enter_context(tc.psum_pool(name="pu", bufs=1))
+        psum_z = ctx.enter_context(tc.psum_pool(name="psum_z", bufs=2))
+        psum_flip = ctx.enter_context(tc.psum_pool(name="psum_flip", bufs=2))
+        psum_r = ctx.enter_context(tc.psum_pool(name="psum_r", bufs=2))
+        psum_mom = ctx.enter_context(tc.psum_pool(name="psum_mom", bufs=1))
+        psum_u = ctx.enter_context(tc.psum_pool(name="psum_u", bufs=1))
         ctx.enter_context(tc.manual_schedule())
 
-        nm = const.tile([P, P], F32)
-        nc.gpsimd.memset(nm[:], 0.0)
-        raw_w = const.tile([P, 2, ND, 4, NW], BF16)
-        nc.scalar.dma_start(
-            out=raw_w[:, 0].rearrange("p d t c -> p d (t c)"),
-            in_=o_xi.rearrange("d (p t) c -> p d (t c)", t=4),
-        )
-        nc.scalar.dma_start(
-            out=raw_w[:, 1].rearrange("p d t c -> p d (t c)"),
-            in_=rel_o_xi.rearrange("d (p t) c -> p d (t c)", t=4),
-        )
-        raw_p = const.tile([P, ND, 4, NW], BF16)
+        neg_max = const.tile([P, P], F32)
+        nc.gpsimd.memset(neg_max[:], 0.0)
+        exp_sum = const.tile([P, P], F32)
+        nc.vector.memset(exp_sum[:], 0.0)
+
+        raw_w = const.tile([P, 2, ND, PACK, NW], BF16)
+        for s, w in enumerate((o_xi, rel_o_xi)):
+            nc.scalar.dma_start(
+                out=raw_w[:, s].rearrange("p d t c -> p d (t c)"),
+                in_=w.rearrange("d (p t) c -> p d (t c)", t=PACK),
+            )
+        raw_p = const.tile([P, ND, PACK, NW], BF16)
         for u in range(2):
             nc.scalar.dma_start(
                 out=raw_p[:, :, 2 * u : 2 * u + 2, :].rearrange("p d e q -> p d (e q)"),
                 in_=p_xi[:, 2 * P * u : 2 * P * (u + 1), :].rearrange("d (p e) q -> p d (e q)", e=2),
             )
 
-        warm = const.tile([P, 1], F32)
-        nc.scalar.activation(out=warm[:], in_=nm[:, 0:1], func=ACT.Exp)
+        scratch = const.tile([P, 1], F32)
+
+        def load_table(func):
+            nc.scalar.activation(out=scratch[:], in_=neg_max[:, P - 1 : P], func=func)
+
+        load_table(ACT.Exp)
 
         raws = []
         for g in range(NB // 2):
-            raw = rawp.tile([P, 2, 4, NJ], BF16, name="raw")
-            if g == 0:
-                for cols in (slice(0, NJ // 2), slice(NJ // 2, NJ)):
-                    nc.sync.dma_start(
-                        out=raw[:, 0, :, cols],
-                        in_=x[0, :, cols].rearrange("(p t) j -> p t j", t=4),
-                    )
-                nc.sync.dma_start(
-                    out=raw[:, 1].rearrange("p t j -> p (t j)"),
-                    in_=x[1].rearrange("(p t) j -> p (t j)", t=4),
-                )
-            elif g < 2:
-                for bb in range(2):
-                    nc.sync.dma_start(
-                        out=raw[:, bb].rearrange("p t j -> p (t j)"),
-                        in_=x[2 * g + bb].rearrange("(p t) j -> p (t j)", t=4),
-                    )
-            else:
-                nc.sync.dma_start(
-                    out=raw[:].rearrange("p b t j -> p b (t j)"),
-                    in_=x[2 * g : 2 * g + 2].rearrange("b (p t) j -> p b (t j)", t=4),
-                )
+            raw = load.tile([P, 2, PACK, NJ], BF16, name="raw")
             raws.append(raw)
+            if g >= 2:
+                nc.sync.dma_start(
+                    out=raw[:].rearrange("p h t j -> p h (t j)"),
+                    in_=x[2 * g : 2 * g + 2].rearrange("h (p t) j -> p h (t j)", t=PACK),
+                )
+                continue
+            for h in range(2):
+                b = 2 * g + h
+                width = NJ // 2 if b == 0 else NJ
+                for lo in range(0, NJ, width):
+                    nc.sync.dma_start(
+                        out=raw[:, h, :, lo : lo + width],
+                        in_=x[b, :, lo : lo + width].rearrange("(p t) j -> p t j", t=PACK),
+                    )
 
-        blk1 = const.tile([P, P], F32)
-        nc.gpsimd.memset(blk1[:], 0.0)
-        blk2 = const.tile([P, P], F32)
-        nc.gpsimd.memset(blk2[:], 0.0)
+        mean_t = const.tile([P, P], F32)
+        nc.gpsimd.memset(mean_t[:], 0.0)
+        mean_proj = const.tile([P, P], F32)
+        nc.gpsimd.memset(mean_proj[:], 0.0)
         for d in range(ND):
             rows = slice(NW * d, NW * (d + 1))
-            nc.gpsimd.memset(blk1[rows, rows], 1.0 / N1)
-            nc.gpsimd.memset(blk2[rows, rows], 1.0 / N2)
+            nc.gpsimd.memset(mean_t[rows, rows], 1.0 / N_T)
+            nc.gpsimd.memset(mean_proj[rows, rows], 1.0 / N_PROJ)
         ident = const.tile([P, P], F32)
         make_identity(nc, ident[:])
-        se = const.tile([P, P], F32)
-        nc.vector.memset(se[:], 0.0)
 
-        gw = const.tile([P, 2, ND * NW, 4], BF16, align_bytes=64)
+        w_grouped = const.tile([P, 2, ND * NW, PACK], BF16, align_bytes=64)
         w_codes = const.tile([P, 2 * P], U32, align_bytes=64)
-        w_plane = const.tile([P, 2 * P], U8, align_bytes=64)
+        w_scales = const.tile([P, 2 * P], U8, align_bytes=64)
 
-        def prep_w():
-            nc.scalar.copy(
-                out=gw[:, 0].rearrange("p (d c) t -> p d c t", d=ND),
-                in_=raw_w[:, 0].rearrange("p d t c -> p d c t"),
-            )
-            nc.vector.tensor_copy(
-                out=gw[:, 1].rearrange("p (d c) t -> p d c t", d=ND),
-                in_=raw_w[:, 1].rearrange("p d t c -> p d c t"),
-            )
+        def pack_w():
+            for s, copy in enumerate((nc.scalar.copy, nc.vector.tensor_copy)):
+                copy(
+                    out=w_grouped[:, s].rearrange("p (d c) t -> p d c t", d=ND),
+                    in_=raw_w[:, s].rearrange("p d t c -> p d c t"),
+                )
             nc.vector.quantize_mx(
                 out=w_codes[:].bitcast(FP8X4),
-                scales=w_plane[:],
-                in_=gw[:].rearrange("p s w t -> p (s w t)"),
+                scales=w_scales[:],
+                in_=w_grouped[:].rearrange("p s w t -> p (s w t)"),
             )
 
-        gp = const.tile([P, ND, ND * NW + NW, 4], BF16, align_bytes=64)
-        gp_words = gp[:].rearrange("p d w t -> p (d w t)")
-        nc.vector.memset(gp[:], 0.0)
-        p_codes = const.tile([P, ND, P], U32, align_bytes=64)
-        p_plane = const.tile([P, ND, P], U8, align_bytes=64)
+        p_grouped = const.tile([P, ND * NW, PACK], BF16, align_bytes=64)
+        p_codes = const.tile([P, P], U32, align_bytes=64)
+        p_scales = const.tile([P, P], U8, align_bytes=64)
+        p_wide = const.tile([P, ND * (P + NW)], U32, align_bytes=64)
+        nc.vector.memset(p_wide[:].bitcast(I32), 0)
+        p_wide_scales = const.tile([P, ND * (P + NW)], U8, align_bytes=64)
+        nc.vector.memset(p_wide_scales[:].bitcast(I32), 0)
 
-        def prep_p_copy():
+        def group_p():
             nc.vector.tensor_copy(
-                out=gp[:, :, 0:NW, :], in_=raw_p[:].rearrange("p d t q -> p d q t")
+                out=p_grouped[:].rearrange("p (d q) t -> p d q t", d=ND),
+                in_=raw_p[:].rearrange("p d t q -> p d q t"),
             )
 
-        def prep_p_quant():
+        def pack_p():
             nc.vector.quantize_mx(
-                out=p_codes[:].rearrange("p d w -> p (d w)").bitcast(FP8X4),
-                scales=p_plane[:].rearrange("p d w -> p (d w)"),
-                in_=gp_words[:, 0 : ND * ND * NW * 4],
+                out=p_codes[:].bitcast(FP8X4),
+                scales=p_scales[:],
+                in_=p_grouped[:].rearrange("p w t -> p (w t)"),
             )
+
+        def spread_p():
+            for wide, narrow in (
+                (p_wide[:].bitcast(I32), p_codes[:].bitcast(I32)),
+                (p_wide_scales[:], p_scales[:]),
+            ):
+                nc.vector.tensor_copy(
+                    out=wide.rearrange("p (d w) -> p d w", d=ND)[:, :, 0:NW],
+                    in_=narrow.rearrange("p (d q) -> p d q", d=ND),
+                )
 
         state = {}
         pending = []
-        done = [0]
+        written = [0]
 
-        def small_step(count=1):
-            for n in range(count):
-                if done[0] < len(pending):
-                    pending[done[0]]()
-                    done[0] = done[0] + 1
+        def small_step():
+            if written[0] < len(pending):
+                pending[written[0]]()
+                written[0] = written[0] + 1
 
-        def flush(upto):
-            for n in range(len(pending)):
-                if done[0] < upto:
-                    small_step()
+        def finish_chain(end):
+            for n in range(end - written[0]):
+                small_step()
 
-        def regroup_s(b):
-            grouped = grp.tile([P, NJ, 4], BF16, align_bytes=64, name="grouped")
-            state[("grouped", b)] = grouped
-            src = raws[b // 2][:, b % 2]
-            jv = NJ - s_cols(b)
-            nc.scalar.copy(
-                out=grouped[:, jv:NJ, :].rearrange("p (c i) t -> p c t i", i=4),
-                in_=src[:, :, jv:NJ].rearrange("p t (c i) -> p c t i", i=4),
+        def regroup_columns(b, copy, lo, hi):
+            copy(
+                out=state[("grouped", b)][:, lo:hi, :].rearrange("p (c i) t -> p c t i", i=RUN),
+                in_=raws[b // 2][:, b % 2, :, lo:hi].rearrange("p t (c i) -> p c t i", i=RUN),
             )
 
-        def regroup_v(b):
-            grouped = state[("grouped", b)]
-            src = raws[b // 2][:, b % 2]
-            jv = NJ - s_cols(b)
-            for lo, hi in ((0, NJ // 2), (NJ // 2, jv)) if b == 0 else ((0, jv),):
-                nc.vector.tensor_copy(
-                    out=grouped[:, lo:hi, :].rearrange("p (c i) t -> p c t i", i=4),
-                    in_=src[:, :, lo:hi].rearrange("p t (c i) -> p c t i", i=4),
-                )
+        def regroup_scalar(b):
+            state[("grouped", b)] = regroup.tile([P, NJ, PACK], BF16, align_bytes=64, name="grouped")
+            regroup_columns(b, nc.scalar.copy, NJ - SCALAR_COLS, NJ)
+
+        def regroup_vector(b):
+            cuts = (0, NJ // 2, NJ - SCALAR_COLS) if b == 0 else (0, NJ - SCALAR_COLS)
+            for lo, hi in zip(cuts, cuts[1:]):
+                regroup_columns(b, nc.vector.tensor_copy, lo, hi)
             small_step()
 
-        def quant_x(b):
-            grouped = state[("grouped", b)]
-            codes = xl.tile([P, NJ], U32, align_bytes=64, name="codes")
-            plane = xl.tile([P, NJ], U8, align_bytes=64, name="plane")
+        def pack_x(b):
+            codes = packed_x.tile([P, NJ], U32, align_bytes=64, name="codes")
+            scales = packed_x.tile([P, NJ], U8, align_bytes=64, name="scales")
             nc.vector.quantize_mx(
                 out=codes[:].bitcast(FP8X4),
-                scales=plane[:],
-                in_=grouped[:].rearrange("p j t -> p (j t)"),
+                scales=scales[:],
+                in_=state[("grouped", b)][:].rearrange("p j t -> p (j t)"),
             )
-            state[("xq", b)] = (codes, plane)
+            state[("x", b)] = (codes, scales)
             small_step()
 
-        def mm_x(b, which, out):
-            codes, plane = state[("xq", b)]
-            cols = slice(which * P, (which + 1) * P)
+        def multiply_x(b, s, pool, tag):
+            codes, scales = state[("x", b)]
+            cols = slice(s * P, (s + 1) * P)
+            out = pool.tile([P, NJ], F32, name="product", tag=tag)
             nc.tensor.matmul_mx(
-                out=out,
+                out=out[:],
                 lhsT=w_codes[:, cols].bitcast(FP8X4),
-                lhsT_scale=w_plane[:, cols],
+                lhsT_scale=w_scales[:, cols],
                 rhs=codes[:].bitcast(FP8X4),
-                rhs_scale=plane[:],
+                rhs_scale=scales[:],
                 start=True,
                 stop=True,
             )
+            state[(("z", "r")[s], b)] = out
 
-        def mm_z(b):
-            z_ps = pz.tile([P, NJ], F32, name="z_ps", tag="z_ps")
-            mm_x(b, 0, z_ps[:])
-            state[("z_ps", b)] = z_ps
+        def multiply_z(b):
+            multiply_x(b, 0, psum_z, "z")
 
-        def mm_r(b, pool=pr, tag="r_ps"):
-            r_ps = pool.tile([P, NJ], F32, name="r_ps", tag=tag)
-            mm_x(b, 1, r_ps[:])
-            state[("r_ps", b)] = r_ps
+        def multiply_r(b, pool, tag):
+            multiply_x(b, 1, pool, tag)
 
         def row_max(b):
-            r_ps = state[("r_ps", b)]
             nc.vector.tensor_reduce(
-                out=nm[:, b : b + 1], in_=r_ps[:], axis=AX.X, op=ALU.max, negate=True
+                out=neg_max[:, b : b + 1], in_=state[("r", b)][:], axis=AX.X, op=ALU.max, negate=True
             )
             small_step()
 
-        group_of = {}
-        for g, members in enumerate(GROUPS):
-            for b in members:
-                group_of[b] = (g, b - members[0])
-
-        def tanh1(b):
-            z_ps = state[("z_ps", b)]
-            g, k = group_of[b]
-            if k == 0:
-                state[("acc", g)] = small.tile([P, 2, 8], F32, name="acc")
-            acc = state[("acc", g)]
-            t_raw = tp.tile([P, NJ], F32, name="t_raw")
-            nc.scalar.activation(out=t_raw[:], in_=z_ps[:], func=ACT.Tanh, accum_out=acc[:, 0, k : k + 1])
-            state[("t_raw", b)] = t_raw
-
-        def square1(b):
-            g, k = group_of[b]
-            sq = junk.tile([P, NJ], BF16, name="sq")
+        def row_exp(b):
+            out = unread.tile([P, NJ], BF16, name="exp")
             nc.scalar.activation(
-                out=sq[:], in_=state[("t_raw", b)][:], func=ACT.Square,
-                accum_out=state[("acc", g)][:, 1, k : k + 1],
+                out=out[:], in_=state[("r", b)][:], func=ACT.Exp, bias=neg_max[:, b : b + 1], scale=1.0,
+                accum_out=exp_sum[:, b : b + 1],
             )
 
-        def exp1(b):
-            r_ps = state[("r_ps", b)]
-            ex = junk.tile([P, NJ], BF16, name="ex")
-            nc.scalar.activation(
-                out=ex[:], in_=r_ps[:], func=ACT.Exp, bias=nm[:, b : b + 1], scale=1.0,
-                accum_out=se[:, b : b + 1],
+        def mass_factors():
+            flipped = psum_r.tile([P, P], F32, name="flipped_max", tag="r")
+            nc.tensor.transpose(out=flipped[:], in_=neg_max[:], identity=ident[:])
+            by_depth = flipped[0:NB, :].rearrange("b (d c) -> b d c", d=ND)
+            least = fin.tile([NB, ND], F32, name="least")
+            nc.vector.tensor_reduce(out=least[:], in_=by_depth, axis=AX.X, op=ALU.min)
+            diff = fin.tile([NB, ND, NW], F32, name="diff")
+            nc.vector.tensor_tensor(
+                out=diff[:], in0=least[:].unsqueeze(2).to_broadcast([NB, ND, NW]), in1=by_depth, op=ALU.subtract
             )
+            factor = fin.tile([NB, ND, NW], F32, name="factor")
+            nc.scalar.activation(out=factor[:], in_=diff[:], func=ACT.Exp)
+            state["factor"] = factor
 
-        def mom_tile(c):
-            if ("mom_ps", c) not in state:
-                state[("mom_ps", c)] = pm.tile([P, 2, W], F32, name="mom_ps")
-            return state[("mom_ps", c)]
+        def mass_out():
+            flipped = psum_r.tile([P, P], F32, name="flipped_sum", tag="r")
+            nc.tensor.transpose(out=flipped[:], in_=exp_sum[:], identity=ident[:])
+            part = fin.tile([NB, ND, NW], F32, name="part")
+            nc.vector.tensor_tensor(
+                out=part[:], in0=state["factor"][:], in1=flipped[0:NB, :].rearrange("b (d c) -> b d c", d=ND),
+                op=ALU.mult,
+            )
+            total = fin.tile([NB, ND], F32, name="total")
+            nc.vector.tensor_reduce(out=total[:], in_=part[:], axis=AX.X, op=ALU.add)
+            inverse = fin.tile([NB, ND], F32, name="inverse")
+            nc.vector.reciprocal(out=inverse[:], in_=total[:])
+            mass = fin.tile([NB, ND, NW], F32, name="mass")
+            nc.vector.tensor_tensor(
+                out=mass[:], in0=part[:], in1=inverse[:].unsqueeze(2).to_broadcast([NB, ND, NW]), op=ALU.mult
+            )
+            nc.sync.dma_start(out=out_1, in_=mass[:])
 
-        def moments(c, lo, sums, blk):
-            width = sums.shape[2]
+        def moments(chain, lo, sums, average):
+            if ("moments", chain) not in state:
+                state[("moments", chain)] = psum_mom.tile([P, 2, STATS], F32, name="moments")
             nc.tensor.matmul(
-                out=mom_tile(c)[:, :, lo : lo + width], lhsT=blk[:], rhs=sums, start=True, stop=True
+                out=state[("moments", chain)][:, :, lo : lo + sums.shape[2]],
+                lhsT=average[:], rhs=sums, start=True, stop=True,
             )
 
-        def t_moments(g):
-            moments(g, 0, state[("acc", g)][:, :, 0 : len(GROUPS[g])], blk1)
-
-        def chain_tiles(c):
-            mom = small.tile([P, 2, W], F32, name="mom")
-            var = small.tile([P, W], F32, name="var")
-            tmp = small.tile([P, W], F32, name="tmp")
-            rstd = small.tile([P, W], F32, name="rstd")
-            return mom, var, tmp, rstd
-
-        def chain(c, n1, n2):
-            mom_ps = mom_tile(c)
-            mom, var, tmp, rstd = chain_tiles(c)
-            guess = small.tile([P, W], I32, name="guess")
-            cs = slice(0, n1 + n2)
-            y = guess[:, cs].bitcast(F32)
-            v = var[:, cs]
-            w = tmp[:, cs]
-            tt = nc.vector.tensor_tensor
-            ts = nc.vector.tensor_scalar
-            stt = nc.vector.scalar_tensor_tensor
+        def variances(chain, n):
+            mom = small.tile([P, 2, STATS], F32, name="mom")
+            var = small.tile([P, STATS], F32, name="var")
+            tmp = small.tile([P, STATS], F32, name="tmp")
+            rstd = small.tile([P, STATS], F32, name="rstd")
+            cols = slice(0, n)
+            mean, var_n, tmp_n = mom[:, 0, cols], var[:, cols], tmp[:, cols]
+            source = state[("moments", chain)][:, :, cols]
             ops = [
-                lambda: nc.vector.tensor_copy(out=mom[:, :, cs], in_=mom_ps[:, :, cs]),
-                lambda: tt(out=w, in0=mom[:, 0, cs], in1=mom[:, 0, cs], op=ALU.mult),
-                lambda: tt(out=v, in0=mom[:, 1, cs], in1=w, op=ALU.subtract),
-                lambda: ts(out=v, in0=v, scalar1=1e-30, scalar2=None, op0=ALU.max),
-                lambda: ts(out=guess[:, cs], in0=v.bitcast(I32), scalar1=-0.5, scalar2=MAGIC,
-                           op0=ALU.mult, op1=ALU.add),
+                lambda: nc.vector.tensor_copy(out=mom[:, :, cols], in_=source),
+                lambda: nc.vector.tensor_tensor(out=tmp_n, in0=mean, in1=mean, op=ALU.mult),
+                lambda: nc.vector.tensor_tensor(out=var_n, in0=mom[:, 1, cols], in1=tmp_n, op=ALU.subtract),
+                lambda: nc.vector.tensor_scalar(
+                    out=var_n, in0=var_n, scalar1=VAR_FLOOR, scalar2=None, op0=ALU.max
+                ),
             ]
-            for n in range(3):
+            return ops, mom, var_n, tmp, rstd
+
+        def inverses(tmp, rstd, n_t, n_proj):
+            n = n_t + n_proj
+            ops = [
+                lambda lo=lo, hi=hi, root=root: nc.vector.tensor_scalar(
+                    out=tmp[:, lo:hi], in0=tmp[:, lo:hi], scalar1=root, scalar2=EPS, op0=ALU.mult, op1=ALU.add
+                )
+                for lo, hi, root in ((0, n_t, ROOT_T), (n_t, n, ROOT_PROJ))
+                if lo < hi
+            ]
+            ops.append(lambda: nc.vector.reciprocal(out=rstd[:, 0:n], in_=tmp[:, 0:n]))
+            return ops
+
+        def newton_chain(chain, n_t, n_proj):
+            n = n_t + n_proj
+            ops, mom, var, tmp, rstd = variances(chain, n)
+            guess = small.tile([P, STATS], I32, name="guess")
+            y, tmp_n = guess[:, 0:n].bitcast(F32), tmp[:, 0:n]
+            stt = nc.vector.scalar_tensor_tensor
+            ops.append(lambda: nc.vector.tensor_scalar(
+                out=guess[:, 0:n], in0=var.bitcast(I32), scalar1=-0.5, scalar2=RSQRT_GUESS,
+                op0=ALU.mult, op1=ALU.add,
+            ))
+            for n_step in range(3):
                 ops.extend([
-                    lambda: tt(out=w, in0=y, in1=y, op=ALU.mult),
-                    lambda: stt(out=w, in0=w, scalar=-0.5, in1=v, op0=ALU.mult, op1=ALU.mult),
-                    lambda: stt(out=y, in0=w, scalar=1.5, in1=y, op0=ALU.add, op1=ALU.mult),
+                    lambda: nc.vector.tensor_tensor(out=tmp_n, in0=y, in1=y, op=ALU.mult),
+                    lambda: stt(out=tmp_n, in0=tmp_n, scalar=-0.5, in1=var, op0=ALU.mult, op1=ALU.mult),
+                    lambda: stt(out=y, in0=tmp_n, scalar=1.5, in1=y, op0=ALU.add, op1=ALU.mult),
                 ])
-            ops.append(lambda: tt(out=w, in0=v, in1=y, op=ALU.mult))
-            if n1:
-                ops.append(lambda: ts(out=tmp[:, 0:n1], in0=tmp[:, 0:n1], scalar1=ROOT1, scalar2=EPS,
-                                      op0=ALU.mult, op1=ALU.add))
-            if n2:
-                ops.append(lambda: ts(out=tmp[:, n1 : n1 + n2], in0=tmp[:, n1 : n1 + n2], scalar1=ROOT2,
-                                      scalar2=EPS, op0=ALU.mult, op1=ALU.add))
-            ops.append(lambda: nc.vector.reciprocal(out=rstd[:, cs], in_=w))
-            pending.extend(ops)
-            state[("st", c)] = (mom, rstd, len(pending))
+            ops.append(lambda: nc.vector.tensor_tensor(out=tmp_n, in0=var, in1=y, op=ALU.mult))
+            pending.extend(ops + inverses(tmp, rstd, n_t, n_proj))
+            state[("chain", chain)] = (mom, rstd, len(pending))
 
-        def root_a(c, n1, n2):
-            mom_ps = mom_tile(c)
-            mom, var, tmp, rstd = chain_tiles(c)
-            cs = slice(0, n1 + n2)
-            nc.vector.tensor_copy(out=mom[:, :, cs], in_=mom_ps[:, :, cs])
-            nc.vector.tensor_tensor(out=tmp[:, cs], in0=mom[:, 0, cs], in1=mom[:, 0, cs], op=ALU.mult)
-            nc.vector.tensor_tensor(out=var[:, cs], in0=mom[:, 1, cs], in1=tmp[:, cs], op=ALU.subtract)
-            nc.vector.tensor_scalar(out=var[:, cs], in0=var[:, cs], scalar1=1e-30, scalar2=None, op0=ALU.max)
-            nc.scalar.activation(out=tmp[:, cs], in_=var[:, cs], func=ACT.Sqrt)
-            state[("st", c)] = (mom, rstd, len(pending))
-            state[("root", c)] = (tmp, rstd, n1, n2)
+        def root_chain_begin(chain, n_t, n_proj):
+            ops, mom, var, tmp, rstd = variances(chain, n_t + n_proj)
+            for op in ops:
+                op()
+            nc.scalar.activation(out=tmp[:, 0 : n_t + n_proj], in_=var, func=ACT.Sqrt)
+            state[("rest", chain)] = inverses(tmp, rstd, n_t, n_proj)
+            state[("chain", chain)] = (mom, rstd, len(pending))
 
-        def root_b(c):
-            tmp, rstd, n1, n2 = state[("root", c)]
-            cs = slice(0, n1 + n2)
-            for root, lo, hi in ((ROOT1, 0, n1), (ROOT2, n1, n1 + n2)):
-                if lo < hi:
-                    nc.vector.tensor_scalar(
-                        out=tmp[:, lo:hi], in0=tmp[:, lo:hi], scalar1=root, scalar2=EPS,
-                        op0=ALU.mult, op1=ALU.add,
-                    )
-            nc.vector.reciprocal(out=rstd[:, cs], in_=tmp[:, cs])
+        def root_chain_end(chain):
+            for op in state[("rest", chain)]:
+                op()
 
-        def affine(b):
-            g, k = group_of[b]
-            mom, rstd, end = state[("st", g)]
-            flush(end)
-            tb = tbp.tile([P, NJ], BF16, align_bytes=64, name="tb")
-            nc.vector.tensor_scalar(
-                out=tb[:], in0=state[("t_raw", b)][:], scalar1=mom[:, 0, k : k + 1],
-                scalar2=rstd[:, k : k + 1], op0=ALU.subtract, op1=ALU.mult,
-            )
-            state[("tb", b)] = tb
-            small_step()
-
-        def offsets(c, n):
-            mom, rstd, end = state[("st", c)]
-            flush(end)
-            off = small.tile([P, W], F32, name="off")
-            nc.vector.scalar_tensor_tensor(
-                out=off[:, 0:n], in0=mom[:, 0, 0:n], scalar=-1.0, in1=rstd[:, 0:n],
-                op0=ALU.mult, op1=ALU.mult,
-            )
-            state[("off", c)] = off
-
-        def affine_s(b):
-            g, k = group_of[b]
-            tb = tbp.tile([P, NJ], BF16, align_bytes=64, name="tb")
+        def tanh_t(b):
+            if b % GROUP == 0:
+                state[("sums", b // GROUP)] = small.tile([P, 2, GROUP], F32, name="sums")
+            t = tanh.tile([P, NJ], F32, name="t")
             nc.scalar.activation(
-                out=tb[:], in_=state[("t_raw", b)][:], func=ACT.Identity,
-                bias=state[("off", g)][:, k : k + 1], scale=state[("st", g)][1][:, k : k + 1],
+                out=t[:], in_=state[("z", b)][:], func=ACT.Tanh,
+                accum_out=state[("sums", b // GROUP)][:, 0, b % GROUP : b % GROUP + 1],
             )
-            state[("tb", b)] = tb
+            state[("t", b)] = t
+
+        def square_t(b):
+            out = unread.tile([P, NJ], BF16, name="square")
+            nc.scalar.activation(
+                out=out[:], in_=state[("t", b)][:], func=ACT.Square,
+                accum_out=state[("sums", b // GROUP)][:, 1, b % GROUP : b % GROUP + 1],
+            )
+
+        def moments_t(g):
+            moments(g, 0, state[("sums", g)][:], mean_t)
+
+        def standardise(b):
+            mom, rstd, end = state[("chain", b // GROUP)]
+            finish_chain(end)
+            col = slice(b % GROUP, b % GROUP + 1)
+            ts = standard.tile([P, NJ], BF16, align_bytes=64, name="ts")
+            nc.vector.tensor_scalar(
+                out=ts[:], in0=state[("t", b)][:], scalar1=mom[:, 0, col], scalar2=rstd[:, col],
+                op0=ALU.subtract, op1=ALU.mult,
+            )
+            state[("ts", b)] = ts
+            small_step()
 
         def flip(b):
             if b % 2 == 0:
-                state[("tp", b // 2)] = pt.tile([P, 2, 2, P], F32, name="tp_ps", tag="tp_ps")
-            tp_ps = state[("tp", b // 2)]
-            words = state[("tb", b)][:].bitcast(F32)
+                state[("flipped", b // 2)] = psum_flip.tile([P, 2, 2, P], F32, name="flipped", tag="flipped")
+            words = state[("ts", b)][:].bitcast(F32)
             for u in range(2):
-                nc.tensor.transpose(out=tp_ps[:, b % 2, u, :], in_=words[:, P * u : P * (u + 1)], identity=ident[:])
+                nc.tensor.transpose(
+                    out=state[("flipped", b // 2)][:, b % 2, u, :], in_=words[:, P * u : P * (u + 1)],
+                    identity=ident[:],
+                )
 
-        def gather(pair, engine_copy):
-            q = pair // 2
-            h = 2 * (pair % 2)
+        def gather(b):
+            quad, h = b // QUAD, b % QUAD - 1
             if h == 0:
-                state[("tg", q)] = (
-                    tq.tile([P, ND, 4, NW, 4], BF16, align_bytes=64, name="tg"),
-                    tq.tile([P, ND, P], U32, align_bytes=64, name="t_codes"),
-                    tq.tile([P, ND, P], U8, align_bytes=64, name="t_plane"),
+                state[("quad", quad)] = (
+                    packed_t.tile([P, ND, QUAD, NW, PACK], BF16, align_bytes=64, name="grouped_t"),
+                    packed_t.tile([P, ND * P], U32, align_bytes=64, name="codes_t"),
+                    packed_t.tile([P, ND * P], U8, align_bytes=64, name="scales_t"),
                 )
-            tg = state[("tg", q)][0]
-            dst = tg[:, :, h : h + 2].rearrange("p d b c t -> p d b (c t)").bitcast(F32)
-            src = state[("tp", pair)]
-            engine_copy(
-                out=dst.rearrange("p d b (c u) -> p b d c u", u=2),
-                in_=src[:].rearrange("p b u (d c) -> p b d c u", d=ND),
+            grouped = state[("quad", quad)][0]
+            nc.scalar.copy(
+                out=grouped[:, :, h : h + 2].rearrange("p d b c t -> p d b (c t)").bitcast(F32)
+                .rearrange("p d b (c u) -> p b d c u", u=2),
+                in_=state[("flipped", b // 2)][:].rearrange("p b u (d c) -> p b d c u", d=ND),
             )
-
-        def quant_t(q):
-            tg, t_codes, t_plane = state[("tg", q)]
-            nc.vector.quantize_mx(
-                out=t_codes[:].rearrange("p d w -> p (d w)").bitcast(FP8X4),
-                scales=t_plane[:].rearrange("p d w -> p (d w)"),
-                in_=tg[:].rearrange("p d b c t -> p (d b c t)"),
-            )
-            small_step()
-
-        unit_of = {}
-        for n, quads in enumerate(UNITS):
-            for k, q in enumerate(quads):
-                unit_of[q] = (n, k)
-
-        def s2_mm(q):
-            tg, t_codes, t_plane = state[("tg", q)]
-            n, k = unit_of[q]
-            if k == 0:
-                pool, tag = (pr, "r_ps") if n == len(UNITS) - 1 else (pu, "u_ps")
-                state[("u_ps", n)] = pool.tile([P, 3, P], F32, name="u_ps", tag=tag)
-            u_ps = state[("u_ps", n)]
-            for d in range(ND):
-                nc.tensor.matmul_mx(
-                    out=u_ps[:, k, :],
-                    lhsT=p_codes[:, d].bitcast(FP8X4),
-                    lhsT_scale=p_plane[:, d],
-                    rhs=t_codes[:, d].bitcast(FP8X4),
-                    rhs_scale=t_plane[:, d],
-                    start=(d == 0),
-                    stop=(d == ND - 1),
-                )
-
-        def unit_batches(n):
-            return slice(4 * UNITS[n][0], 4 * UNITS[n][-1] + 4)
-
-        def s2_tanh(n):
-            nq = len(UNITS[n])
-            uu = up.tile([P, 2, 12, NW], F32, name="uu")
-            flat = uu[:, 0, 0 : 4 * nq].rearrange("p b c -> p (b c)")
-            nc.scalar.activation(
-                out=flat, in_=state[("u_ps", n)][:, 0:nq, :].rearrange("p k c -> p (k c)"), func=ACT.Tanh
-            )
-            nc.scalar.activation(
-                out=uu[:, 1, 0 : 4 * nq].rearrange("p b c -> p (b c)"), in_=flat, func=ACT.Square
-            )
-            state[("uu", n)] = uu
-
-        def s2_sums(n, c, lo):
-            nb = 4 * len(UNITS[n])
-            st2 = small.tile([P, 2, 12], F32, name="st2")
-            nc.vector.tensor_reduce(
-                out=st2[:, :, 0:nb], in_=state[("uu", n)][:, :, 0:nb], axis=AX.X, op=ALU.add
-            )
-            small_step()
-            moments(c, lo, st2[:, :, 0:nb], blk2)
-            state[("place", n)] = (c, lo)
-
-        def s2_out(n, nb):
-            bs = slice(4 * UNITS[n][0], 4 * UNITS[n][0] + nb)
-            c, lo = state[("place", n)]
-            mom, rstd, end = state[("st", c)]
-            flush(end)
-            cen = fin.tile([P, 12, NW], F32, name="cen")
-            nc.vector.tensor_tensor(
-                out=cen[:, 0:nb], in0=state[("uu", n)][:, 0, 0:nb],
-                in1=mom[:, 0, lo : lo + nb].unsqueeze(2).to_broadcast([P, nb, NW]), op=ALU.subtract,
-            )
-            small_step()
-            res = fin.tile([P, 12, NW], F32, name="res")
-            nc.vector.tensor_tensor(
-                out=res[:, 0:nb], in0=cen[:, 0:nb],
-                in1=rstd[:, lo : lo + nb].unsqueeze(2).to_broadcast([P, nb, NW]), op=ALU.mult,
-            )
-            small_step()
-            nc.sync.dma_start(out=out_0[bs].rearrange("b d q c -> (d q) b c"), in_=res[:, 0:nb])
-
-        def s2_out_s(batches):
-            res = fin.tile([P, 12, NW], F32, name="res")
-            for m, b in enumerate(batches):
-                n = unit_of[b // 4][0]
-                k = b - 4 * UNITS[n][0]
-                c, lo = state[("place", n)]
-                nc.scalar.activation(
-                    out=res[:, m], in_=state[("uu", n)][:, 0, k], func=ACT.Identity,
-                    bias=state[("off", c)][:, lo + k : lo + k + 1],
-                    scale=state[("st", c)][1][:, lo + k : lo + k + 1],
-                )
-            nc.scalar.dma_start(
-                out=out_0[batches[0] : batches[-1] + 1].rearrange("b d q c -> (d q) b c"),
-                in_=res[:, 0 : len(batches)],
-            )
-
-        def mass_a():
-            nm_ps = pr.tile([P, P], F32, name="nm_ps", tag="r_ps")
-            nc.tensor.transpose(out=nm_ps[:], in_=nm[:], identity=ident[:])
-            nmt = nm_ps[0:NB, :].rearrange("b (d c) -> b d c", d=ND)
-            ntop = fin.tile([NB, ND], F32, name="ntop")
-            nc.vector.tensor_reduce(out=ntop[:], in_=nmt, axis=AX.X, op=ALU.min)
-            diff = fin.tile([NB, ND, NW], F32, name="diff")
-            nc.vector.tensor_tensor(
-                out=diff[:], in0=ntop[:].unsqueeze(2).to_broadcast([NB, ND, NW]), in1=nmt, op=ALU.subtract
-            )
-            corr = fin.tile([NB, ND, NW], F32, name="corr")
-            nc.scalar.activation(out=corr[:], in_=diff[:], func=ACT.Exp)
-            state["mass"] = corr
-
-        def warm_sqrt():
-            nc.scalar.activation(out=warm[:], in_=blk1[:, 0:1], func=ACT.Sqrt)
-
-        def mass_b():
-            corr = state["mass"]
-            se_ps = pr.tile([P, P], F32, name="se_ps", tag="r_ps")
-            nc.tensor.transpose(out=se_ps[:], in_=se[:], identity=ident[:])
-            set_ = se_ps[0:NB, :].rearrange("b (d c) -> b d c", d=ND)
-            part = fin.tile([NB, ND, NW], F32, name="part")
-            nc.vector.tensor_tensor(out=part[:], in0=corr[:], in1=set_, op=ALU.mult)
-            den = fin.tile([NB, ND], F32, name="den")
-            nc.vector.tensor_reduce(out=den[:], in_=part[:], axis=AX.X, op=ALU.add)
-            rden = fin.tile([NB, ND], F32, name="rden")
-            nc.vector.reciprocal(out=rden[:], in_=den[:])
-            mres = fin.tile([NB, ND, NW], F32, name="mres")
-            nc.vector.tensor_tensor(
-                out=mres[:], in0=part[:],
-                in1=rden[:].unsqueeze(2).to_broadcast([NB, ND, NW]), op=ALU.mult,
-            )
-            nc.sync.dma_start(out=out_1, in_=mres[:])
-
-        def on(v):
-            return 0 <= v < NB
-
-        def affine_list(i):
-            if 13 <= i <= 27:
-                return [i - 13]
-            return {28: [15, 16], 29: [17, 18], 30: [19, 20], 31: [21, 22, 23]}.get(i, [])
-
-        def flips(batches):
-            for b in batches:
-                flip(b)
 
         def gathers(batches):
             for b in batches:
                 if b % 2 == 1:
-                    gather(b // 2, nc.scalar.copy)
+                    gather(b)
 
-        def softmax_mm(i):
-            if on(i - LAG + 1):
-                if i < NB - 1:
-                    mm_r(i - LAG + 1)
-                else:
-                    mm_r(i - LAG + 1, pz, "z_ps")
+        def pack_t(quad):
+            grouped, codes, scales = state[("quad", quad)]
+            nc.vector.quantize_mx(
+                out=codes[:].bitcast(FP8X4), scales=scales[:],
+                in_=grouped[:].rearrange("p d b c t -> p (d b c t)"),
+            )
+            small_step()
+
+        place = {quad: (unit, k) for unit, quads in enumerate(UNITS) for k, quad in enumerate(quads)}
+
+        def multiply_u(quad, pool=psum_u, tag="u"):
+            grouped, codes, scales = state[("quad", quad)]
+            unit, k = place[quad]
+            if k == 0:
+                state[("u", unit)] = pool.tile([P, 3, P], F32, name="u", tag=tag)
+            for d in range(ND):
+                cols = slice(P * d, P * (d + 1))
+                nc.tensor.matmul_mx(
+                    out=state[("u", unit)][:, k, :],
+                    lhsT=p_wide[:, cols].bitcast(FP8X4),
+                    lhsT_scale=p_wide_scales[:, cols],
+                    rhs=codes[:, cols].bitcast(FP8X4),
+                    rhs_scale=scales[:, cols],
+                    start=(d == 0),
+                    stop=(d == ND - 1),
+                )
+
+        def tanh_u(unit):
+            quads = len(UNITS[unit])
+            both = proj.tile([P, 2, UNIT_MAX, NW], F32, name="both")
+            flat = [both[:, k, 0 : QUAD * quads].rearrange("p b c -> p (b c)") for k in range(2)]
+            nc.scalar.activation(
+                out=flat[0], in_=state[("u", unit)][:, 0:quads, :].rearrange("p k c -> p (k c)"), func=ACT.Tanh
+            )
+            nc.scalar.activation(out=flat[1], in_=flat[0], func=ACT.Square)
+            state[("both", unit)] = both
+
+        def moments_u(unit, chain, lo):
+            n = QUAD * len(UNITS[unit])
+            sums = small.tile([P, 2, UNIT_MAX], F32, name="sums_u")
+            nc.vector.tensor_reduce(
+                out=sums[:, :, 0:n], in_=state[("both", unit)][:, :, 0:n], axis=AX.X, op=ALU.add
+            )
+            small_step()
+            moments(chain, lo, sums[:, :, 0:n], mean_proj)
+            state[("columns", unit)] = (chain, lo)
+
+        def store_proj(queue, res, first, n):
+            queue.dma_start(
+                out=out_0[first : first + n].rearrange("b d q c -> (d q) b c"), in_=res[:, 0:n]
+            )
+
+        def proj_vector(unit, n):
+            chain, lo = state[("columns", unit)]
+            mom, rstd, end = state[("chain", chain)]
+            finish_chain(end)
+            tanh_of_u = state[("both", unit)][:, 0, 0:n]
+            centred = fin.tile([P, UNIT_MAX, NW], F32, name="centred")
+            nc.vector.tensor_tensor(
+                out=centred[:, 0:n], in0=tanh_of_u,
+                in1=mom[:, 0, lo : lo + n].unsqueeze(2).to_broadcast([P, n, NW]), op=ALU.subtract,
+            )
+            small_step()
+            res = fin.tile([P, UNIT_MAX, NW], F32, name="res")
+            nc.vector.tensor_tensor(
+                out=res[:, 0:n], in0=centred[:, 0:n],
+                in1=rstd[:, lo : lo + n].unsqueeze(2).to_broadcast([P, n, NW]), op=ALU.mult,
+            )
+            small_step()
+            store_proj(nc.sync, res, QUAD * UNITS[unit][0], n)
+
+        def proj_scalar(chain, first, n):
+            mom, rstd, end = state[("chain", chain)]
+            offset = small.tile([P, STATS], F32, name="offset")
+            used = slice(0, sum(QUAD * len(UNITS[unit]) for unit in range(len(UNITS)) if state[("columns", unit)][0] == chain))
+            nc.vector.scalar_tensor_tensor(
+                out=offset[:, used], in0=mom[:, 0, used], scalar=-1.0, in1=rstd[:, used],
+                op0=ALU.mult, op1=ALU.mult,
+            )
+            res = fin.tile([P, UNIT_MAX, NW], F32, name="res")
+            for k in range(n):
+                unit = place[(first + k) // QUAD][0]
+                row = first + k - QUAD * UNITS[unit][0]
+                col = state[("columns", unit)][1] + row
+                nc.scalar.activation(
+                    out=res[:, k], in_=state[("both", unit)][:, 0, row], func=ACT.Identity,
+                    bias=offset[:, col : col + 1], scale=rstd[:, col : col + 1],
+                )
+            store_proj(nc.scalar, res, first, n)
+
+        LAST = NB - 1
+
+        def standardised(i):
+            if i < 28:
+                return [i - T_LAG] if i >= T_LAG else []
+            return {28: [15, 16], 29: [17, 18], 30: [19, 20], 31: [21, 22, 23]}[i]
 
         for i in range(-3, NB):
-            if on(i):
-                tanh1(i)
-            if i == NB - 1:
-                s2_tanh(1)
-            elif on(i - LAG - 1):
-                exp1(i - LAG - 1)
-            flips(affine_list(i - 1))
-            if on(i + 1) and i >= 0:
-                quant_x(i + 1)
-                mm_z(i + 1)
-            if on(i + 3):
-                regroup_s(i + 3)
-            if on(i):
-                square1(i)
-            softmax_mm(i)
-            if i in (18, 22, 26, 30):
-                quant_t((i - 18) // 4)
-                s2_mm((i - 18) // 4)
+            if i >= 0:
+                tanh_t(i)
+            if i == LAST:
+                tanh_u(1)
+            elif i > SOFTMAX_LAG:
+                row_exp(i - SOFTMAX_LAG - 1)
+            before = standardised(i - 1)
+            for b in before:
+                flip(b)
+            if 0 <= i < LAST:
+                pack_x(i + 1)
+                multiply_z(i + 1)
+            if i + 3 < NB:
+                regroup_scalar(i + 3)
+            if i >= 0:
+                square_t(i)
+            if i >= SOFTMAX_LAG - 1:
+                pool, tag = (psum_r, "r") if i < LAST else (psum_z, "z")
+                multiply_r(i - SOFTMAX_LAG + 1, pool, tag)
+            done = i - T_LAG - 1
+            if done > 0 and done % QUAD == 0:
+                pack_t(done // QUAD - 1)
+                multiply_u(done // QUAD - 1)
             if i == 24:
-                s2_sums(0, 2, 8)
-            if on(i + 3):
-                regroup_v(i + 3)
+                moments_u(0, 2, GROUP)
+            if i + 3 < NB:
+                regroup_vector(i + 3)
             if i == -3:
-                prep_w()
-                quant_x(0)
-                mm_z(0)
+                pack_w()
+                pack_x(0)
+                multiply_z(0)
             if i in (8, 16):
-                chain(i // 8 - 1, 8, 0)
+                newton_chain(i // GROUP - 1, GROUP, 0)
             if i == 24:
-                chain(2, 8, 8)
-            if on(i - LAG):
-                row_max(i - LAG)
+                newton_chain(2, GROUP, QUAD * len(UNITS[0]))
+            if i >= SOFTMAX_LAG:
+                row_max(i - SOFTMAX_LAG)
             if i == 8:
-                prep_p_copy()
-            if on(i):
-                g, k = group_of[i]
-                if i == GROUPS[g][-1] and i < NB - 1:
-                    t_moments(g)
-            gathers(affine_list(i - 1))
+                group_p()
+            if i in (7, 15, 23):
+                moments_t(i // GROUP)
+            gathers(before)
             if i == 9:
-                prep_p_quant()
-            for b in affine_list(i):
-                affine(b)
+                pack_p()
+            if i == 10:
+                spread_p()
+            for b in standardised(i):
+                standardise(b)
             if i == 23:
-                s2_tanh(0)
+                tanh_u(0)
 
-        next_max = [NB - LAG]
-        next_exp = [NB - LAG - 2]
-
-        def late_max():
-            b = next_max[0]
-            next_max[0] = b + 1
-            row_max(b)
-
-        def late_exp():
-            b = next_exp[0]
-            next_exp[0] = b + 1
-            exp1(b)
-
-        s2_sums(1, 3, 8)
-        t_moments(3)
-        s2_out(0, 8)
-        flips(affine_list(NB - 1))
-        warm_sqrt()
-        mm_r(29, pz, "z_ps")
-        root_a(3, 8, 8)
-        gathers([21, 23])
-        late_max()
-        quant_t(4)
-        s2_mm(4)
-        root_b(3)
-        for b in range(24, 32):
-            affine(b)
+        moments_u(1, 3, GROUP)
+        moments_t(3)
+        proj_vector(0, 8)
+        for b in standardised(LAST):
             flip(b)
-        gathers([25, 27, 29, 31])
-        mm_r(30, pt, "tp_ps")
-        mm_r(31, pt, "tp_ps")
-        quant_t(5)
-        s2_mm(5)
-        late_max()
-        quant_t(6)
-        s2_mm(6)
-        late_exp()
-        late_exp()
-        late_max()
-        quant_t(7)
-        s2_mm(7)
-        late_exp()
-        late_max()
-        s2_tanh(2)
-        s2_out(1, 8)
-        mass_a()
-        s2_tanh(3)
-        s2_sums(2, 5, 0)
-        late_exp()
-        late_exp()
-        late_exp()
-        warm_sqrt()
-        s2_sums(3, 5, 12)
-        root_a(5, 0, 16)
-        mass_b()
-        root_b(5)
-        offsets(5, 16)
-        s2_out_s(range(24, 32))
-        s2_out(2, 8)
-        assert done[0] == len(pending)
-        assert next_exp[0] == NB
-        assert next_max[0] == NB
+        load_table(ACT.Sqrt)
+        multiply_r(29, psum_z, "z")
+        root_chain_begin(3, GROUP, QUAD * len(UNITS[1]))
+        gathers(standardised(LAST))
+        load_table(ACT.Exp)
+        row_max(28)
+        pack_t(4)
+        multiply_u(4)
+        root_chain_end(3)
+        for b in range(24, 32):
+            standardise(b)
+            flip(b)
+        gathers(range(24, 32))
+        multiply_r(30, psum_flip, "flipped")
+        multiply_r(31, psum_flip, "flipped")
+        pack_t(5)
+        multiply_u(5)
+        row_max(29)
+        pack_t(6)
+        multiply_u(6)
+        row_exp(26)
+        row_exp(27)
+        row_max(30)
+        pack_t(7)
+        multiply_u(7, psum_r, "r")
+        row_exp(28)
+        row_max(31)
+        tanh_u(2)
+        proj_vector(1, 8)
+        mass_factors()
+        tanh_u(3)
+        moments_u(2, 4, 0)
+        row_exp(29)
+        row_exp(30)
+        row_exp(31)
+        load_table(ACT.Sqrt)
+        moments_u(3, 4, UNIT_MAX)
+        root_chain_begin(4, 0, 16)
+        mass_out()
+        root_chain_end(4)
+        proj_scalar(4, 24, 8)
+        proj_vector(2, 8)
+        assert written[0] == len(pending)

import math
from contextlib import ExitStack

import concourse.mybir as mybir
from concourse.masks import make_identity

F32 = mybir.dt.float32
BF16 = mybir.dt.bfloat16
I32 = mybir.dt.int32
U32 = mybir.dt.uint32
U8 = mybir.dt.uint8
FP8X4 = mybir.dt.float8_e4m3fn_x4
ACT = mybir.ActivationFunctionType
ALU = mybir.AluOpType
AX = mybir.AxisListType

P = 128
NB = 32
NI = 512
NJ = 512
NW = 32
ND = 4
PACK = 4
EPS = 1e-5
N_T = NJ * NW
N_PROJ = NW * NW
ROOT_T = math.sqrt(N_T / (N_T - 1.0))
ROOT_PROJ = math.sqrt(N_PROJ / (N_PROJ - 1.0))
VAR_FLOOR = 1e-30
RSQRT_GUESS = float(0x5F3759DF)
SCALAR_COLS = 96
RUN = 4
SOFTMAX_LAG = 4
T_LAG = 13
GROUP = 8
QUAD = 4
UNITS = [(0, 1), (2, 3), (4, 5, 6), (7,)]
UNIT_MAX = 12
STATS = 24

FLOPS = 2 * NB * ND * (2 * NI * NJ * NW + NW * NJ * NW)


def tile_selfprojectiondev_pb_t_kernel(tc, x, o_xi, p_xi, rel_o_xi, out_0, out_1):
    nc = tc.nc
    with ExitStack() as ctx:
        const = ctx.enter_context(tc.tile_pool(name="const", bufs=1))
        load = ctx.enter_context(tc.tile_pool(name="load", bufs=8))
        regroup = ctx.enter_context(tc.tile_pool(name="regroup", bufs=4))
        packed_x = ctx.enter_context(tc.tile_pool(name="packed_x", bufs=SOFTMAX_LAG + 4))
        tanh = ctx.enter_context(tc.tile_pool(name="tanh", bufs=T_LAG + 5))
        standard = ctx.enter_context(tc.tile_pool(name="standard", bufs=GROUP))
        unread = ctx.enter_context(tc.tile_pool(name="unread", bufs=2))
        small = ctx.enter_context(tc.tile_pool(name="small", bufs=3))
        packed_t = ctx.enter_context(tc.tile_pool(name="packed_t", bufs=4))
        proj = ctx.enter_context(tc.tile_pool(name="proj", bufs=len(UNITS)))
        fin = ctx.enter_context(tc.tile_pool(name="fin", bufs=3))
        psum_z = ctx.enter_context(tc.psum_pool(name="psum_z", bufs=2))
        psum_flip = ctx.enter_context(tc.psum_pool(name="psum_flip", bufs=2))
        psum_r = ctx.enter_context(tc.psum_pool(name="psum_r", bufs=2))
        psum_mom = ctx.enter_context(tc.psum_pool(name="psum_mom", bufs=1))
        psum_u = ctx.enter_context(tc.psum_pool(name="psum_u", bufs=1))
        ctx.enter_context(tc.manual_schedule())

        neg_max = const.tile([P, P], F32)
        nc.gpsimd.memset(neg_max[:], 0.0)
        exp_sum = const.tile([P, P], F32)
        nc.vector.memset(exp_sum[:], 0.0)

        raw_w = const.tile([P, 2, ND, PACK, NW], BF16)
        for s, w in enumerate((o_xi, rel_o_xi)):
            nc.scalar.dma_start(
                out=raw_w[:, s].rearrange("p d t c -> p d (t c)"),
                in_=w.rearrange("d (p t) c -> p d (t c)", t=PACK),
            )
        raw_p = const.tile([P, ND, PACK, NW], BF16)
        for u in range(2):
            nc.scalar.dma_start(
                out=raw_p[:, :, 2 * u : 2 * u + 2, :].rearrange("p d e q -> p d (e q)"),
                in_=p_xi[:, 2 * P * u : 2 * P * (u + 1), :].rearrange("d (p e) q -> p d (e q)", e=2),
            )

        scratch = const.tile([P, 1], F32)

        def load_table(func):
            nc.scalar.activation(out=scratch[:], in_=neg_max[:, P - 1 : P], func=func)

        load_table(ACT.Exp)

        raws = []
        for g in range(NB // 2):
            raw = load.tile([P, 2, PACK, NJ], BF16, name="raw")
            raws.append(raw)
            if g >= 2:
                nc.sync.dma_start(
                    out=raw[:].rearrange("p h t j -> p h (t j)"),
                    in_=x[2 * g : 2 * g + 2].rearrange("h (p t) j -> p h (t j)", t=PACK),
                )
                continue
            for h in range(2):
                b = 2 * g + h
                width = NJ // 2 if b == 0 else NJ
                for lo in range(0, NJ, width):
                    nc.sync.dma_start(
                        out=raw[:, h, :, lo : lo + width],
                        in_=x[b, :, lo : lo + width].rearrange("(p t) j -> p t j", t=PACK),
                    )

        mean_t = const.tile([P, P], F32)
        nc.gpsimd.memset(mean_t[:], 0.0)
        mean_proj = const.tile([P, P], F32)
        nc.gpsimd.memset(mean_proj[:], 0.0)
        for d in range(ND):
            rows = slice(NW * d, NW * (d + 1))
            nc.gpsimd.memset(mean_t[rows, rows], 1.0 / N_T)
            nc.gpsimd.memset(mean_proj[rows, rows], 1.0 / N_PROJ)
        ident = const.tile([P, P], F32)
        make_identity(nc, ident[:])

        w_grouped = const.tile([P, 2, ND * NW, PACK], BF16, align_bytes=64)
        w_codes = const.tile([P, 2 * P], U32, align_bytes=64)
        w_scales = const.tile([P, 2 * P], U8, align_bytes=64)

        def pack_w():
            for s, copy in enumerate((nc.scalar.copy, nc.vector.tensor_copy)):
                copy(
                    out=w_grouped[:, s].rearrange("p (d c) t -> p d c t", d=ND),
                    in_=raw_w[:, s].rearrange("p d t c -> p d c t"),
                )
            nc.vector.quantize_mx(
                out=w_codes[:].bitcast(FP8X4),
                scales=w_scales[:],
                in_=w_grouped[:].rearrange("p s w t -> p (s w t)"),
            )

        p_grouped = const.tile([P, ND * NW, PACK], BF16, align_bytes=64)
        p_codes = const.tile([P, P], U32, align_bytes=64)
        p_scales = const.tile([P, P], U8, align_bytes=64)
        p_wide = const.tile([P, ND * (P + NW)], U32, align_bytes=64)
        nc.vector.memset(p_wide[:].bitcast(I32), 0)
        p_wide_scales = const.tile([P, ND * (P + NW)], U8, align_bytes=64)
        nc.vector.memset(p_wide_scales[:].bitcast(I32), 0)

        def group_p():
            nc.vector.tensor_copy(
                out=p_grouped[:].rearrange("p (d q) t -> p d q t", d=ND),
                in_=raw_p[:].rearrange("p d t q -> p d q t"),
            )

        def pack_p():
            nc.vector.quantize_mx(
                out=p_codes[:].bitcast(FP8X4),
                scales=p_scales[:],
                in_=p_grouped[:].rearrange("p w t -> p (w t)"),
            )

        def spread_p():
            for wide, narrow in (
                (p_wide[:].bitcast(I32), p_codes[:].bitcast(I32)),
                (p_wide_scales[:], p_scales[:]),
            ):
                nc.vector.tensor_copy(
                    out=wide.rearrange("p (d w) -> p d w", d=ND)[:, :, 0:NW],
                    in_=narrow.rearrange("p (d q) -> p d q", d=ND),
                )

        state = {}
        pending = []
        written = [0]

        def small_step():
            if written[0] < len(pending):
                pending[written[0]]()
                written[0] = written[0] + 1

        def finish_chain(end):
            for n in range(end - written[0]):
                small_step()

        def regroup_columns(b, copy, lo, hi):
            copy(
                out=state[("grouped", b)][:, lo:hi, :].rearrange("p (c i) t -> p c t i", i=RUN),
                in_=raws[b // 2][:, b % 2, :, lo:hi].rearrange("p t (c i) -> p c t i", i=RUN),
            )

        def regroup_scalar(b):
            state[("grouped", b)] = regroup.tile([P, NJ, PACK], BF16, align_bytes=64, name="grouped")
            regroup_columns(b, nc.scalar.copy, NJ - SCALAR_COLS, NJ)

        def regroup_vector(b):
            cuts = (0, NJ // 2, NJ - SCALAR_COLS) if b == 0 else (0, NJ - SCALAR_COLS)
            for lo, hi in zip(cuts, cuts[1:]):
                regroup_columns(b, nc.vector.tensor_copy, lo, hi)
            small_step()

        def pack_x(b):
            codes = packed_x.tile([P, NJ], U32, align_bytes=64, name="codes")
            scales = packed_x.tile([P, NJ], U8, align_bytes=64, name="scales")
            nc.vector.quantize_mx(
                out=codes[:].bitcast(FP8X4),
                scales=scales[:],
                in_=state[("grouped", b)][:].rearrange("p j t -> p (j t)"),
            )
            state[("x", b)] = (codes, scales)
            small_step()

        def multiply_x(b, s, pool, tag):
            codes, scales = state[("x", b)]
            cols = slice(s * P, (s + 1) * P)
            out = pool.tile([P, NJ], F32, name="product", tag=tag)
            nc.tensor.matmul_mx(
                out=out[:],
                lhsT=w_codes[:, cols].bitcast(FP8X4),
                lhsT_scale=w_scales[:, cols],
                rhs=codes[:].bitcast(FP8X4),
                rhs_scale=scales[:],
                start=True,
                stop=True,
            )
            state[(("z", "r")[s], b)] = out

        def multiply_z(b):
            multiply_x(b, 0, psum_z, "z")

        def multiply_r(b, pool, tag):
            multiply_x(b, 1, pool, tag)

        def row_max(b):
            nc.vector.tensor_reduce(
                out=neg_max[:, b : b + 1], in_=state[("r", b)][:], axis=AX.X, op=ALU.max, negate=True
            )
            small_step()

        def row_exp(b):
            out = unread.tile([P, NJ], BF16, name="exp")
            nc.scalar.activation(
                out=out[:], in_=state[("r", b)][:], func=ACT.Exp, bias=neg_max[:, b : b + 1], scale=1.0,
                accum_out=exp_sum[:, b : b + 1],
            )

        def mass_factors():
            flipped = psum_r.tile([P, P], F32, name="flipped_max", tag="r")
            nc.tensor.transpose(out=flipped[:], in_=neg_max[:], identity=ident[:])
            by_depth = flipped[0:NB, :].rearrange("b (d c) -> b d c", d=ND)
            least = fin.tile([NB, ND], F32, name="least")
            nc.vector.tensor_reduce(out=least[:], in_=by_depth, axis=AX.X, op=ALU.min)
            diff = fin.tile([NB, ND, NW], F32, name="diff")
            nc.vector.tensor_tensor(
                out=diff[:], in0=least[:].unsqueeze(2).to_broadcast([NB, ND, NW]), in1=by_depth, op=ALU.subtract
            )
            factor = fin.tile([NB, ND, NW], F32, name="factor")
            nc.scalar.activation(out=factor[:], in_=diff[:], func=ACT.Exp)
            state["factor"] = factor

        def mass_out():
            flipped = psum_r.tile([P, P], F32, name="flipped_sum", tag="r")
            nc.tensor.transpose(out=flipped[:], in_=exp_sum[:], identity=ident[:])
            part = fin.tile([NB, ND, NW], F32, name="part")
            nc.vector.tensor_tensor(
                out=part[:], in0=state["factor"][:], in1=flipped[0:NB, :].rearrange("b (d c) -> b d c", d=ND),
                op=ALU.mult,
            )
            total = fin.tile([NB, ND], F32, name="total")
            nc.vector.tensor_reduce(out=total[:], in_=part[:], axis=AX.X, op=ALU.add)
            inverse = fin.tile([NB, ND], F32, name="inverse")
            nc.vector.reciprocal(out=inverse[:], in_=total[:])
            mass = fin.tile([NB, ND, NW], F32, name="mass")
            nc.vector.tensor_tensor(
                out=mass[:], in0=part[:], in1=inverse[:].unsqueeze(2).to_broadcast([NB, ND, NW]), op=ALU.mult
            )
            nc.sync.dma_start(out=out_1, in_=mass[:])

        def moments(chain, lo, sums, average):
            if ("moments", chain) not in state:
                state[("moments", chain)] = psum_mom.tile([P, 2, STATS], F32, name="moments")
            nc.tensor.matmul(
                out=state[("moments", chain)][:, :, lo : lo + sums.shape[2]],
                lhsT=average[:], rhs=sums, start=True, stop=True,
            )

        def variances(chain, n):
            mom = small.tile([P, 2, STATS], F32, name="mom")
            var = small.tile([P, STATS], F32, name="var")
            tmp = small.tile([P, STATS], F32, name="tmp")
            rstd = small.tile([P, STATS], F32, name="rstd")
            cols = slice(0, n)
            mean, var_n, tmp_n = mom[:, 0, cols], var[:, cols], tmp[:, cols]
            source = state[("moments", chain)][:, :, cols]
            ops = [
                lambda: nc.vector.tensor_copy(out=mom[:, :, cols], in_=source),
                lambda: nc.vector.tensor_tensor(out=tmp_n, in0=mean, in1=mean, op=ALU.mult),
                lambda: nc.vector.tensor_tensor(out=var_n, in0=mom[:, 1, cols], in1=tmp_n, op=ALU.subtract),
                lambda: nc.vector.tensor_scalar(
                    out=var_n, in0=var_n, scalar1=VAR_FLOOR, scalar2=None, op0=ALU.max
                ),
            ]
            return ops, mom, var_n, tmp, rstd

        def inverses(tmp, rstd, n_t, n_proj):
            n = n_t + n_proj
            ops = [
                lambda lo=lo, hi=hi, root=root: nc.vector.tensor_scalar(
                    out=tmp[:, lo:hi], in0=tmp[:, lo:hi], scalar1=root, scalar2=EPS, op0=ALU.mult, op1=ALU.add
                )
                for lo, hi, root in ((0, n_t, ROOT_T), (n_t, n, ROOT_PROJ))
                if lo < hi
            ]
            ops.append(lambda: nc.vector.reciprocal(out=rstd[:, 0:n], in_=tmp[:, 0:n]))
            return ops

        def newton_chain(chain, n_t, n_proj):
            n = n_t + n_proj
            ops, mom, var, tmp, rstd = variances(chain, n)
            guess = small.tile([P, STATS], I32, name="guess")
            y, tmp_n = guess[:, 0:n].bitcast(F32), tmp[:, 0:n]
            stt = nc.vector.scalar_tensor_tensor
            ops.append(lambda: nc.vector.tensor_scalar(
                out=guess[:, 0:n], in0=var.bitcast(I32), scalar1=-0.5, scalar2=RSQRT_GUESS,
                op0=ALU.mult, op1=ALU.add,
            ))
            for n_step in range(3):
                ops.extend([
                    lambda: nc.vector.tensor_tensor(out=tmp_n, in0=y, in1=y, op=ALU.mult),
                    lambda: stt(out=tmp_n, in0=tmp_n, scalar=-0.5, in1=var, op0=ALU.mult, op1=ALU.mult),
                    lambda: stt(out=y, in0=tmp_n, scalar=1.5, in1=y, op0=ALU.add, op1=ALU.mult),
                ])
            ops.append(lambda: nc.vector.tensor_tensor(out=tmp_n, in0=var, in1=y, op=ALU.mult))
            pending.extend(ops + inverses(tmp, rstd, n_t, n_proj))
            state[("chain", chain)] = (mom, rstd, len(pending))

        def root_chain_begin(chain, n_t, n_proj):
            ops, mom, var, tmp, rstd = variances(chain, n_t + n_proj)
            for op in ops:
                op()
            nc.scalar.activation(out=tmp[:, 0 : n_t + n_proj], in_=var, func=ACT.Sqrt)
            state[("rest", chain)] = inverses(tmp, rstd, n_t, n_proj)
            state[("chain", chain)] = (mom, rstd, len(pending))

        def root_chain_end(chain):
            for op in state[("rest", chain)]:
                op()

        def tanh_t(b):
            if b % GROUP == 0:
                state[("sums", b // GROUP)] = small.tile([P, 2, GROUP], F32, name="sums")
            t = tanh.tile([P, NJ], F32, name="t")
            nc.scalar.activation(
                out=t[:], in_=state[("z", b)][:], func=ACT.Tanh,
                accum_out=state[("sums", b // GROUP)][:, 0, b % GROUP : b % GROUP + 1],
            )
            state[("t", b)] = t

        def square_t(b):
            out = unread.tile([P, NJ], BF16, name="square")
            nc.scalar.activation(
                out=out[:], in_=state[("t", b)][:], func=ACT.Square,
                accum_out=state[("sums", b // GROUP)][:, 1, b % GROUP : b % GROUP + 1],
            )

        def moments_t(g):
            moments(g, 0, state[("sums", g)][:], mean_t)

        def standardise(b):
            mom, rstd, end = state[("chain", b // GROUP)]
            finish_chain(end)
            col = slice(b % GROUP, b % GROUP + 1)
            ts = standard.tile([P, NJ], BF16, align_bytes=64, name="ts")
            nc.vector.tensor_scalar(
                out=ts[:], in0=state[("t", b)][:], scalar1=mom[:, 0, col], scalar2=rstd[:, col],
                op0=ALU.subtract, op1=ALU.mult,
            )
            state[("ts", b)] = ts
            small_step()

        def flip(b):
            if b % 2 == 0:
                state[("flipped", b // 2)] = psum_flip.tile([P, 2, 2, P], F32, name="flipped", tag="flipped")
            words = state[("ts", b)][:].bitcast(F32)
            for u in range(2):
                nc.tensor.transpose(
                    out=state[("flipped", b // 2)][:, b % 2, u, :], in_=words[:, P * u : P * (u + 1)],
                    identity=ident[:],
                )

        def gather(b):
            quad, h = b // QUAD, b % QUAD - 1
            if h == 0:
                state[("quad", quad)] = (
                    packed_t.tile([P, ND, QUAD, NW, PACK], BF16, align_bytes=64, name="grouped_t"),
                    packed_t.tile([P, ND * P], U32, align_bytes=64, name="codes_t"),
                    packed_t.tile([P, ND * P], U8, align_bytes=64, name="scales_t"),
                )
            grouped = state[("quad", quad)][0]
            nc.scalar.copy(
                out=grouped[:, :, h : h + 2].rearrange("p d b c t -> p d b (c t)").bitcast(F32)
                .rearrange("p d b (c u) -> p b d c u", u=2),
                in_=state[("flipped", b // 2)][:].rearrange("p b u (d c) -> p b d c u", d=ND),
            )

        def gathers(batches):
            for b in batches:
                if b % 2 == 1:
                    gather(b)

        def pack_t(quad):
            grouped, codes, scales = state[("quad", quad)]
            nc.vector.quantize_mx(
                out=codes[:].bitcast(FP8X4), scales=scales[:],
                in_=grouped[:].rearrange("p d b c t -> p (d b c t)"),
            )
            small_step()

        place = {quad: (unit, k) for unit, quads in enumerate(UNITS) for k, quad in enumerate(quads)}

        def multiply_u(quad, pool=psum_u, tag="u"):
            grouped, codes, scales = state[("quad", quad)]
            unit, k = place[quad]
            if k == 0:
                state[("u", unit)] = pool.tile([P, 3, P], F32, name="u", tag=tag)
            for d in range(ND):
                cols = slice(P * d, P * (d + 1))
                nc.tensor.matmul_mx(
                    out=state[("u", unit)][:, k, :],
                    lhsT=p_wide[:, cols].bitcast(FP8X4),
                    lhsT_scale=p_wide_scales[:, cols],
                    rhs=codes[:, cols].bitcast(FP8X4),
                    rhs_scale=scales[:, cols],
                    start=(d == 0),
                    stop=(d == ND - 1),
                )

        def tanh_u(unit):
            quads = len(UNITS[unit])
            both = proj.tile([P, 2, UNIT_MAX, NW], F32, name="both")
            flat = [both[:, k, 0 : QUAD * quads].rearrange("p b c -> p (b c)") for k in range(2)]
            nc.scalar.activation(
                out=flat[0], in_=state[("u", unit)][:, 0:quads, :].rearrange("p k c -> p (k c)"), func=ACT.Tanh
            )
            nc.scalar.activation(out=flat[1], in_=flat[0], func=ACT.Square)
            state[("both", unit)] = both

        def moments_u(unit, chain, lo):
            n = QUAD * len(UNITS[unit])
            sums = small.tile([P, 2, UNIT_MAX], F32, name="sums_u")
            nc.vector.tensor_reduce(
                out=sums[:, :, 0:n], in_=state[("both", unit)][:, :, 0:n], axis=AX.X, op=ALU.add
            )
            small_step()
            moments(chain, lo, sums[:, :, 0:n], mean_proj)
            state[("columns", unit)] = (chain, lo)

        def store_proj(queue, res, first, n):
            queue.dma_start(
                out=out_0[first : first + n].rearrange("b d q c -> (d q) b c"), in_=res[:, 0:n]
            )

        def proj_vector(unit, n):
            chain, lo = state[("columns", unit)]
            mom, rstd, end = state[("chain", chain)]
            finish_chain(end)
            tanh_of_u = state[("both", unit)][:, 0, 0:n]
            centred = fin.tile([P, UNIT_MAX, NW], F32, name="centred")
            nc.vector.tensor_tensor(
                out=centred[:, 0:n], in0=tanh_of_u,
                in1=mom[:, 0, lo : lo + n].unsqueeze(2).to_broadcast([P, n, NW]), op=ALU.subtract,
            )
            small_step()
            res = fin.tile([P, UNIT_MAX, NW], F32, name="res")
            nc.vector.tensor_tensor(
                out=res[:, 0:n], in0=centred[:, 0:n],
                in1=rstd[:, lo : lo + n].unsqueeze(2).to_broadcast([P, n, NW]), op=ALU.mult,
            )
            small_step()
            store_proj(nc.sync, res, QUAD * UNITS[unit][0], n)

        def proj_scalar(chain, first, n):
            mom, rstd, end = state[("chain", chain)]
            offset = small.tile([P, STATS], F32, name="offset")
            used = slice(0, sum(QUAD * len(UNITS[unit]) for unit in range(len(UNITS)) if state[("columns", unit)][0] == chain))
            nc.vector.scalar_tensor_tensor(
                out=offset[:, used], in0=mom[:, 0, used], scalar=-1.0, in1=rstd[:, used],
                op0=ALU.mult, op1=ALU.mult,
            )
            res = fin.tile([P, UNIT_MAX, NW], F32, name="res")
            for k in range(n):
                unit = place[(first + k) // QUAD][0]
                row = first + k - QUAD * UNITS[unit][0]
                col = state[("columns", unit)][1] + row
                nc.scalar.activation(
                    out=res[:, k], in_=state[("both", unit)][:, 0, row], func=ACT.Identity,
                    bias=offset[:, col : col + 1], scale=rstd[:, col : col + 1],
                )
            store_proj(nc.scalar, res, first, n)

        LAST = NB - 1

        def standardised(i):
            if i < 28:
                return [i - T_LAG] if i >= T_LAG else []
            return {28: [15, 16], 29: [17, 18], 30: [19, 20], 31: [21, 22, 23]}[i]

        for i in range(-3, NB):
            if i >= 0:
                tanh_t(i)
            if i == LAST:
                tanh_u(1)
            elif i > SOFTMAX_LAG:
                row_exp(i - SOFTMAX_LAG - 1)
            before = standardised(i - 1)
            for b in before:
                flip(b)
            if 0 <= i < LAST:
                pack_x(i + 1)
                multiply_z(i + 1)
            if i + 3 < NB:
                regroup_scalar(i + 3)
            if i >= 0:
                square_t(i)
            if i >= SOFTMAX_LAG - 1:
                pool, tag = (psum_r, "r") if i < LAST else (psum_z, "z")
                multiply_r(i - SOFTMAX_LAG + 1, pool, tag)
            done = i - T_LAG - 1
            if done > 0 and done % QUAD == 0:
                pack_t(done // QUAD - 1)
                multiply_u(done // QUAD - 1)
            if i == 24:
                moments_u(0, 2, GROUP)
            if i + 3 < NB:
                regroup_vector(i + 3)
            if i == -3:
                pack_w()
                pack_x(0)
                multiply_z(0)
            if i in (8, 16):
                newton_chain(i // GROUP - 1, GROUP, 0)
            if i == 24:
                newton_chain(2, GROUP, QUAD * len(UNITS[0]))
            if i >= SOFTMAX_LAG:
                row_max(i - SOFTMAX_LAG)
            if i == 8:
                group_p()
            if i in (7, 15, 23):
                moments_t(i // GROUP)
            gathers(before)
            if i == 9:
                pack_p()
            if i == 10:
                spread_p()
            for b in standardised(i):
                standardise(b)
            if i == 23:
                tanh_u(0)

        moments_u(1, 3, GROUP)
        moments_t(3)
        proj_vector(0, 8)
        for b in standardised(LAST):
            flip(b)
        load_table(ACT.Sqrt)
        multiply_r(29, psum_z, "z")
        root_chain_begin(3, GROUP, QUAD * len(UNITS[1]))
        gathers(standardised(LAST))
        load_table(ACT.Exp)
        row_max(28)
        pack_t(4)
        multiply_u(4)
        root_chain_end(3)
        for b in range(24, 32):
            standardise(b)
            flip(b)
        gathers(range(24, 32))
        multiply_r(30, psum_flip, "flipped")
        multiply_r(31, psum_flip, "flipped")
        pack_t(5)
        multiply_u(5)
        row_max(29)
        pack_t(6)
        multiply_u(6)
        row_exp(26)
        row_exp(27)
        row_max(30)
        pack_t(7)
        multiply_u(7, psum_r, "r")
        row_exp(28)
        row_max(31)
        tanh_u(2)
        proj_vector(1, 8)
        mass_factors()
        tanh_u(3)
        moments_u(2, 4, 0)
        row_exp(29)
        row_exp(30)
        row_exp(31)
        load_table(ACT.Sqrt)
        moments_u(3, 4, UNIT_MAX)
        root_chain_begin(4, 0, 16)
        mass_out()
        root_chain_end(4)
        proj_scalar(4, 24, 8)
        proj_vector(2, 8)
        assert written[0] == len(pending)
